import numpy as np
import ml_dtypes


def mxq(x, axis, fmt="e4m3"):
    dtype, down = {"e4m3": (ml_dtypes.float8_e4m3fn, 7), "e5m2": (ml_dtypes.float8_e5m2, 14)}[fmt]
    v = np.moveaxis(np.asarray(x, np.float32).astype(ml_dtypes.bfloat16).astype(np.float64), axis, -1)
    blocks = v.reshape(v.shape[:-1] + (-1, 32))
    amax = np.abs(blocks).max(-1, keepdims=True)
    byte = np.maximum(np.where(amax > 0, np.frexp(amax)[1] - 1 + 127, 0) - down, 1)
    scale = np.exp2(byte - 127.0)
    codes = (blocks / scale).astype(np.float32).astype(dtype).astype(np.float64)
    return np.moveaxis((codes * scale).reshape(v.shape), -1, axis)


WIDE = False


def mx_kscale(k):
    if not WIDE:
        return np.ones(k)
    levels = np.array([10, -10, 5, -5, 0])
    a = np.random.permutation(np.resize(levels, k // 512 * 4)).reshape(k // 512, 4)
    idx = np.arange(k)
    return np.exp2(a[idx // 512, idx % 128 // 32])


BF16 = ml_dtypes.bfloat16


def bf(x):
    return np.asarray(x, np.float32).astype(BF16)


def f64(x):
    return np.asarray(x).astype(np.float64)


B, T, H, DK, DH, E, V = 128, 1, 24, 64, 64, 1536, 1536
EPS = 1e-6


def setup_inputs():
    s = mx_kscale(E)
    return {"x": bf(np.random.standard_normal((B, T, E)) * s),
            "qr": bf(np.random.standard_normal((B, H, T, DK))),
            "kr": bf(np.random.standard_normal((B, H, T, DK))),
            "decay": bf(np.random.uniform(0.7, 1.0, H)),
            "prev_kv": bf(np.random.standard_normal((B, H, DH, DK))),
            "Wv": bf(np.random.standard_normal((E, V)) / np.sqrt(E) / s[:, None]),
            "Wo": bf(np.random.standard_normal((V, E)) / np.sqrt(V))}


def reference(x, qr, kr, decay, prev_kv, Wv, Wo):
    v = (mxq(f64(x), 2, "e4m3") @ mxq(f64(Wv), 0, "e4m3")).reshape(B, H, DH, T)
    kv = f64(prev_kv) * f64(decay)[:, None, None] + f64(kr) * v
    out = np.sum(f64(qr) * kv, axis=3)
    out = out * (1.0 / np.sqrt(np.mean(out * out, axis=-1, keepdims=True) + EPS))
    out = out.reshape(B, T, V)
    return mxq(out, 2, "e4m3") @ mxq(f64(Wo), 0, "e4m3")

@@ -1,0 +1,306 @@
+from contextlib import ExitStack
+
+import concourse.bass as bass
+import concourse.mybir as mybir
+import concourse.tile as tile
+from concourse.masks import make_identity
+
+F32 = mybir.dt.float32
+BF16 = mybir.dt.bfloat16
+U8 = mybir.dt.uint8
+U32 = mybir.dt.uint32
+FP8X4 = mybir.dt.float8_e4m3fn_x4
+ALU = mybir.AluOpType
+ACT = mybir.ActivationFunctionType
+AX = mybir.AxisListType
+
+P = 128
+B, H, DK, DH, E, V = 128, 24, 64, 64, 1536, 1536
+HEAD = DH * DK
+EPS = 1e-6
+FLOPS = 2 * 2 * B * E * V + 4 * B * H * DH * DK
+
+N_PAIR = 3
+V_HEADS = (6, 7, 8, 9, 10, 11, 18, 19, 20, 21, 22, 23)
+RED = ("VS", "VS", "VS", "SS", "SS", "SS", "SS", "SS", "SS", "SS", "SS", "SV")
+SEQ = ("p0", "v0", "p1", "w0", "p2", "v1", "p3", "w1", "p4", "v2", "p5", "w2", "vv",
+       "v3", "n0", "w3", "o0", "v4", "v5", "w4", "v6", "v7", "n1", "o1", "w5", "v8", "v9", "v10", "n2a", "v11", "n2b", "o2")
+
+
+def tile_multiscaleretention_pb_kernel(tc, x, qr, kr, decay, prev_kv, Wv, Wo, out):
+    nc = tc.nc
+    xf = x.rearrange("b t e -> b (t e)")
+    qf = qr.rearrange("b h t c -> b (h t c)")
+    kf = kr.rearrange("b h t c -> b (h t c)")
+    pb = prev_kv.rearrange("b h d c -> b (h d c)")
+    pp = prev_kv.rearrange("b (hh hp) d c -> (b hh) (hp d c)", hh=2)
+    of = out.rearrange("b t e -> b (t e)")
+
+    with ExitStack() as ctx:
+        keep = ctx.enter_context(tc.tile_pool(name="keep", bufs=1))
+        small = ctx.enter_context(tc.tile_pool(name="small", bufs=2))
+        rawp = ctx.enter_context(tc.tile_pool(name="rawp", bufs=2))
+        grpp = ctx.enter_context(tc.tile_pool(name="grpp", bufs=2))
+        xpp = ctx.enter_context(tc.tile_pool(name="xpp", bufs=2))
+        zp = ctx.enter_context(tc.tile_pool(name="zp", bufs=2))
+        xvp = ctx.enter_context(tc.tile_pool(name="xvp", bufs=3))
+        prp = ctx.enter_context(tc.tile_pool(name="prp", bufs=2))
+        ctp = ctx.enter_context(tc.tile_pool(name="ctp", bufs=1))
+        psa = ctx.enter_context(tc.psum_pool(name="psa", bufs=3))
+        psb = ctx.enter_context(tc.psum_pool(name="psb", bufs=2))
+        psc = ctx.enter_context(tc.psum_pool(name="psc", bufs=3))
+
+        q_sb = keep.tile([P, E], BF16)
+        nc.sync.dma_start(out=q_sb[:], in_=qf)
+        dec_b = keep.tile([P, H], BF16)
+        nc.sync.dma_start(out=dec_b[:], in_=decay.partition_broadcast(P))
+        k_sb = rawp.tile([P, E], BF16, tag="raw")
+        nc.sync.dma_start(out=k_sb[:], in_=kf)
+        x_sb = rawp.tile([P, E], BF16, tag="raw")
+        nc.sync.dma_start(out=x_sb[:], in_=xf)
+
+        ident_b = keep.tile([P, P], BF16)
+        make_identity(nc, ident_b[:])
+        ident_f = keep.tile([P, P], F32)
+        make_identity(nc, ident_f[:])
+        eps_t = keep.tile([P, 1], F32)
+        nc.vector.memset(eps_t[:], EPS)
+        dum = keep.tile([P, 1], F32)
+        nc.scalar.activation(out=dum[:], in_=eps_t[:], func=ACT.Sqrt)
+
+        dec_f = keep.tile([P, H], F32)
+        nc.vector.tensor_copy(out=dec_f[:], in_=dec_b[:])
+        qd = keep.tile([P, H, DK], F32)
+        nc.vector.tensor_tensor(
+            out=qd[:],
+            in0=q_sb[:].rearrange("p (h c) -> p h c", c=DK),
+            in1=dec_f[:].unsqueeze(2).to_broadcast([P, H, DK]),
+            op=ALU.mult,
+        )
+
+        qz = zp.tile([P, 2 * N_PAIR * 2 * 2 * P], BF16, tag="z")
+        nc.vector.memset(qz[:], 0.0)
+        qzv = qz[:].rearrange("p (hp hh e k) -> p hp hh e k", hh=2, e=2, k=P)
+        qpe = q_sb[:].rearrange("p (hh hp c) -> p hp hh c", hh=2, c=DK)[:, 0:2 * N_PAIR, :, :]
+        nc.vector.tensor_copy(out=qzv[:, :, :, 0, 0:DK], in_=qpe)
+        nc.vector.tensor_copy(out=qzv[:, :, :, 1, DK:P], in_=qpe)
+        rq = keep.tile([P, N_PAIR * P * 8], BF16)
+        rqv = rq[:].rearrange("p (t b n) -> p t b n", b=P, n=8)
+        for t in range(N_PAIR):
+            pq = psc.tile([P, 8, P], BF16, tag="c")
+            for a in range(2):
+                for hh in range(2):
+                    for e in range(2):
+                        nc.tensor.transpose(pq[:, a * 4 + hh * 2 + e, :], qzv[:, 2 * t + a, hh, e, :], ident_b[:])
+            nc.vector.tensor_copy(out=rqv[:, t], in_=pq[:].rearrange("p n b -> p b n"))
+
+        qk = prp.tile([P, H, DK], F32, tag="prod")
+        nc.vector.tensor_tensor(
+            out=qk[:].rearrange("p h c -> p (h c)"), in0=q_sb[:], in1=k_sb[:], op=ALU.mult
+        )
+        s_t = keep.tile([P, H], F32)
+        nc.vector.tensor_reduce(out=s_t[:], in_=qk[:], axis=AX.X, op=ALU.add)
+
+        xc = keep.tile([P, 3, P], U32, align_bytes=64)
+        xs = keep.tile([P, 3, P], U8, align_bytes=64)
+        xw = x_sb[:].bitcast(F32)
+        xg = grpp.tile([P, 3 * 512], BF16, tag="grp", align_bytes=64)
+        for g in range(3):
+            xt = psc.tile([P, 2, P], F32, tag="c")
+            for u in range(2):
+                nc.tensor.transpose(xt[:, u, :], xw[:, 256 * g + 128 * u:256 * g + 128 * u + 128], ident_f[:])
+            nc.vector.tensor_copy(
+                out=xg[:, 512 * g:512 * g + 512].bitcast(F32).rearrange("p (b u) -> p b u", u=2),
+                in_=xt[:].rearrange("p u b -> p b u"),
+            )
+        for g in range(3):
+            nc.vector.quantize_mx(out=xc[:, g, :].bitcast(FP8X4), scales=xs[:, g, :], in_=xg[:, 512 * g:512 * g + 512])
+
+        wc = keep.tile([P, 3, V], U32, align_bytes=64)
+        ws = keep.tile([P, 3, V], U8, align_bytes=64)
+        sv = keep.tile([P, V], F32)
+        r = keep.tile([P, V], F32)
+        ncd = keep.tile([P, 3, P], U32, align_bytes=64)
+        nsc = keep.tile([P, 3, P], U8, align_bytes=64)
+        state = {}
+
+        def weight_chunk(w, g, paired):
+            raw = rawp.tile([P, 4, V], BF16, tag="raw")
+            if paired:
+                for u in range(2):
+                    nc.sync.dma_start(
+                        out=raw[:, 2 * u:2 * u + 2, :],
+                        in_=w[512 * g + 256 * u:512 * g + 256 * u + 256, :].rearrange("(q e) c -> q e c", e=2),
+                    )
+            else:
+                nc.sync.dma_start(out=raw[:], in_=w[512 * g:512 * g + 512, :].rearrange("(t p) c -> p t c", p=P))
+            pieces = ((0, 1024), (1024, 512))
+            grps = []
+            for w0, wn in pieces:
+                grp = grpp.tile([P, 4096], BF16, tag="grp", align_bytes=64)
+                nc.vector.tensor_copy(
+                    out=grp[:, 0:4 * wn].rearrange("p (c i t) -> p c t i", i=4, t=4),
+                    in_=raw[:, :, w0:w0 + wn].rearrange("p t (c i) -> p c t i", i=4),
+                )
+                grps.append(grp)
+            for (w0, wn), grp in zip(pieces, grps):
+                nc.vector.quantize_mx(
+                    out=wc[:, g, w0:w0 + wn].bitcast(FP8X4), scales=ws[:, g, w0:w0 + wn], in_=grp[:, 0:4 * wn]
+                )
+
+        def v_passes():
+            for nb in range(3):
+                acc = psc.tile([P, 512], F32, tag="c")
+                for g in range(3):
+                    nc.tensor.matmul_mx(
+                        out=acc[:],
+                        lhsT=xc[:, g, :].bitcast(FP8X4),
+                        lhsT_scale=xs[:, g, :],
+                        rhs=wc[:, g, 512 * nb:512 * nb + 512].bitcast(FP8X4),
+                        rhs_scale=ws[:, g, 512 * nb:512 * nb + 512],
+                        start=(g == 0),
+                        stop=(g == 2),
+                    )
+                nc.vector.tensor_tensor(
+                    out=sv[:, 512 * nb:512 * nb + 512].rearrange("p (h d) -> p h d", d=DH),
+                    in0=acc[:].rearrange("p (h d) -> p h d", d=DH),
+                    in1=s_t[:, 8 * nb:8 * nb + 8].unsqueeze(2).to_broadcast([P, 8, DH]),
+                    op=ALU.mult,
+                )
+
+        def vector_head(vi):
+            h = V_HEADS[vi]
+            xv = xvp.tile([P, HEAD], BF16, tag="xv")
+            nc.sync.dma_start(out=xv[:], in_=pb[:, h * HEAD:(h + 1) * HEAD])
+            for half in range(2):
+                prod = prp.tile([P, 32, DK], F32, tag="prod")
+                nc.vector.tensor_tensor(
+                    out=prod[:],
+                    in0=xv[:, half * 2048:(half + 1) * 2048].rearrange("p (d c) -> p d c", c=DK),
+                    in1=qd[:, h, :].unsqueeze(1).to_broadcast([P, 32, DK]),
+                    op=ALU.mult,
+                )
+                c0 = h * DH + half * 32
+                if RED[vi][half] == "V":
+                    nc.vector.tensor_reduce(out=r[:, c0:c0 + 32], in_=prod[:], axis=AX.X, op=ALU.add)
+                else:
+                    for dd in range(32):
+                        nc.scalar.activation(
+                            out=prod[:, dd, :], in_=prod[:, dd, :], func=ACT.Copy,
+                            accum_out=r[:, c0 + dd:c0 + dd + 1],
+                        )
+
+        def tensor_tile(i):
+            t, half = i // 2, i % 2
+            xp = xpp.tile([P, 2 * HEAD], BF16, tag="xp")
+            nc.sync.dma_start(out=xp[:], in_=pp[P * half:P * half + P, 2 * t * HEAD:(2 * t + 2) * HEAD])
+            z = zp.tile([P, 64 * P], BF16, tag="z")
+            zw = z[:].bitcast(F32).rearrange("p (b s) -> p b s", s=64)
+            for sg in range(8):
+                tp = psa.tile([P, 8, P], BF16, tag="a")
+                for k in range(8):
+                    s = 8 * sg + k
+                    nc.tensor.transpose(tp[:, k, :], xp[:, s * P:(s + 1) * P], ident_b[:])
+                nc.scalar.copy(out=zw[:, :, 8 * sg:8 * sg + 8], in_=tp[:].bitcast(F32).rearrange("p k w -> p w k"))
+            mm = psb.tile([P, 64, 8], F32, tag="b")
+            for bi in range(64):
+                nc.tensor.matmul(
+                    out=mm[:, bi, :], lhsT=z[:, bi * P:(bi + 1) * P], rhs=rqv[:, t, 64 * half + bi, :],
+                    start=True, stop=True,
+                )
+            if half == 0:
+                state["ct"] = ctp.tile([P, 8, P], F32, name="ct", tag="ct")
+            ct = state["ct"]
+            nc.vector.tensor_copy(out=ct[:, :, 64 * half:64 * half + 64], in_=mm[:].rearrange("p b n -> p n b"))
+            if half == 1:
+                for a in range(2):
+                    rb = psc.tile([P, 4, P], F32, tag="c")
+                    for n in range(4):
+                        nc.tensor.transpose(rb[:, n, :], ct[:, 4 * a + n, :], ident_f[:])
+                    for hh in range(2):
+                        h = hh * 12 + 2 * t + a
+                        m0 = 64 * a + hh
+                        nc.vector.tensor_scalar_mul(
+                            out=r[:, h * DH:(h + 1) * DH].rearrange("p (j e) -> p j e", e=2),
+                            in0=rb[:, 2 * hh:2 * hh + 2, m0:m0 + 63:2].rearrange("p e j -> p j e"),
+                            scalar1=dec_f[:, h:h + 1],
+                        )
+
+        def norm(h0, nh):
+            c0, cn = h0 * DH, nh * DH
+            kg = h0 // 8
+            if "nb%d" % kg not in state:
+                state["nb%d" % kg] = keep.tile([P, 512], BF16, name="nbf%d" % kg)
+            n_bf = state["nb%d" % kg]
+            nc.vector.tensor_tensor(out=r[:, c0:c0 + cn], in0=r[:, c0:c0 + cn], in1=sv[:, c0:c0 + cn], op=ALU.add)
+            sq = small.tile([P, 8, DH], F32, tag="sq")
+            nc.vector.tensor_tensor(
+                out=sq[:, 0:nh, :].rearrange("p h d -> p (h d)"), in0=r[:, c0:c0 + cn], in1=r[:, c0:c0 + cn], op=ALU.mult
+            )
+            ss = small.tile([P, 8], F32, tag="ss")
+            nc.vector.tensor_reduce(out=ss[:, 0:nh], in_=sq[:, 0:nh, :], axis=AX.X, op=ALU.add)
+            rms = small.tile([P, 8], F32, tag="rms")
+            nc.scalar.activation(out=rms[:, 0:nh], in_=ss[:, 0:nh], func=ACT.Sqrt, bias=eps_t[:], scale=1.0 / DH)
+            rstd = small.tile([P, 8], F32, tag="rstd")
+            nc.vector.reciprocal(out=rstd[:, 0:nh], in_=rms[:, 0:nh])
+            o0 = c0 - kg * 512
+            nc.vector.tensor_tensor(
+                out=n_bf[:, o0:o0 + cn].rearrange("p (h d) -> p h d", d=DH),
+                in0=r[:, c0:c0 + cn].rearrange("p (h d) -> p h d", d=DH),
+                in1=rstd[:, 0:nh].unsqueeze(2).to_broadcast([P, nh, DH]),
+                op=ALU.mult,
+            )
+
+        def out_pass(kg):
+            n_bf = state["nb%d" % kg]
+            nt = psc.tile([P, 4, P], BF16, tag="c")
+            for t in range(4):
+                nc.tensor.transpose(nt[:, t, :], n_bf[:, P * t:P * t + P], ident_b[:])
+            ng = small.tile([P, 512], BF16, tag="ng", align_bytes=64)
+            nc.vector.tensor_copy(out=ng[:].rearrange("p (b t) -> p b t", t=4), in_=nt[:].rearrange("p t b -> p b t"))
+            nc.vector.quantize_mx(out=ncd[:, kg, :].bitcast(FP8X4), scales=nsc[:, kg, :], in_=ng[:])
+            if kg == 0:
+                for nb in range(3):
+                    state["oa%d" % nb] = psa.tile([P, 512], F32, name="oa%d" % nb, tag="a")
+            for nb in range(3):
+                nc.tensor.matmul_mx(
+                    out=state["oa%d" % nb][:],
+                    lhsT=ncd[:, kg, :].bitcast(FP8X4),
+                    lhsT_scale=nsc[:, kg, :],
+                    rhs=wc[:, kg, 512 * nb:512 * nb + 512].bitcast(FP8X4),
+                    rhs_scale=ws[:, kg, 512 * nb:512 * nb + 512],
+                    start=(kg == 0),
+                    stop=(kg == 2),
+                )
+
+        for u in SEQ:
+            kind, idx = u[0], u[1:]
+            if kind == "p":
+                tensor_tile(int(idx))
+            elif u == "vv":
+                v_passes()
+            elif kind == "v":
+                vector_head(int(idx))
+            elif kind == "w":
+                g = int(idx)
+                if g < 3:
+                    weight_chunk(Wv, g, True)
+                else:
+                    weight_chunk(Wo, g - 3, False)
+            elif u == "n0":
+                norm(0, 8)
+            elif u == "n1":
+                norm(8, 8)
+            elif u == "n2a":
+                norm(16, 6)
+            elif u == "n2b":
+                norm(22, 2)
+            elif kind == "o":
+                out_pass(int(idx))
+        for nb in range(3):
+            ob = small.tile([P, 512], F32, tag="ob", bufs=3)
+            if nb == 1:
+                nc.scalar.copy(out=ob[:], in_=state["oa%d" % nb][:])
+            else:
+                nc.vector.tensor_copy(out=ob[:], in_=state["oa%d" % nb][:])
+            nc.sync.dma_start(out=of[:, 512 * nb:512 * nb + 512], in_=ob[:])

@@ -1,8 +1,6 @@
 from contextlib import ExitStack
 
-import concourse.bass as bass
 import concourse.mybir as mybir
-import concourse.tile as tile
 from concourse.masks import make_identity
 
 F32 = mybir.dt.float32
@@ -21,10 +19,11 @@ EPS = 1e-6
 FLOPS = 2 * 2 * B * E * V + 4 * B * H * DH * DK
 
 N_PAIR = 3
-V_HEADS = (6, 7, 8, 9, 10, 11, 18, 19, 20, 21, 22, 23)
-RED = ("VS", "VS", "VS", "SS", "SS", "SS", "SS", "SS", "SS", "SS", "SS", "SV")
-SEQ = ("p0", "v0", "p1", "w0", "p2", "v1", "p3", "w1", "p4", "v2", "p5", "w2", "vv",
-       "v3", "n0", "w3", "o0", "v4", "v5", "w4", "v6", "v7", "n1", "o1", "w5", "v8", "v9", "v10", "n2a", "v11", "n2b", "o2")
+V_PAIRS = (6, 8, 10, 18, 20, 22)
+CCH = 16
+UNITS = ((0, 6), (3, 4), (1, 7), (5, 9), (2, 8), (10, 11))
+SEQ = ("p0", "v0", "w0", "p1", "v1", "w1", "p2", "v2", "w2", "vv", "n0", "n1", "p3", "v3", "w3", "o0",
+       "n2", "n3", "p4", "w4", "o1", "p5", "v4", "w5", "n4", "v5", "n5", "o2")
 
 
 def tile_multiscaleretention_pb_kernel(tc, x, qr, kr, decay, prev_kv, Wv, Wo, out):
@@ -43,12 +42,13 @@ def tile_multiscaleretention_pb_kernel(tc, x, qr, kr, decay, prev_kv, Wv, Wo, ou
         grpp = ctx.enter_context(tc.tile_pool(name="grpp", bufs=2))
         xpp = ctx.enter_context(tc.tile_pool(name="xpp", bufs=2))
         zp = ctx.enter_context(tc.tile_pool(name="zp", bufs=2))
-        xvp = ctx.enter_context(tc.tile_pool(name="xvp", bufs=3))
-        prp = ctx.enter_context(tc.tile_pool(name="prp", bufs=2))
+        xvp = ctx.enter_context(tc.tile_pool(name="xvp", bufs=2))
+        prp = ctx.enter_context(tc.tile_pool(name="prp", bufs=3))
         ctp = ctx.enter_context(tc.tile_pool(name="ctp", bufs=1))
         psa = ctx.enter_context(tc.psum_pool(name="psa", bufs=3))
-        psb = ctx.enter_context(tc.psum_pool(name="psb", bufs=2))
-        psc = ctx.enter_context(tc.psum_pool(name="psc", bufs=3))
+        psb = ctx.enter_context(tc.psum_pool(name="psb", bufs=1))
+        psc = ctx.enter_context(tc.psum_pool(name="psc", bufs=2))
+        psr = ctx.enter_context(tc.psum_pool(name="psr", bufs=2))
 
         q_sb = keep.tile([P, E], BF16)
         nc.sync.dma_start(out=q_sb[:], in_=qf)
@@ -70,11 +70,11 @@ def tile_multiscaleretention_pb_kernel(tc, x, qr, kr, decay, prev_kv, Wv, Wo, ou
 
         dec_f = keep.tile([P, H], F32)
         nc.vector.tensor_copy(out=dec_f[:], in_=dec_b[:])
-        qd = keep.tile([P, H, DK], F32)
+        qd = keep.tile([P, 12, DK], F32)
         nc.vector.tensor_tensor(
-            out=qd[:],
-            in0=q_sb[:].rearrange("p (h c) -> p h c", c=DK),
-            in1=dec_f[:].unsqueeze(2).to_broadcast([P, H, DK]),
+            out=qd[:].rearrange("p (hh hp) c -> p hh hp c", hh=2),
+            in0=q_sb[:].rearrange("p (hh hp c) -> p hh hp c", hh=2, c=DK)[:, :, 6:12, :],
+            in1=dec_f[:].rearrange("p (hh hp) -> p hh hp", hh=2)[:, :, 6:12].unsqueeze(3).to_broadcast([P, 2, 6, DK]),
             op=ALU.mult,
         )
 
@@ -92,7 +92,7 @@ def tile_multiscaleretention_pb_kernel(tc, x, qr, kr, decay, prev_kv, Wv, Wo, ou
                 for hh in range(2):
                     for e in range(2):
                         nc.tensor.transpose(pq[:, a * 4 + hh * 2 + e, :], qzv[:, 2 * t + a, hh, e, :], ident_b[:])
-            nc.vector.tensor_copy(out=rqv[:, t], in_=pq[:].rearrange("p n b -> p b n"))
+            nc.scalar.copy(out=rqv[:, t], in_=pq[:].rearrange("p n b -> p b n"))
 
         qk = prp.tile([P, H, DK], F32, tag="prod")
         nc.vector.tensor_tensor(
@@ -118,27 +118,29 @@ def tile_multiscaleretention_pb_kernel(tc, x, qr, kr, decay, prev_kv, Wv, Wo, ou
 
         wc = keep.tile([P, 3, V], U32, align_bytes=64)
         ws = keep.tile([P, 3, V], U8, align_bytes=64)
-        sv = keep.tile([P, V], F32)
-        r = keep.tile([P, V], F32)
+        sv = keep.tile([P, 12, P], F32)
+        r = keep.tile([P, 12, P], F32)
         ncd = keep.tile([P, 3, P], U32, align_bytes=64)
         nsc = keep.tile([P, 3, P], U8, align_bytes=64)
         state = {}
 
-        def weight_chunk(w, g, paired):
+        def weight_chunk(w, g, first):
             raw = rawp.tile([P, 4, V], BF16, tag="raw")
-            if paired:
+            if first:
                 for u in range(2):
                     nc.sync.dma_start(
                         out=raw[:, 2 * u:2 * u + 2, :],
                         in_=w[512 * g + 256 * u:512 * g + 256 * u + 256, :].rearrange("(q e) c -> q e c", e=2),
                     )
             else:
-                nc.sync.dma_start(out=raw[:], in_=w[512 * g:512 * g + 512, :].rearrange("(t p) c -> p t c", p=P))
+                for tb in range(4):
+                    blk = UNITS[2 * g + tb // 2][tb % 2]
+                    nc.sync.dma_start(out=raw[:, tb, :], in_=w[P * blk:P * blk + P, :])
             pieces = ((0, 1024), (1024, 512))
             grps = []
             for w0, wn in pieces:
                 grp = grpp.tile([P, 4096], BF16, tag="grp", align_bytes=64)
-                nc.vector.tensor_copy(
+                nc.scalar.copy(
                     out=grp[:, 0:4 * wn].rearrange("p (c i t) -> p c t i", i=4, t=4),
                     in_=raw[:, :, w0:w0 + wn].rearrange("p t (c i) -> p c t i", i=4),
                 )
@@ -162,33 +164,38 @@ def tile_multiscaleretention_pb_kernel(tc, x, qr, kr, decay, prev_kv, Wv, Wo, ou
                         stop=(g == 2),
                     )
                 nc.vector.tensor_tensor(
-                    out=sv[:, 512 * nb:512 * nb + 512].rearrange("p (h d) -> p h d", d=DH),
+                    out=sv[:, 4 * nb:4 * nb + 4, :].rearrange("p k (h d) -> p (k h) d", d=DH),
                     in0=acc[:].rearrange("p (h d) -> p h d", d=DH),
                     in1=s_t[:, 8 * nb:8 * nb + 8].unsqueeze(2).to_broadcast([P, 8, DH]),
                     op=ALU.mult,
                 )
 
-        def vector_head(vi):
-            h = V_HEADS[vi]
-            xv = xvp.tile([P, HEAD], BF16, tag="xv")
-            nc.sync.dma_start(out=xv[:], in_=pb[:, h * HEAD:(h + 1) * HEAD])
-            for half in range(2):
-                prod = prp.tile([P, 32, DK], F32, tag="prod")
-                nc.vector.tensor_tensor(
-                    out=prod[:],
-                    in0=xv[:, half * 2048:(half + 1) * 2048].rearrange("p (d c) -> p d c", c=DK),
-                    in1=qd[:, h, :].unsqueeze(1).to_broadcast([P, 32, DK]),
-                    op=ALU.mult,
-                )
-                c0 = h * DH + half * 32
-                if RED[vi][half] == "V":
-                    nc.vector.tensor_reduce(out=r[:, c0:c0 + 32], in_=prod[:], axis=AX.X, op=ALU.add)
-                else:
-                    for dd in range(32):
-                        nc.scalar.activation(
-                            out=prod[:, dd, :], in_=prod[:, dd, :], func=ACT.Copy,
-                            accum_out=r[:, c0 + dd:c0 + dd + 1],
-                        )
+        def vector_pair(vi):
+            h0 = V_PAIRS[vi]
+            xv = xvp.tile([P, 2 * HEAD], BF16, tag="xv")
+            nc.sync.dma_start(out=xv[:], in_=pb[:, h0 * HEAD:(h0 + 2) * HEAD])
+            racc = psr.tile([P, P], F32, tag="r")
+            for ch in range(DK // CCH):
+                c0 = ch * CCH
+                pc = prp.tile([P, CCH, 2, DH], F32, tag="prod")
+                for a in range(2):
+                    nc.vector.tensor_tensor(
+                        out=pc[:, :, a, :].rearrange("p c (k i) -> p k c i", i=4),
+                        in0=xv[:, a * HEAD:(a + 1) * HEAD].rearrange("p (d c) -> p d c", c=DK)[:, :, c0:c0 + CCH]
+                        .rearrange("p (k i) c -> p k c i", i=4),
+                        in1=qd[:, 2 * vi + a, c0:c0 + CCH].unsqueeze(1).unsqueeze(3).to_broadcast([P, DH // 4, CCH, 4]),
+                        op=ALU.mult,
+                    )
+                for c in range(CCH):
+                    nc.tensor.matmul(
+                        out=racc[:], lhsT=pc[:, c, :, :].rearrange("p a d -> p (a d)"), rhs=ident_f[:],
+                        is_transpose=True, start=(c0 + c == 0), stop=(c0 + c == DK - 1),
+                    )
+            rt = small.tile([P, P], F32, tag="rt")
+            nc.scalar.copy(out=rt[:], in_=racc[:])
+            rbk = psc.tile([P, P], F32, tag="c")
+            nc.tensor.transpose(rbk[:], rt[:], ident_f[:])
+            nc.scalar.copy(out=r[:, h0 // 2, :], in_=rbk[:])
 
         def tensor_tile(i):
             t, half = i // 2, i % 2
@@ -221,57 +228,64 @@ def tile_multiscaleretention_pb_kernel(tc, x, qr, kr, decay, prev_kv, Wv, Wo, ou
                         h = hh * 12 + 2 * t + a
                         m0 = 64 * a + hh
                         nc.vector.tensor_scalar_mul(
-                            out=r[:, h * DH:(h + 1) * DH].rearrange("p (j e) -> p j e", e=2),
+                            out=r[:, h // 2, (h % 2) * DH:(h % 2) * DH + DH].rearrange("p (j e) -> p j e", e=2),
                             in0=rb[:, 2 * hh:2 * hh + 2, m0:m0 + 63:2].rearrange("p e j -> p j e"),
                             scalar1=dec_f[:, h:h + 1],
                         )
 
-        def norm(h0, nh):
-            c0, cn = h0 * DH, nh * DH
-            kg = h0 // 8
-            if "nb%d" % kg not in state:
-                state["nb%d" % kg] = keep.tile([P, 512], BF16, name="nbf%d" % kg)
+        def norm(ui):
+            b0, b1 = UNITS[ui]
+            step = b1 - b0
+            kg = ui // 2
+            if ui % 2 == 0:
+                state["nb%d" % kg] = keep.tile([P, 4, P], BF16, name="nbf%d" % kg)
             n_bf = state["nb%d" % kg]
-            nc.vector.tensor_tensor(out=r[:, c0:c0 + cn], in0=r[:, c0:c0 + cn], in1=sv[:, c0:c0 + cn], op=ALU.add)
-            sq = small.tile([P, 8, DH], F32, tag="sq")
-            nc.vector.tensor_tensor(
-                out=sq[:, 0:nh, :].rearrange("p h d -> p (h d)"), in0=r[:, c0:c0 + cn], in1=r[:, c0:c0 + cn], op=ALU.mult
-            )
-            ss = small.tile([P, 8], F32, tag="ss")
-            nc.vector.tensor_reduce(out=ss[:, 0:nh], in_=sq[:, 0:nh, :], axis=AX.X, op=ALU.add)
-            rms = small.tile([P, 8], F32, tag="rms")
-            nc.scalar.activation(out=rms[:, 0:nh], in_=ss[:, 0:nh], func=ACT.Sqrt, bias=eps_t[:], scale=1.0 / DH)
-            rstd = small.tile([P, 8], F32, tag="rstd")
-            nc.vector.reciprocal(out=rstd[:, 0:nh], in_=rms[:, 0:nh])
-            o0 = c0 - kg * 512
-            nc.vector.tensor_tensor(
-                out=n_bf[:, o0:o0 + cn].rearrange("p (h d) -> p h d", d=DH),
-                in0=r[:, c0:c0 + cn].rearrange("p (h d) -> p h d", d=DH),
-                in1=rstd[:, 0:nh].unsqueeze(2).to_broadcast([P, nh, DH]),
-                op=ALU.mult,
-            )
+            rv = r[:, b0:b1 + 1:step, :]
+            nc.vector.tensor_tensor(out=rv, in0=rv, in1=sv[:, b0:b1 + 1:step, :], op=ALU.add)
+            sq = small.tile([P, 2, P], F32, tag="sq")
+            nc.vector.tensor_tensor(out=sq[:], in0=rv, in1=rv, op=ALU.mult)
+            ss = small.tile([P, 4], F32, tag="ss")
+            nc.vector.tensor_reduce(out=ss[:], in_=sq[:].rearrange("p k (h d) -> p (k h) d", d=DH), axis=AX.X, op=ALU.add)
+            rms = small.tile([P, 4], F32, tag="rms")
+            nc.scalar.activation(out=rms[:], in_=ss[:], func=ACT.Sqrt, bias=eps_t[:], scale=1.0 / DH)
+            rstd = small.tile([P, 4], F32, tag="rstd")
+            nc.vector.reciprocal(out=rstd[:], in_=rms[:])
+            for k in range(2):
+                nc.vector.tensor_tensor(
+                    out=n_bf[:, 2 * (ui % 2) + k, :].rearrange("p (h d) -> p h d", d=DH),
+                    in0=r[:, b0 + k * step, :].rearrange("p (h d) -> p h d", d=DH),
+                    in1=rstd[:, 2 * k:2 * k + 2].unsqueeze(2).to_broadcast([P, 2, DH]),
+                    op=ALU.mult,
+                )
 
         def out_pass(kg):
             n_bf = state["nb%d" % kg]
             nt = psc.tile([P, 4, P], BF16, tag="c")
             for t in range(4):
-                nc.tensor.transpose(nt[:, t, :], n_bf[:, P * t:P * t + P], ident_b[:])
+                nc.tensor.transpose(nt[:, t, :], n_bf[:, t, :], ident_b[:])
             ng = small.tile([P, 512], BF16, tag="ng", align_bytes=64)
             nc.vector.tensor_copy(out=ng[:].rearrange("p (b t) -> p b t", t=4), in_=nt[:].rearrange("p t b -> p b t"))
             nc.vector.quantize_mx(out=ncd[:, kg, :].bitcast(FP8X4), scales=nsc[:, kg, :], in_=ng[:])
-            if kg == 0:
-                for nb in range(3):
-                    state["oa%d" % nb] = psa.tile([P, 512], F32, name="oa%d" % nb, tag="a")
+
+        def final_passes():
             for nb in range(3):
-                nc.tensor.matmul_mx(
-                    out=state["oa%d" % nb][:],
-                    lhsT=ncd[:, kg, :].bitcast(FP8X4),
-                    lhsT_scale=nsc[:, kg, :],
-                    rhs=wc[:, kg, 512 * nb:512 * nb + 512].bitcast(FP8X4),
-                    rhs_scale=ws[:, kg, 512 * nb:512 * nb + 512],
-                    start=(kg == 0),
-                    stop=(kg == 2),
-                )
+                oa = psa.tile([P, 512], F32, tag="a")
+                for kg in range(3):
+                    nc.tensor.matmul_mx(
+                        out=oa[:],
+                        lhsT=ncd[:, kg, :].bitcast(FP8X4),
+                        lhsT_scale=nsc[:, kg, :],
+                        rhs=wc[:, kg, 512 * nb:512 * nb + 512].bitcast(FP8X4),
+                        rhs_scale=ws[:, kg, 512 * nb:512 * nb + 512],
+                        start=(kg == 0),
+                        stop=(kg == 2),
+                    )
+                ob = prp.tile([P, 512], F32, tag="prod")
+                if nb == 1:
+                    nc.scalar.copy(out=ob[:], in_=oa[:])
+                else:
+                    nc.vector.tensor_copy(out=ob[:], in_=oa[:])
+                nc.sync.dma_start(out=of[:, 512 * nb:512 * nb + 512], in_=ob[:])
 
         for u in SEQ:
             kind, idx = u[0], u[1:]
@@ -280,27 +294,15 @@ def tile_multiscaleretention_pb_kernel(tc, x, qr, kr, decay, prev_kv, Wv, Wo, ou
             elif u == "vv":
                 v_passes()
             elif kind == "v":
-                vector_head(int(idx))
+                vector_pair(int(idx))
             elif kind == "w":
                 g = int(idx)
                 if g < 3:
                     weight_chunk(Wv, g, True)
                 else:
                     weight_chunk(Wo, g - 3, False)
-            elif u == "n0":
-                norm(0, 8)
-            elif u == "n1":
-                norm(8, 8)
-            elif u == "n2a":
-                norm(16, 6)
-            elif u == "n2b":
-                norm(22, 2)
+            elif kind == "n":
+                norm(int(idx))
             elif kind == "o":
                 out_pass(int(idx))
-        for nb in range(3):
-            ob = small.tile([P, 512], F32, tag="ob", bufs=3)
-            if nb == 1:
-                nc.scalar.copy(out=ob[:], in_=state["oa%d" % nb][:])
-            else:
-                nc.vector.tensor_copy(out=ob[:], in_=state["oa%d" % nb][:])
-            nc.sync.dma_start(out=of[:, 512 * nb:512 * nb + 512], in_=ob[:])
+        final_passes()

@@ -180,10 +180,11 @@ def tile_multiscaleretention_pb_kernel(tc, x, qr, kr, decay, prev_kv, Wv, Wo, ou
                 pc = prp.tile([P, CCH, 2, DH], F32, tag="prod")
                 for a in range(2):
                     nc.vector.tensor_tensor(
-                        out=pc[:, :, a, :].rearrange("p c (k i) -> p k c i", i=4),
+                        out=pc[:, :, a, :].rearrange("p (k i) d -> p k d i", i=4),
                         in0=xv[:, a * HEAD:(a + 1) * HEAD].rearrange("p (d c) -> p d c", c=DK)[:, :, c0:c0 + CCH]
-                        .rearrange("p (k i) c -> p k c i", i=4),
-                        in1=qd[:, 2 * vi + a, c0:c0 + CCH].unsqueeze(1).unsqueeze(3).to_broadcast([P, DH // 4, CCH, 4]),
+                        .rearrange("p d (k i) -> p k d i", i=4),
+                        in1=qd[:, 2 * vi + a, c0:c0 + CCH].rearrange("p (k i) -> p k i", i=4).unsqueeze(2)
+                        .to_broadcast([P, CCH // 4, DH, 4]),
                         op=ALU.mult,
                     )
                 for c in range(CCH):
@@ -208,7 +209,10 @@ def tile_multiscaleretention_pb_kernel(tc, x, qr, kr, decay, prev_kv, Wv, Wo, ou
                 for k in range(8):
                     s = 8 * sg + k
                     nc.tensor.transpose(tp[:, k, :], xp[:, s * P:(s + 1) * P], ident_b[:])
-                nc.scalar.copy(out=zw[:, :, 8 * sg:8 * sg + 8], in_=tp[:].bitcast(F32).rearrange("p k w -> p w k"))
+                nc.scalar.copy(
+                    out=zw[:, :, 8 * sg:8 * sg + 8].rearrange("p (v i) k -> p v k i", i=2),
+                    in_=tp[:].bitcast(F32).rearrange("p k (v i) -> p v k i", i=2),
+                )
             mm = psb.tile([P, 64, 8], F32, tag="b")
             for bi in range(64):
                 nc.tensor.matmul(
@@ -218,7 +222,7 @@ def tile_multiscaleretention_pb_kernel(tc, x, qr, kr, decay, prev_kv, Wv, Wo, ou
             if half == 0:
                 state["ct"] = ctp.tile([P, 8, P], F32, name="ct", tag="ct")
             ct = state["ct"]
-            nc.vector.tensor_copy(out=ct[:, :, 64 * half:64 * half + 64], in_=mm[:].rearrange("p b n -> p n b"))
+            nc.scalar.copy(out=ct[:, :, 64 * half:64 * half + 64], in_=mm[:].rearrange("p b n -> p n b"))
             if half == 1:
                 for a in range(2):
                     rb = psc.tile([P, 4, P], F32, tag="c")

@@ -101,8 +101,8 @@ def tile_multiscaleretention_pb_kernel(tc, x, qr, kr, decay, prev_kv, Wv, Wo, ou
         s_t = keep.tile([P, H], F32)
         nc.vector.tensor_reduce(out=s_t[:], in_=qk[:], axis=AX.X, op=ALU.add)
 
-        xc = keep.tile([P, 3, P], U32, align_bytes=64)
-        xs = keep.tile([P, 3, P], U8, align_bytes=64)
+        xc = keep.tile([P, 4, P], U32, align_bytes=64)
+        xs = keep.tile([P, 4, P], U8, align_bytes=64)
         xw = x_sb[:].bitcast(F32)
         xg = grpp.tile([P, 3 * 512], BF16, tag="grp", align_bytes=64)
         for g in range(3):
@@ -113,8 +113,10 @@ def tile_multiscaleretention_pb_kernel(tc, x, qr, kr, decay, prev_kv, Wv, Wo, ou
                 out=xg[:, 512 * g:512 * g + 512].bitcast(F32).rearrange("p (b u) -> p b u", u=2),
                 in_=xt[:].rearrange("p u b -> p b u"),
             )
-        for g in range(3):
-            nc.vector.quantize_mx(out=xc[:, g, :].bitcast(FP8X4), scales=xs[:, g, :], in_=xg[:, 512 * g:512 * g + 512])
+        for g in range(4):
+            nc.vector.quantize_mx(
+                out=xc[:, g, :].bitcast(FP8X4), scales=xs[:, g, :], in_=xg[:, 512 * (g % 3):512 * (g % 3) + 512]
+            )
 
         wc = keep.tile([P, 3, V], U32, align_bytes=64)
         ws = keep.tile([P, 3, V], U8, align_bytes=64)
@@ -123,6 +125,14 @@ def tile_multiscaleretention_pb_kernel(tc, x, qr, kr, decay, prev_kv, Wv, Wo, ou
         ncd = keep.tile([P, 3, P], U32, align_bytes=64)
         nsc = keep.tile([P, 3, P], U8, align_bytes=64)
         state = {}
+
+        def idle_pass():
+            dm = psa.tile([P, 512], F32, tag="a")
+            nc.tensor.matmul_mx(
+                out=dm[:], lhsT=xc[:, 0, :].bitcast(FP8X4), lhsT_scale=xs[:, 0, :],
+                rhs=xc[:].rearrange("p g b -> p (g b)").bitcast(FP8X4), rhs_scale=xs[:].rearrange("p g b -> p (g b)"),
+                start=True, stop=True,
+            )
 
         def weight_chunk(w, g, first):
             raw = rawp.tile([P, 4, V], BF16, tag="raw")
@@ -192,6 +202,7 @@ def tile_multiscaleretention_pb_kernel(tc, x, qr, kr, decay, prev_kv, Wv, Wo, ou
                         out=racc[:], lhsT=pc[:, c, :, :].rearrange("p a d -> p (a d)"), rhs=ident_f[:],
                         is_transpose=True, start=(c0 + c == 0), stop=(c0 + c == DK - 1),
                     )
+                idle_pass()
             rt = small.tile([P, P], F32, tag="rt")
             nc.scalar.copy(out=rt[:], in_=racc[:])
             rbk = psc.tile([P, P], F32, tag="c")
@@ -213,6 +224,7 @@ def tile_multiscaleretention_pb_kernel(tc, x, qr, kr, decay, prev_kv, Wv, Wo, ou
                     out=zw[:, :, 8 * sg:8 * sg + 8].rearrange("p (v i) k -> p v k i", i=2),
                     in_=tp[:].bitcast(F32).rearrange("p k (v i) -> p v k i", i=2),
                 )
+                idle_pass()
             mm = psb.tile([P, 64, 8], F32, tag="b")
             for bi in range(64):
                 nc.tensor.matmul(

@@ -45,10 +45,10 @@ def tile_multiscaleretention_pb_kernel(tc, x, qr, kr, decay, prev_kv, Wv, Wo, ou
         xvp = ctx.enter_context(tc.tile_pool(name="xvp", bufs=2))
         prp = ctx.enter_context(tc.tile_pool(name="prp", bufs=3))
         ctp = ctx.enter_context(tc.tile_pool(name="ctp", bufs=1))
-        psa = ctx.enter_context(tc.psum_pool(name="psa", bufs=3))
+        psa = ctx.enter_context(tc.psum_pool(name="psa", bufs=4))
         psb = ctx.enter_context(tc.psum_pool(name="psb", bufs=1))
         psc = ctx.enter_context(tc.psum_pool(name="psc", bufs=2))
-        psr = ctx.enter_context(tc.psum_pool(name="psr", bufs=2))
+        psr = ctx.enter_context(tc.psum_pool(name="psr", bufs=1))
 
         q_sb = keep.tile([P, E], BF16)
         nc.sync.dma_start(out=q_sb[:], in_=qf)
@@ -101,8 +101,8 @@ def tile_multiscaleretention_pb_kernel(tc, x, qr, kr, decay, prev_kv, Wv, Wo, ou
         s_t = keep.tile([P, H], F32)
         nc.vector.tensor_reduce(out=s_t[:], in_=qk[:], axis=AX.X, op=ALU.add)
 
-        xc = keep.tile([P, 4, P], U32, align_bytes=64)
-        xs = keep.tile([P, 4, P], U8, align_bytes=64)
+        xc = keep.tile([P, 3, P], U32, align_bytes=64)
+        xs = keep.tile([P, 3, P], U8, align_bytes=64)
         xw = x_sb[:].bitcast(F32)
         xg = grpp.tile([P, 3 * 512], BF16, tag="grp", align_bytes=64)
         for g in range(3):
@@ -113,10 +113,8 @@ def tile_multiscaleretention_pb_kernel(tc, x, qr, kr, decay, prev_kv, Wv, Wo, ou
                 out=xg[:, 512 * g:512 * g + 512].bitcast(F32).rearrange("p (b u) -> p b u", u=2),
                 in_=xt[:].rearrange("p u b -> p b u"),
             )
-        for g in range(4):
-            nc.vector.quantize_mx(
-                out=xc[:, g, :].bitcast(FP8X4), scales=xs[:, g, :], in_=xg[:, 512 * (g % 3):512 * (g % 3) + 512]
-            )
+        for g in range(3):
+            nc.vector.quantize_mx(out=xc[:, g, :].bitcast(FP8X4), scales=xs[:, g, :], in_=xg[:, 512 * g:512 * g + 512])
 
         wc = keep.tile([P, 3, V], U32, align_bytes=64)
         ws = keep.tile([P, 3, V], U8, align_bytes=64)
@@ -125,14 +123,6 @@ def tile_multiscaleretention_pb_kernel(tc, x, qr, kr, decay, prev_kv, Wv, Wo, ou
         ncd = keep.tile([P, 3, P], U32, align_bytes=64)
         nsc = keep.tile([P, 3, P], U8, align_bytes=64)
         state = {}
-
-        def idle_pass():
-            dm = psa.tile([P, 512], F32, tag="a")
-            nc.tensor.matmul_mx(
-                out=dm[:], lhsT=xc[:, 0, :].bitcast(FP8X4), lhsT_scale=xs[:, 0, :],
-                rhs=xc[:].rearrange("p g b -> p (g b)").bitcast(FP8X4), rhs_scale=xs[:].rearrange("p g b -> p (g b)"),
-                start=True, stop=True,
-            )
 
         def weight_chunk(w, g, first):
             raw = rawp.tile([P, 4, V], BF16, tag="raw")
@@ -202,7 +192,6 @@ def tile_multiscaleretention_pb_kernel(tc, x, qr, kr, decay, prev_kv, Wv, Wo, ou
                         out=racc[:], lhsT=pc[:, c, :, :].rearrange("p a d -> p (a d)"), rhs=ident_f[:],
                         is_transpose=True, start=(c0 + c == 0), stop=(c0 + c == DK - 1),
                     )
-                idle_pass()
             rt = small.tile([P, P], F32, tag="rt")
             nc.scalar.copy(out=rt[:], in_=racc[:])
             rbk = psc.tile([P, P], F32, tag="c")
@@ -215,16 +204,15 @@ def tile_multiscaleretention_pb_kernel(tc, x, qr, kr, decay, prev_kv, Wv, Wo, ou
             nc.sync.dma_start(out=xp[:], in_=pp[P * half:P * half + P, 2 * t * HEAD:(2 * t + 2) * HEAD])
             z = zp.tile([P, 64 * P], BF16, tag="z")
             zw = z[:].bitcast(F32).rearrange("p (b s) -> p b s", s=64)
-            for sg in range(8):
-                tp = psa.tile([P, 8, P], BF16, tag="a")
-                for k in range(8):
-                    s = 8 * sg + k
+            for sg in range(16):
+                tp = psa.tile([P, 4, P], BF16, tag="a")
+                for k in range(4):
+                    s = 4 * sg + k
                     nc.tensor.transpose(tp[:, k, :], xp[:, s * P:(s + 1) * P], ident_b[:])
                 nc.scalar.copy(
-                    out=zw[:, :, 8 * sg:8 * sg + 8].rearrange("p (v i) k -> p v k i", i=2),
+                    out=zw[:, :, 4 * sg:4 * sg + 4].rearrange("p (v i) k -> p v k i", i=2),
                     in_=tp[:].bitcast(F32).rearrange("p k (v i) -> p v k i", i=2),
                 )
-                idle_pass()
             mm = psb.tile([P, 64, 8], F32, tag="b")
             for bi in range(64):
                 nc.tensor.matmul(

@@ -174,6 +174,24 @@ def tile_multiscaleretention_pb_kernel(tc, x, qr, kr, decay, prev_kv, Wv, Wo, ou
             h0 = V_PAIRS[vi]
             xv = xvp.tile([P, 2 * HEAD], BF16, tag="xv")
             nc.sync.dma_start(out=xv[:], in_=pb[:, h0 * HEAD:(h0 + 2) * HEAD])
+            if vi % 2 == 1:
+                for hf in range(4):
+                    prod = prp.tile([P, 32, DK], F32, tag="prod")
+                    nc.vector.tensor_tensor(
+                        out=prod[:],
+                        in0=xv[:, hf * 2048:(hf + 1) * 2048].rearrange("p (d c) -> p d c", c=DK),
+                        in1=qd[:, 2 * vi + hf // 2, :].unsqueeze(1).to_broadcast([P, 32, DK]),
+                        op=ALU.mult,
+                    )
+                    if hf == 3:
+                        nc.vector.tensor_reduce(out=r[:, h0 // 2, 96:128], in_=prod[:], axis=AX.X, op=ALU.add)
+                    else:
+                        for dd in range(32):
+                            nc.scalar.activation(
+                                out=prod[:, dd, :], in_=prod[:, dd, :], func=ACT.Copy,
+                                accum_out=r[:, h0 // 2, hf * 32 + dd:hf * 32 + dd + 1],
+                            )
+                return
             racc = psr.tile([P, P], F32, tag="r")
             for ch in range(DK // CCH):
                 c0 = ch * CCH

@@ -18,12 +18,11 @@ HEAD = DH * DK
 EPS = 1e-6
 FLOPS = 2 * 2 * B * E * V + 4 * B * H * DH * DK
 
-N_PAIR = 3
-V_PAIRS = (6, 8, 10, 18, 20, 22)
-CCH = 16
+V_HEADS = (6, 7, 8, 9, 10, 11, 18, 19, 20, 21, 22, 23)
 UNITS = ((0, 6), (3, 4), (1, 7), (5, 9), (2, 8), (10, 11))
-SEQ = ("p0", "v0", "w0", "p1", "v1", "w1", "p2", "v2", "w2", "vv", "n0", "n1", "p3", "v3", "w3", "o0",
-       "n2", "n3", "p4", "w4", "o1", "p5", "v4", "w5", "n4", "v5", "n5", "o2")
+UNIT_TICK = (32, 32, 39, 37, 55, 53)
+PIECE_TICK = (2, 4, 7)
+N_TICKS = 62
 
 
 def tile_multiscaleretention_pb_kernel(tc, x, qr, kr, decay, prev_kv, Wv, Wo, out):
@@ -42,22 +41,55 @@ def tile_multiscaleretention_pb_kernel(tc, x, qr, kr, decay, prev_kv, Wv, Wo, ou
         grpp = ctx.enter_context(tc.tile_pool(name="grpp", bufs=2))
         xpp = ctx.enter_context(tc.tile_pool(name="xpp", bufs=2))
         zp = ctx.enter_context(tc.tile_pool(name="zp", bufs=2))
-        xvp = ctx.enter_context(tc.tile_pool(name="xvp", bufs=2))
-        prp = ctx.enter_context(tc.tile_pool(name="prp", bufs=3))
+        xvp = ctx.enter_context(tc.tile_pool(name="xvp", bufs=3))
+        prp = ctx.enter_context(tc.tile_pool(name="prp", bufs=4))
         ctp = ctx.enter_context(tc.tile_pool(name="ctp", bufs=1))
         psa = ctx.enter_context(tc.psum_pool(name="psa", bufs=4))
         psb = ctx.enter_context(tc.psum_pool(name="psb", bufs=1))
         psc = ctx.enter_context(tc.psum_pool(name="psc", bufs=2))
-        psr = ctx.enter_context(tc.psum_pool(name="psr", bufs=1))
+        psq = ctx.enter_context(tc.psum_pool(name="psq", bufs=1))
+        ctx.enter_context(tc.manual_schedule())
+
+        st = {}
+
+        def load_xp(i):
+            t, half = i // 2, i % 2
+            st["xp%d" % i] = xpp.tile([P, 2 * HEAD], BF16, name="xp", tag="xp")
+            nc.sync.dma_start(out=st["xp%d" % i][:], in_=pp[P * half:P * half + P, 2 * t * HEAD:(2 * t + 2) * HEAD])
+
+        def load_xv(v):
+            h = V_HEADS[v]
+            st["xv%d" % v] = xvp.tile([P, HEAD], BF16, name="xv", tag="xv")
+            nc.sync.dma_start(out=st["xv%d" % v][:], in_=pb[:, h * HEAD:(h + 1) * HEAD])
+
+        def load_raw(c):
+            raw = rawp.tile([P, 4, V], BF16, name="raw", tag="raw")
+            st["raw%d" % c] = raw
+            if c < 3:
+                for u in range(2):
+                    nc.sync.dma_start(
+                        out=raw[:, 2 * u:2 * u + 2, :],
+                        in_=Wv[512 * c + 256 * u:512 * c + 256 * u + 256, :].rearrange("(q e) c -> q e c", e=2),
+                    )
+            else:
+                for tb in range(4):
+                    blk = UNITS[2 * (c - 3) + tb // 2][tb % 2]
+                    nc.sync.dma_start(out=raw[:, tb, :], in_=Wo[P * blk:P * blk + P, :])
 
         q_sb = keep.tile([P, E], BF16)
         nc.sync.dma_start(out=q_sb[:], in_=qf)
         dec_b = keep.tile([P, H], BF16)
         nc.sync.dma_start(out=dec_b[:], in_=decay.partition_broadcast(P))
-        k_sb = rawp.tile([P, E], BF16, tag="raw")
+        load_xp(0)
+        load_xv(0)
+        k_sb = keep.tile([P, E], BF16)
         nc.sync.dma_start(out=k_sb[:], in_=kf)
-        x_sb = rawp.tile([P, E], BF16, tag="raw")
+        x_sb = keep.tile([P, E], BF16)
         nc.sync.dma_start(out=x_sb[:], in_=xf)
+        load_xv(1)
+        load_raw(0)
+        load_xp(1)
+        load_xv(2)
 
         ident_b = keep.tile([P, P], BF16)
         make_identity(nc, ident_b[:])
@@ -68,91 +100,162 @@ def tile_multiscaleretention_pb_kernel(tc, x, qr, kr, decay, prev_kv, Wv, Wo, ou
         dum = keep.tile([P, 1], F32)
         nc.scalar.activation(out=dum[:], in_=eps_t[:], func=ACT.Sqrt)
 
+        qz = zp.tile([P, 6 * 2 * 2 * P], BF16, tag="z")
+        nc.vector.memset(qz[:], 0.0)
+        qzv = qz[:].rearrange("p (hp hh e k) -> p hp hh e k", hh=2, e=2, k=P)
+        qpe = q_sb[:].rearrange("p (hh hp c) -> p hp hh c", hh=2, c=DK)[:, 0:6, :, :]
+        nc.vector.tensor_copy(out=qzv[:, :, :, 0, 0:DK], in_=qpe)
+        nc.vector.tensor_copy(out=qzv[:, :, :, 1, DK:P], in_=qpe)
         dec_f = keep.tile([P, H], F32)
         nc.vector.tensor_copy(out=dec_f[:], in_=dec_b[:])
         qd = keep.tile([P, 12, DK], F32)
-        nc.vector.tensor_tensor(
+        nc.gpsimd.tensor_tensor(
             out=qd[:].rearrange("p (hh hp) c -> p hh hp c", hh=2),
             in0=q_sb[:].rearrange("p (hh hp c) -> p hh hp c", hh=2, c=DK)[:, :, 6:12, :],
             in1=dec_f[:].rearrange("p (hh hp) -> p hh hp", hh=2)[:, :, 6:12].unsqueeze(3).to_broadcast([P, 2, 6, DK]),
             op=ALU.mult,
         )
+        qtp = psa.tile([P, 6, P], BF16, tag="a")
+        for j in range(6):
+            nc.tensor.transpose(qtp[:, j, :], q_sb[:, V_HEADS[2 * j] * DK:V_HEADS[2 * j] * DK + P], ident_b[:])
+        q_t = keep.tile([P, 6, P], BF16)
+        nc.scalar.copy(out=q_t[:], in_=qtp[:])
+        qps = psq.tile([P, 12, DK], BF16, tag="q")
+        for j in range(6):
+            nc.tensor.transpose(qps[:, 2 * j:2 * j + 2, :].rearrange("p a c -> p (a c)"), q_t[:, j, :], ident_b[:])
+        qk = keep.tile([P, H, DK], F32)
+        nc.gpsimd.tensor_tensor(out=qk[:].rearrange("p h c -> p (h c)"), in0=q_sb[:], in1=k_sb[:], op=ALU.mult)
 
-        qz = zp.tile([P, 2 * N_PAIR * 2 * 2 * P], BF16, tag="z")
-        nc.vector.memset(qz[:], 0.0)
-        qzv = qz[:].rearrange("p (hp hh e k) -> p hp hh e k", hh=2, e=2, k=P)
-        qpe = q_sb[:].rearrange("p (hh hp c) -> p hp hh c", hh=2, c=DK)[:, 0:2 * N_PAIR, :, :]
-        nc.vector.tensor_copy(out=qzv[:, :, :, 0, 0:DK], in_=qpe)
-        nc.vector.tensor_copy(out=qzv[:, :, :, 1, DK:P], in_=qpe)
-        rq = keep.tile([P, N_PAIR * P * 8], BF16)
+        rq = keep.tile([P, 3 * P * 8], BF16)
         rqv = rq[:].rearrange("p (t b n) -> p t b n", b=P, n=8)
-        for t in range(N_PAIR):
-            pq = psc.tile([P, 8, P], BF16, tag="c")
-            for a in range(2):
-                for hh in range(2):
-                    for e in range(2):
-                        nc.tensor.transpose(pq[:, a * 4 + hh * 2 + e, :], qzv[:, 2 * t + a, hh, e, :], ident_b[:])
-            nc.scalar.copy(out=rqv[:, t], in_=pq[:].rearrange("p n b -> p b n"))
-
-        qk = prp.tile([P, H, DK], F32, tag="prod")
-        nc.vector.tensor_tensor(
-            out=qk[:].rearrange("p h c -> p (h c)"), in0=q_sb[:], in1=k_sb[:], op=ALU.mult
-        )
         s_t = keep.tile([P, H], F32)
-        nc.vector.tensor_reduce(out=s_t[:], in_=qk[:], axis=AX.X, op=ALU.add)
-
         xc = keep.tile([P, 3, P], U32, align_bytes=64)
         xs = keep.tile([P, 3, P], U8, align_bytes=64)
-        xw = x_sb[:].bitcast(F32)
-        xg = grpp.tile([P, 3 * 512], BF16, tag="grp", align_bytes=64)
-        for g in range(3):
-            xt = psc.tile([P, 2, P], F32, tag="c")
-            for u in range(2):
-                nc.tensor.transpose(xt[:, u, :], xw[:, 256 * g + 128 * u:256 * g + 128 * u + 128], ident_f[:])
-            nc.vector.tensor_copy(
-                out=xg[:, 512 * g:512 * g + 512].bitcast(F32).rearrange("p (b u) -> p b u", u=2),
-                in_=xt[:].rearrange("p u b -> p b u"),
-            )
-        for g in range(3):
-            nc.vector.quantize_mx(out=xc[:, g, :].bitcast(FP8X4), scales=xs[:, g, :], in_=xg[:, 512 * g:512 * g + 512])
-
         wc = keep.tile([P, 3, V], U32, align_bytes=64)
         ws = keep.tile([P, 3, V], U8, align_bytes=64)
         sv = keep.tile([P, 12, P], F32)
         r = keep.tile([P, 12, P], F32)
         ncd = keep.tile([P, 3, P], U32, align_bytes=64)
         nsc = keep.tile([P, 3, P], U8, align_bytes=64)
-        state = {}
 
-        def weight_chunk(w, g, first):
-            raw = rawp.tile([P, 4, V], BF16, tag="raw")
-            if first:
-                for u in range(2):
-                    nc.sync.dma_start(
-                        out=raw[:, 2 * u:2 * u + 2, :],
-                        in_=w[512 * g + 256 * u:512 * g + 256 * u + 256, :].rearrange("(q e) c -> q e c", e=2),
+        def rq_transposes(t):
+            pq = psa.tile([P, 8, P], BF16, name="pq", tag="a")
+            st["pq"] = pq
+            for a in range(2):
+                for hh in range(2):
+                    for e in range(2):
+                        nc.tensor.transpose(pq[:, a * 4 + hh * 2 + e, :], qzv[:, 2 * t + a, hh, e, :], ident_b[:])
+
+        def rq_copy(t):
+            nc.scalar.copy(out=rqv[:, t], in_=st["pq"][:].rearrange("p n b -> p b n"))
+
+        def transposes(i, g):
+            xp = st["xp%d" % i]
+            if g == 0:
+                st["z%d" % i] = zp.tile([P, 64 * P], BF16, name="z", tag="z")
+            zw = st["z%d" % i][:].bitcast(F32).rearrange("p (b s) -> p b s", s=64)
+            tp = psa.tile([P, 4, P], BF16, tag="a")
+            for k in range(4):
+                s = 4 * g + k
+                nc.tensor.transpose(tp[:, k, :], xp[:, s * P:(s + 1) * P], ident_b[:])
+            nc.scalar.copy(
+                out=zw[:, :, 4 * g:4 * g + 4].rearrange("p (v i) k -> p v k i", i=2),
+                in_=tp[:].bitcast(F32).rearrange("p k (v i) -> p v k i", i=2),
+            )
+
+        def readout_matmuls(i, q):
+            t, half = i // 2, i % 2
+            if q == 0:
+                st["mm"] = psb.tile([P, 64, 8], F32, name="mm", tag="b")
+            z = st["z%d" % i]
+            for bi in range(16 * q, 16 * q + 16):
+                nc.tensor.matmul(
+                    out=st["mm"][:, bi, :], lhsT=z[:, bi * P:(bi + 1) * P], rhs=rqv[:, t, 64 * half + bi, :],
+                    start=True, stop=True,
+                )
+
+        def collect(i):
+            half = i % 2
+            if half == 0:
+                st["ct"] = ctp.tile([P, 8, P], F32, name="ct", tag="ct")
+            nc.scalar.copy(out=st["ct"][:, :, 64 * half:64 * half + 64], in_=st["mm"][:].rearrange("p b n -> p n b"))
+
+        def back_transposes():
+            for a in range(2):
+                rb = psc.tile([P, 4, P], F32, name="rb", tag="c")
+                st["rb%d" % a] = rb
+                for n in range(4):
+                    nc.tensor.transpose(rb[:, n, :], st["ct"][:, 4 * a + n, :], ident_f[:])
+
+        def back_copies(t):
+            for a in range(2):
+                for hh in range(2):
+                    h = hh * 12 + 2 * t + a
+                    m0 = 64 * a + hh
+                    nc.scalar.activation(
+                        out=r[:, h // 2, (h % 2) * DH:(h % 2) * DH + DH].rearrange("p (j e) -> p j e", e=2),
+                        in_=st["rb%d" % a][:, 2 * hh:2 * hh + 2, m0:m0 + 63:2].rearrange("p e j -> p j e"),
+                        func=ACT.Copy, scale=dec_f[:, h:h + 1],
                     )
+
+        def product(hf):
+            v, half = hf // 2, hf % 2
+            xv = st["xv%d" % v]
+            prod = prp.tile([P, 32, DK], F32, name="prod", tag="prod")
+            st["prod%d" % hf] = prod
+            if hf % 4 == 3:
+                nc.gpsimd.tensor_tensor(
+                    out=prod[:],
+                    in0=xv[:, half * 2048:(half + 1) * 2048].rearrange("p (d c) -> p d c", c=DK),
+                    in1=qd[:, v, :].unsqueeze(1).to_broadcast([P, 32, DK]),
+                    op=ALU.mult,
+                )
             else:
-                for tb in range(4):
-                    blk = UNITS[2 * g + tb // 2][tb % 2]
-                    nc.sync.dma_start(out=raw[:, tb, :], in_=w[P * blk:P * blk + P, :])
-            pieces = ((0, 1024), (1024, 512))
-            grps = []
-            for w0, wn in pieces:
-                grp = grpp.tile([P, 4096], BF16, tag="grp", align_bytes=64)
-                nc.scalar.copy(
-                    out=grp[:, 0:4 * wn].rearrange("p (c i t) -> p c t i", i=4, t=4),
-                    in_=raw[:, :, w0:w0 + wn].rearrange("p t (c i) -> p c t i", i=4),
+                nc.vector.scalar_tensor_tensor(
+                    out=prod[:],
+                    in0=xv[:, half * 2048:(half + 1) * 2048].rearrange("p (d c) -> p d c", c=DK),
+                    scalar=dec_f[:, V_HEADS[v]:V_HEADS[v] + 1],
+                    in1=qps[:, v, :].unsqueeze(1).to_broadcast([P, 32, DK]),
+                    op0=ALU.mult,
+                    op1=ALU.mult,
                 )
-                grps.append(grp)
-            for (w0, wn), grp in zip(pieces, grps):
-                nc.vector.quantize_mx(
-                    out=wc[:, g, w0:w0 + wn].bitcast(FP8X4), scales=ws[:, g, w0:w0 + wn], in_=grp[:, 0:4 * wn]
+
+        def r_cols(hf):
+            h = V_HEADS[hf // 2]
+            return h // 2, (h % 2) * DH + (hf % 2) * 32
+
+        def scalar_sums(hf, q):
+            prod = st["prod%d" % hf]
+            blk, c0 = r_cols(hf)
+            for dd in range(8 * q, 8 * q + 8):
+                nc.scalar.activation(
+                    out=prod[:, dd, :], in_=prod[:, dd, :], func=ACT.Copy, accum_out=r[:, blk, c0 + dd:c0 + dd + 1]
                 )
+
+        def vector_sums(hf):
+            blk, c0 = r_cols(hf)
+            nc.vector.tensor_reduce(out=r[:, blk, c0:c0 + 32], in_=st["prod%d" % hf][:], axis=AX.X, op=ALU.add)
+
+        def regroup(c, j):
+            grp = grpp.tile([P, 2048], BF16, name="grp", tag="grp", align_bytes=64)
+            st["grp%d" % (3 * c + j)] = grp
+            nc.gpsimd.tensor_scalar(
+                out=grp[:].rearrange("p (w t) -> p w t", t=4),
+                in0=st["raw%d" % c][:, :, 512 * j:512 * j + 512].rearrange("p t w -> p w t"),
+                scalar1=1.0, scalar2=0.0, op0=ALU.mult, op1=ALU.add,
+            )
+
+        def quantise(c, j):
+            g = c % 3
+            nc.vector.quantize_mx(
+                out=wc[:, g, 512 * j:512 * j + 512].bitcast(FP8X4), scales=ws[:, g, 512 * j:512 * j + 512],
+                in_=st["grp%d" % (3 * c + j)][:],
+            )
 
         def v_passes():
             for nb in range(3):
-                acc = psc.tile([P, 512], F32, tag="c")
+                acc = psc.tile([P, 512], F32, name="acc%d" % nb, tag="c") if nb < 2 else psb.tile([P, 512], F32, name="acc2", tag="b")
+                st["acc%d" % nb] = acc
                 for g in range(3):
                     nc.tensor.matmul_mx(
                         out=acc[:],
@@ -163,168 +266,155 @@ def tile_multiscaleretention_pb_kernel(tc, x, qr, kr, decay, prev_kv, Wv, Wo, ou
                         start=(g == 0),
                         stop=(g == 2),
                     )
+
+        def v_scale():
+            for nb in range(3):
                 nc.vector.tensor_tensor(
                     out=sv[:, 4 * nb:4 * nb + 4, :].rearrange("p k (h d) -> p (k h) d", d=DH),
-                    in0=acc[:].rearrange("p (h d) -> p h d", d=DH),
+                    in0=st["acc%d" % nb][:].rearrange("p (h d) -> p h d", d=DH),
                     in1=s_t[:, 8 * nb:8 * nb + 8].unsqueeze(2).to_broadcast([P, 8, DH]),
                     op=ALU.mult,
                 )
 
-        def vector_pair(vi):
-            h0 = V_PAIRS[vi]
-            xv = xvp.tile([P, 2 * HEAD], BF16, tag="xv")
-            nc.sync.dma_start(out=xv[:], in_=pb[:, h0 * HEAD:(h0 + 2) * HEAD])
-            if vi % 2 == 1:
-                for hf in range(4):
-                    prod = prp.tile([P, 32, DK], F32, tag="prod")
-                    nc.vector.tensor_tensor(
-                        out=prod[:],
-                        in0=xv[:, hf * 2048:(hf + 1) * 2048].rearrange("p (d c) -> p d c", c=DK),
-                        in1=qd[:, 2 * vi + hf // 2, :].unsqueeze(1).to_broadcast([P, 32, DK]),
-                        op=ALU.mult,
-                    )
-                    if hf == 3:
-                        nc.vector.tensor_reduce(out=r[:, h0 // 2, 96:128], in_=prod[:], axis=AX.X, op=ALU.add)
-                    else:
-                        for dd in range(32):
-                            nc.scalar.activation(
-                                out=prod[:, dd, :], in_=prod[:, dd, :], func=ACT.Copy,
-                                accum_out=r[:, h0 // 2, hf * 32 + dd:hf * 32 + dd + 1],
-                            )
-                return
-            racc = psr.tile([P, P], F32, tag="r")
-            for ch in range(DK // CCH):
-                c0 = ch * CCH
-                pc = prp.tile([P, CCH, 2, DH], F32, tag="prod")
-                for a in range(2):
-                    nc.vector.tensor_tensor(
-                        out=pc[:, :, a, :].rearrange("p (k i) d -> p k d i", i=4),
-                        in0=xv[:, a * HEAD:(a + 1) * HEAD].rearrange("p (d c) -> p d c", c=DK)[:, :, c0:c0 + CCH]
-                        .rearrange("p d (k i) -> p k d i", i=4),
-                        in1=qd[:, 2 * vi + a, c0:c0 + CCH].rearrange("p (k i) -> p k i", i=4).unsqueeze(2)
-                        .to_broadcast([P, CCH // 4, DH, 4]),
-                        op=ALU.mult,
-                    )
-                for c in range(CCH):
-                    nc.tensor.matmul(
-                        out=racc[:], lhsT=pc[:, c, :, :].rearrange("p a d -> p (a d)"), rhs=ident_f[:],
-                        is_transpose=True, start=(c0 + c == 0), stop=(c0 + c == DK - 1),
-                    )
-            rt = small.tile([P, P], F32, tag="rt")
-            nc.scalar.copy(out=rt[:], in_=racc[:])
-            rbk = psc.tile([P, P], F32, tag="c")
-            nc.tensor.transpose(rbk[:], rt[:], ident_f[:])
-            nc.scalar.copy(out=r[:, h0 // 2, :], in_=rbk[:])
-
-        def tensor_tile(i):
-            t, half = i // 2, i % 2
-            xp = xpp.tile([P, 2 * HEAD], BF16, tag="xp")
-            nc.sync.dma_start(out=xp[:], in_=pp[P * half:P * half + P, 2 * t * HEAD:(2 * t + 2) * HEAD])
-            z = zp.tile([P, 64 * P], BF16, tag="z")
-            zw = z[:].bitcast(F32).rearrange("p (b s) -> p b s", s=64)
-            for sg in range(16):
-                tp = psa.tile([P, 4, P], BF16, tag="a")
-                for k in range(4):
-                    s = 4 * sg + k
-                    nc.tensor.transpose(tp[:, k, :], xp[:, s * P:(s + 1) * P], ident_b[:])
-                nc.scalar.copy(
-                    out=zw[:, :, 4 * sg:4 * sg + 4].rearrange("p (v i) k -> p v k i", i=2),
-                    in_=tp[:].bitcast(F32).rearrange("p k (v i) -> p v k i", i=2),
-                )
-            mm = psb.tile([P, 64, 8], F32, tag="b")
-            for bi in range(64):
-                nc.tensor.matmul(
-                    out=mm[:, bi, :], lhsT=z[:, bi * P:(bi + 1) * P], rhs=rqv[:, t, 64 * half + bi, :],
-                    start=True, stop=True,
-                )
-            if half == 0:
-                state["ct"] = ctp.tile([P, 8, P], F32, name="ct", tag="ct")
-            ct = state["ct"]
-            nc.scalar.copy(out=ct[:, :, 64 * half:64 * half + 64], in_=mm[:].rearrange("p b n -> p n b"))
-            if half == 1:
-                for a in range(2):
-                    rb = psc.tile([P, 4, P], F32, tag="c")
-                    for n in range(4):
-                        nc.tensor.transpose(rb[:, n, :], ct[:, 4 * a + n, :], ident_f[:])
-                    for hh in range(2):
-                        h = hh * 12 + 2 * t + a
-                        m0 = 64 * a + hh
-                        nc.vector.tensor_scalar_mul(
-                            out=r[:, h // 2, (h % 2) * DH:(h % 2) * DH + DH].rearrange("p (j e) -> p j e", e=2),
-                            in0=rb[:, 2 * hh:2 * hh + 2, m0:m0 + 63:2].rearrange("p e j -> p j e"),
-                            scalar1=dec_f[:, h:h + 1],
-                        )
-
-        def norm(ui):
+        def norm_a(ui):
             b0, b1 = UNITS[ui]
-            step = b1 - b0
-            kg = ui // 2
-            if ui % 2 == 0:
-                state["nb%d" % kg] = keep.tile([P, 4, P], BF16, name="nbf%d" % kg)
-            n_bf = state["nb%d" % kg]
-            rv = r[:, b0:b1 + 1:step, :]
-            nc.vector.tensor_tensor(out=rv, in0=rv, in1=sv[:, b0:b1 + 1:step, :], op=ALU.add)
+            rv = r[:, b0:b1 + 1:b1 - b0, :]
+            nc.vector.tensor_tensor(out=rv, in0=rv, in1=sv[:, b0:b1 + 1:b1 - b0, :], op=ALU.add)
             sq = small.tile([P, 2, P], F32, tag="sq")
             nc.vector.tensor_tensor(out=sq[:], in0=rv, in1=rv, op=ALU.mult)
-            ss = small.tile([P, 4], F32, tag="ss")
+            ss = small.tile([P, 4], F32, name="ss", tag="ss")
+            st["ss%d" % ui] = ss
             nc.vector.tensor_reduce(out=ss[:], in_=sq[:].rearrange("p k (h d) -> p (k h) d", d=DH), axis=AX.X, op=ALU.add)
-            rms = small.tile([P, 4], F32, tag="rms")
-            nc.scalar.activation(out=rms[:], in_=ss[:], func=ACT.Sqrt, bias=eps_t[:], scale=1.0 / DH)
+
+        def norm_s(ui):
+            rms = small.tile([P, 4], F32, name="rms", tag="rms")
+            st["rms%d" % ui] = rms
+            nc.scalar.activation(out=rms[:], in_=st["ss%d" % ui][:], func=ACT.Sqrt, bias=eps_t[:], scale=1.0 / DH)
+
+        def norm_b(ui):
+            b0, b1 = UNITS[ui]
+            kg = ui // 2
+            if "nb%d" % kg not in st:
+                st["nb%d" % kg] = keep.tile([P, 4, P], BF16, name="nbf%d" % kg)
             rstd = small.tile([P, 4], F32, tag="rstd")
-            nc.vector.reciprocal(out=rstd[:], in_=rms[:])
+            nc.vector.reciprocal(out=rstd[:], in_=st["rms%d" % ui][:])
             for k in range(2):
                 nc.vector.tensor_tensor(
-                    out=n_bf[:, 2 * (ui % 2) + k, :].rearrange("p (h d) -> p h d", d=DH),
-                    in0=r[:, b0 + k * step, :].rearrange("p (h d) -> p h d", d=DH),
+                    out=st["nb%d" % kg][:, 2 * (ui % 2) + k, :].rearrange("p (h d) -> p h d", d=DH),
+                    in0=r[:, (b0, b1)[k], :].rearrange("p (h d) -> p h d", d=DH),
                     in1=rstd[:, 2 * k:2 * k + 2].unsqueeze(2).to_broadcast([P, 2, DH]),
                     op=ALU.mult,
                 )
 
-        def out_pass(kg):
-            n_bf = state["nb%d" % kg]
-            nt = psc.tile([P, 4, P], BF16, tag="c")
+        def n_transposes(kg):
+            nt = psc.tile([P, 4, P], BF16, name="nt", tag="c")
+            st["nt"] = nt
             for t in range(4):
-                nc.tensor.transpose(nt[:, t, :], n_bf[:, t, :], ident_b[:])
-            ng = small.tile([P, 512], BF16, tag="ng", align_bytes=64)
-            nc.vector.tensor_copy(out=ng[:].rearrange("p (b t) -> p b t", t=4), in_=nt[:].rearrange("p t b -> p b t"))
-            nc.vector.quantize_mx(out=ncd[:, kg, :].bitcast(FP8X4), scales=nsc[:, kg, :], in_=ng[:])
+                nc.tensor.transpose(nt[:, t, :], st["nb%d" % kg][:, t, :], ident_b[:])
 
-        def final_passes():
+        def n_copy(kg):
+            ng = small.tile([P, 512], BF16, name="ng", tag="ng", align_bytes=64)
+            st["ng"] = ng
+            nc.scalar.copy(out=ng[:].rearrange("p (b t) -> p b t", t=4), in_=st["nt"][:].rearrange("p t b -> p b t"))
+
+        def n_quantise(kg):
+            nc.vector.quantize_mx(out=ncd[:, kg, :].bitcast(FP8X4), scales=nsc[:, kg, :], in_=st["ng"][:])
+
+        def out_passes(kg):
             for nb in range(3):
-                oa = psa.tile([P, 512], F32, tag="a")
-                for kg in range(3):
-                    nc.tensor.matmul_mx(
-                        out=oa[:],
-                        lhsT=ncd[:, kg, :].bitcast(FP8X4),
-                        lhsT_scale=nsc[:, kg, :],
-                        rhs=wc[:, kg, 512 * nb:512 * nb + 512].bitcast(FP8X4),
-                        rhs_scale=ws[:, kg, 512 * nb:512 * nb + 512],
-                        start=(kg == 0),
-                        stop=(kg == 2),
-                    )
-                ob = prp.tile([P, 512], F32, tag="prod")
-                if nb == 1:
-                    nc.scalar.copy(out=ob[:], in_=oa[:])
-                else:
-                    nc.vector.tensor_copy(out=ob[:], in_=oa[:])
-                nc.sync.dma_start(out=of[:, 512 * nb:512 * nb + 512], in_=ob[:])
+                if kg == 0:
+                    st["oa%d" % nb] = psa.tile([P, 512], F32, name="oa%d" % nb, tag="a")
+                nc.tensor.matmul_mx(
+                    out=st["oa%d" % nb][:],
+                    lhsT=ncd[:, kg, :].bitcast(FP8X4),
+                    lhsT_scale=nsc[:, kg, :],
+                    rhs=wc[:, kg, 512 * nb:512 * nb + 512].bitcast(FP8X4),
+                    rhs_scale=ws[:, kg, 512 * nb:512 * nb + 512],
+                    start=(kg == 0),
+                    stop=(kg == 2),
+                )
 
-        for u in SEQ:
-            kind, idx = u[0], u[1:]
-            if kind == "p":
-                tensor_tile(int(idx))
-            elif u == "vv":
+        for tick in range(N_TICKS):
+            rnd, k = tick // 8, tick % 8
+            if tick in (1, 3, 5):
+                rq_transposes(tick // 2)
+            if tick in (2, 4, 6):
+                rq_copy(tick // 2 - 1)
+            if rnd < 6:
+                transposes(rnd, 2 * k)
+                transposes(rnd, 2 * k + 1)
+            if 1 <= rnd <= 6:
+                if k < 4:
+                    readout_matmuls(rnd - 1, k)
+                if k == 4:
+                    collect(rnd - 1)
+                if k == 5 and rnd % 2 == 0:
+                    back_transposes()
+                if k == 6 and rnd % 2 == 0:
+                    back_copies(rnd // 2 - 1)
+            for hf in range(24):
+                if tick == (2 * hf - 2 if hf % 4 == 3 else 2 * hf):
+                    product(hf)
+            for hf in range(24):
+                if hf % 2 == 0 and 0 <= tick - 2 * hf - 3 < 4:
+                    scalar_sums(hf, tick - 2 * hf - 3)
+                if hf % 2 == 1 and tick == 2 * hf + 3:
+                    vector_sums(hf)
+            for c in range(6):
+                for j in range(3):
+                    if tick == 8 * c + PIECE_TICK[j]:
+                        regroup(c, j)
+                    if tick == 8 * c + PIECE_TICK[j] + 4:
+                        quantise(c, j)
+            if tick == 12:
+                xw = x_sb[:].bitcast(F32)
+                for g in range(3):
+                    xt = psc.tile([P, 2, P], F32, name="xt%d" % g, tag="c") if g < 2 else psb.tile([P, 2, P], F32, name="xt2", tag="b")
+                    st["xt%d" % g] = xt
+                    for u in range(2):
+                        nc.tensor.transpose(xt[:, u, :], xw[:, 256 * g + 128 * u:256 * g + 128 * u + 128], ident_f[:])
+            if tick == 14:
+                nc.vector.tensor_reduce(out=s_t[:], in_=qk[:], axis=AX.X, op=ALU.add)
+                xg = keep.tile([P, 3 * 512], BF16, align_bytes=64)
+                for g in range(3):
+                    nc.vector.tensor_copy(
+                        out=xg[:, 512 * g:512 * g + 512].bitcast(F32).rearrange("p (b u) -> p b u", u=2),
+                        in_=st["xt%d" % g][:].rearrange("p u b -> p b u"),
+                    )
+                for g in range(3):
+                    nc.vector.quantize_mx(out=xc[:, g, :].bitcast(FP8X4), scales=xs[:, g, :], in_=xg[:, 512 * g:512 * g + 512])
+            if tick == 28:
                 v_passes()
-            elif kind == "v":
-                vector_pair(int(idx))
-            elif kind == "w":
-                g = int(idx)
-                if g < 3:
-                    weight_chunk(Wv, g, True)
-                else:
-                    weight_chunk(Wo, g - 3, False)
-            elif kind == "n":
-                norm(int(idx))
-            elif kind == "o":
-                out_pass(int(idx))
-        final_passes()
+            if tick == 31:
+                v_scale()
+            if k == 7 and rnd + 2 < 6:
+                load_xp(rnd + 2)
+            if k == 0 and rnd + 1 < 6:
+                load_raw(rnd + 1)
+            if tick % 4 == 0 and 3 <= tick // 4 + 2 < 12:
+                load_xv(tick // 4 + 2)
+            for ui in range(6):
+                if tick == UNIT_TICK[ui]:
+                    norm_a(ui)
+                if tick == UNIT_TICK[ui] + 1:
+                    norm_s(ui)
+                if tick == UNIT_TICK[ui] + 2:
+                    norm_b(ui)
+            for kg in range(3):
+                t0 = max(UNIT_TICK[2 * kg], UNIT_TICK[2 * kg + 1])
+                if tick == t0 + 3:
+                    n_transposes(kg)
+                if tick == t0 + 4:
+                    n_copy(kg)
+                if tick == t0 + 5:
+                    n_quantise(kg)
+                if tick == max(t0 + 6, 49 + kg):
+                    out_passes(kg)
+
+        for nb in range(3):
+            ob = prp.tile([P, 512], F32, tag="prod")
+            if nb == 1:
+                nc.vector.tensor_copy(out=ob[:], in_=st["oa%d" % nb][:])
+            else:
+                nc.scalar.copy(out=ob[:], in_=st["oa%d" % nb][:])
+            nc.sync.dma_start(out=of[:, 512 * nb:512 * nb + 512], in_=ob[:])

@@ -13,83 +13,101 @@ ACT = mybir.ActivationFunctionType
 AX = mybir.AxisListType
 
 P = 128
-B, H, DK, DH, E, V = 128, 24, 64, 64, 1536, 1536
+H, DK, DH, E, V = 24, 64, 64, 1536, 1536
 HEAD = DH * DK
 EPS = 1e-6
-FLOPS = 2 * 2 * B * E * V + 4 * B * H * DH * DK
+FLOPS = 2 * 2 * P * E * V + 4 * P * H * DH * DK
 
+N_TILES = 6
 V_HEADS = (6, 7, 8, 9, 10, 11, 18, 19, 20, 21, 22, 23)
+N_HALVES = 2 * len(V_HEADS)
 UNITS = ((0, 6), (3, 4), (1, 7), (5, 9), (2, 8), (10, 11))
-UNIT_TICK = (32, 32, 39, 37, 55, 53)
+TICKS = 8
 PIECE_TICK = (2, 4, 7)
+QUANTISE_LAG = 4
+SUM_LAG = 3
+V_TICK = 28
+FIRST_NORM_TICK = V_TICK + 4
 N_TICKS = 62
+
+
+def unit_tick(ui):
+    if ui % 2 == 0:
+        ready = TICKS * (ui + 2) + 7
+    else:
+        ready = 2 * (4 * ui + 3) + SUM_LAG + 4
+    return max(FIRST_NORM_TICK, ready)
+
+
+def pass_tick(g):
+    return max(unit_tick(2 * g), unit_tick(2 * g + 1)) + 3
 
 
 def tile_multiscaleretention_pb_kernel(tc, x, qr, kr, decay, prev_kv, Wv, Wo, out):
     nc = tc.nc
-    xf = x.rearrange("b t e -> b (t e)")
-    qf = qr.rearrange("b h t c -> b (h t c)")
-    kf = kr.rearrange("b h t c -> b (h t c)")
-    pb = prev_kv.rearrange("b h d c -> b (h d c)")
-    pp = prev_kv.rearrange("b (hh hp) d c -> (b hh) (hp d c)", hh=2)
-    of = out.rearrange("b t e -> b (t e)")
+    x_rows = x.rearrange("b t e -> b (t e)")
+    q_rows = qr.rearrange("b h t c -> b (h t c)")
+    k_rows = kr.rearrange("b h t c -> b (h t c)")
+    state_by_seq = prev_kv.rearrange("b h d c -> b (h d c)")
+    state_by_half = prev_kv.rearrange("b (hh hp) d c -> (b hh) (hp d c)", hh=2)
+    out_rows = out.rearrange("b t e -> b (t e)")
 
     with ExitStack() as ctx:
         keep = ctx.enter_context(tc.tile_pool(name="keep", bufs=1))
         small = ctx.enter_context(tc.tile_pool(name="small", bufs=2))
-        rawp = ctx.enter_context(tc.tile_pool(name="rawp", bufs=2))
-        grpp = ctx.enter_context(tc.tile_pool(name="grpp", bufs=2))
-        xpp = ctx.enter_context(tc.tile_pool(name="xpp", bufs=2))
-        zp = ctx.enter_context(tc.tile_pool(name="zp", bufs=2))
-        xvp = ctx.enter_context(tc.tile_pool(name="xvp", bufs=3))
-        prp = ctx.enter_context(tc.tile_pool(name="prp", bufs=4))
-        ctp = ctx.enter_context(tc.tile_pool(name="ctp", bufs=1))
-        psa = ctx.enter_context(tc.psum_pool(name="psa", bufs=4))
-        psb = ctx.enter_context(tc.psum_pool(name="psb", bufs=1))
-        psc = ctx.enter_context(tc.psum_pool(name="psc", bufs=2))
-        psq = ctx.enter_context(tc.psum_pool(name="psq", bufs=1))
+        raw_pool = ctx.enter_context(tc.tile_pool(name="raw_pool", bufs=2))
+        grp_pool = ctx.enter_context(tc.tile_pool(name="grp_pool", bufs=2))
+        xp_pool = ctx.enter_context(tc.tile_pool(name="xp_pool", bufs=2))
+        z_pool = ctx.enter_context(tc.tile_pool(name="z_pool", bufs=2))
+        xv_pool = ctx.enter_context(tc.tile_pool(name="xv_pool", bufs=3))
+        prod_pool = ctx.enter_context(tc.tile_pool(name="prod_pool", bufs=4))
+        ct_pool = ctx.enter_context(tc.tile_pool(name="ct_pool", bufs=1))
+        ps_rot = ctx.enter_context(tc.psum_pool(name="ps_rot", bufs=4))
+        ps_mm = ctx.enter_context(tc.psum_pool(name="ps_mm", bufs=1))
+        ps_misc = ctx.enter_context(tc.psum_pool(name="ps_misc", bufs=2))
+        ps_q = ctx.enter_context(tc.psum_pool(name="ps_q", bufs=1))
         ctx.enter_context(tc.manual_schedule())
 
-        st = {}
+        live = {}
 
-        def load_xp(i):
+        def load_tile(i):
             t, half = i // 2, i % 2
-            st["xp%d" % i] = xpp.tile([P, 2 * HEAD], BF16, name="xp", tag="xp")
-            nc.sync.dma_start(out=st["xp%d" % i][:], in_=pp[P * half:P * half + P, 2 * t * HEAD:(2 * t + 2) * HEAD])
+            live["xp", i] = xp_pool.tile([P, 2 * HEAD], BF16, name="xp", tag="xp")
+            nc.sync.dma_start(
+                out=live["xp", i][:], in_=state_by_half[P * half:P * half + P, 2 * t * HEAD:(2 * t + 2) * HEAD]
+            )
 
-        def load_xv(v):
+        def load_head(v):
             h = V_HEADS[v]
-            st["xv%d" % v] = xvp.tile([P, HEAD], BF16, name="xv", tag="xv")
-            nc.sync.dma_start(out=st["xv%d" % v][:], in_=pb[:, h * HEAD:(h + 1) * HEAD])
+            live["xv", v] = xv_pool.tile([P, HEAD], BF16, name="xv", tag="xv")
+            nc.sync.dma_start(out=live["xv", v][:], in_=state_by_seq[:, h * HEAD:(h + 1) * HEAD])
 
-        def load_raw(c):
-            raw = rawp.tile([P, 4, V], BF16, name="raw", tag="raw")
-            st["raw%d" % c] = raw
+        def load_weights(c):
+            raw = raw_pool.tile([P, 4, V], BF16, name="raw", tag="raw")
+            live["raw", c] = raw
             if c < 3:
                 for u in range(2):
-                    nc.sync.dma_start(
-                        out=raw[:, 2 * u:2 * u + 2, :],
-                        in_=Wv[512 * c + 256 * u:512 * c + 256 * u + 256, :].rearrange("(q e) c -> q e c", e=2),
-                    )
+                    rows = Wv[512 * c + 256 * u:512 * c + 256 * u + 256, :]
+                    nc.sync.dma_start(out=raw[:, 2 * u:2 * u + 2, :], in_=rows.rearrange("(q e) c -> q e c", e=2))
             else:
-                for tb in range(4):
-                    blk = UNITS[2 * (c - 3) + tb // 2][tb % 2]
-                    nc.sync.dma_start(out=raw[:, tb, :], in_=Wo[P * blk:P * blk + P, :])
+                for t in range(4):
+                    block = UNITS[2 * (c - 3) + t // 2][t % 2]
+                    nc.sync.dma_start(out=raw[:, t, :], in_=Wo[P * block:P * block + P, :])
 
         q_sb = keep.tile([P, E], BF16)
-        nc.sync.dma_start(out=q_sb[:], in_=qf)
+        nc.sync.dma_start(out=q_sb[:], in_=q_rows)
         dec_b = keep.tile([P, H], BF16)
         nc.sync.dma_start(out=dec_b[:], in_=decay.partition_broadcast(P))
-        load_xp(0)
-        load_xv(0)
+        load_tile(0)
+        load_head(0)
         k_sb = keep.tile([P, E], BF16)
-        nc.sync.dma_start(out=k_sb[:], in_=kf)
+        nc.sync.dma_start(out=k_sb[:], in_=k_rows)
         x_sb = keep.tile([P, E], BF16)
-        nc.sync.dma_start(out=x_sb[:], in_=xf)
-        load_xv(1)
-        load_raw(0)
-        load_xp(1)
-        load_xv(2)
+        nc.sync.dma_start(out=x_sb[:], in_=x_rows)
+        load_head(1)
+        load_weights(0)
+        load_tile(1)
+        load_head(2)
 
         ident_b = keep.tile([P, P], BF16)
         make_identity(nc, ident_b[:])
@@ -97,95 +115,84 @@ def tile_multiscaleretention_pb_kernel(tc, x, qr, kr, decay, prev_kv, Wv, Wo, ou
         make_identity(nc, ident_f[:])
         eps_t = keep.tile([P, 1], F32)
         nc.vector.memset(eps_t[:], EPS)
-        dum = keep.tile([P, 1], F32)
-        nc.scalar.activation(out=dum[:], in_=eps_t[:], func=ACT.Sqrt)
+        warm = keep.tile([P, 1], F32)
+        nc.scalar.activation(out=warm[:], in_=eps_t[:], func=ACT.Sqrt)
 
-        qz = zp.tile([P, 6 * 2 * 2 * P], BF16, tag="z")
-        nc.vector.memset(qz[:], 0.0)
-        qzv = qz[:].rearrange("p (hp hh e k) -> p hp hh e k", hh=2, e=2, k=P)
-        qpe = q_sb[:].rearrange("p (hh hp c) -> p hp hh c", hh=2, c=DK)[:, 0:6, :, :]
-        nc.vector.tensor_copy(out=qzv[:, :, :, 0, 0:DK], in_=qpe)
-        nc.vector.tensor_copy(out=qzv[:, :, :, 1, DK:P], in_=qpe)
+        q_pad = z_pool.tile([P, 6 * 2 * 2 * P], BF16, tag="z")
+        nc.vector.memset(q_pad[:], 0.0)
+        q_pad_v = q_pad[:].rearrange("p (hp hh e k) -> p hp hh e k", hh=2, e=2, k=P)
+        q_tensor = q_sb[:].rearrange("p (hh hp c) -> p hp hh c", hh=2, c=DK)[:, 0:6, :, :]
+        nc.vector.tensor_copy(out=q_pad_v[:, :, :, 0, 0:DK], in_=q_tensor)
+        nc.vector.tensor_copy(out=q_pad_v[:, :, :, 1, DK:P], in_=q_tensor)
         dec_f = keep.tile([P, H], F32)
         nc.vector.tensor_copy(out=dec_f[:], in_=dec_b[:])
-        qd = keep.tile([P, 12, DK], F32)
-        nc.gpsimd.tensor_tensor(
-            out=qd[:].rearrange("p (hh hp) c -> p hh hp c", hh=2),
-            in0=q_sb[:].rearrange("p (hh hp c) -> p hh hp c", hh=2, c=DK)[:, :, 6:12, :],
-            in1=dec_f[:].rearrange("p (hh hp) -> p hh hp", hh=2)[:, :, 6:12].unsqueeze(3).to_broadcast([P, 2, 6, DK]),
-            op=ALU.mult,
-        )
-        qtp = psa.tile([P, 6, P], BF16, tag="a")
+        q_up = ps_rot.tile([P, 6, P], BF16, tag="rot")
         for j in range(6):
-            nc.tensor.transpose(qtp[:, j, :], q_sb[:, V_HEADS[2 * j] * DK:V_HEADS[2 * j] * DK + P], ident_b[:])
+            h = V_HEADS[2 * j]
+            nc.tensor.transpose(q_up[:, j, :], q_sb[:, h * DK:h * DK + P], ident_b[:])
         q_t = keep.tile([P, 6, P], BF16)
-        nc.scalar.copy(out=q_t[:], in_=qtp[:])
-        qps = psq.tile([P, 12, DK], BF16, tag="q")
+        nc.scalar.copy(out=q_t[:], in_=q_up[:])
+        q_ps = ps_q.tile([P, len(V_HEADS), DK], BF16, tag="q")
         for j in range(6):
-            nc.tensor.transpose(qps[:, 2 * j:2 * j + 2, :].rearrange("p a c -> p (a c)"), q_t[:, j, :], ident_b[:])
+            nc.tensor.transpose(q_ps[:, 2 * j:2 * j + 2, :].rearrange("p a c -> p (a c)"), q_t[:, j, :], ident_b[:])
         qk = keep.tile([P, H, DK], F32)
         nc.gpsimd.tensor_tensor(out=qk[:].rearrange("p h c -> p (h c)"), in0=q_sb[:], in1=k_sb[:], op=ALU.mult)
 
-        rq = keep.tile([P, 3 * P * 8], BF16)
-        rqv = rq[:].rearrange("p (t b n) -> p t b n", b=P, n=8)
-        s_t = keep.tile([P, H], F32)
-        xc = keep.tile([P, 3, P], U32, align_bytes=64)
-        xs = keep.tile([P, 3, P], U8, align_bytes=64)
-        wc = keep.tile([P, 3, V], U32, align_bytes=64)
-        ws = keep.tile([P, 3, V], U8, align_bytes=64)
+        q_mov = keep.tile([P, 3, P, 8], BF16)
+        qk_sum = keep.tile([P, H], F32)
+        x_codes = keep.tile([P, 3, P], U32, align_bytes=64)
+        x_scales = keep.tile([P, 3, P], U8, align_bytes=64)
+        w_codes = keep.tile([P, 3, V], U32, align_bytes=64)
+        w_scales = keep.tile([P, 3, V], U8, align_bytes=64)
         sv = keep.tile([P, 12, P], F32)
         r = keep.tile([P, 12, P], F32)
-        ncd = keep.tile([P, 3, P], U32, align_bytes=64)
-        nsc = keep.tile([P, 3, P], U8, align_bytes=64)
+        n_codes = keep.tile([P, 3, P], U32, align_bytes=64)
+        n_scales = keep.tile([P, 3, P], U8, align_bytes=64)
 
-        def rq_transposes(t):
-            pq = psa.tile([P, 8, P], BF16, name="pq", tag="a")
-            st["pq"] = pq
+        def q_transposes(t):
+            live["qm"] = ps_rot.tile([P, 8, P], BF16, name="qm", tag="rot")
             for a in range(2):
                 for hh in range(2):
                     for e in range(2):
-                        nc.tensor.transpose(pq[:, a * 4 + hh * 2 + e, :], qzv[:, 2 * t + a, hh, e, :], ident_b[:])
+                        nc.tensor.transpose(live["qm"][:, a * 4 + hh * 2 + e, :], q_pad_v[:, 2 * t + a, hh, e, :], ident_b[:])
 
-        def rq_copy(t):
-            nc.scalar.copy(out=rqv[:, t], in_=st["pq"][:].rearrange("p n b -> p b n"))
+        def q_copy(t):
+            nc.scalar.copy(out=q_mov[:, t], in_=live["qm"][:].rearrange("p n b -> p b n"))
 
         def transposes(i, g):
-            xp = st["xp%d" % i]
             if g == 0:
-                st["z%d" % i] = zp.tile([P, 64 * P], BF16, name="z", tag="z")
-            zw = st["z%d" % i][:].bitcast(F32).rearrange("p (b s) -> p b s", s=64)
-            tp = psa.tile([P, 4, P], BF16, tag="a")
+                live["z", i] = z_pool.tile([P, 64 * P], BF16, name="z", tag="z")
+            z_words = live["z", i][:].bitcast(F32).rearrange("p (b s) -> p b s", s=64)
+            up = ps_rot.tile([P, 4, P], BF16, tag="rot")
             for k in range(4):
                 s = 4 * g + k
-                nc.tensor.transpose(tp[:, k, :], xp[:, s * P:(s + 1) * P], ident_b[:])
+                nc.tensor.transpose(up[:, k, :], live["xp", i][:, s * P:(s + 1) * P], ident_b[:])
             nc.scalar.copy(
-                out=zw[:, :, 4 * g:4 * g + 4].rearrange("p (v i) k -> p v k i", i=2),
-                in_=tp[:].bitcast(F32).rearrange("p k (v i) -> p v k i", i=2),
+                out=z_words[:, :, 4 * g:4 * g + 4].rearrange("p (v i) k -> p v k i", i=2),
+                in_=up[:].bitcast(F32).rearrange("p k (v i) -> p v k i", i=2),
             )
 
-        def readout_matmuls(i, q):
+        def readout_matmuls(i, quarter):
             t, half = i // 2, i % 2
-            if q == 0:
-                st["mm"] = psb.tile([P, 64, 8], F32, name="mm", tag="b")
-            z = st["z%d" % i]
-            for bi in range(16 * q, 16 * q + 16):
+            if quarter == 0:
+                live["mm"] = ps_mm.tile([P, 64, 8], F32, name="mm", tag="mm")
+            for b in range(16 * quarter, 16 * quarter + 16):
                 nc.tensor.matmul(
-                    out=st["mm"][:, bi, :], lhsT=z[:, bi * P:(bi + 1) * P], rhs=rqv[:, t, 64 * half + bi, :],
+                    out=live["mm"][:, b, :], lhsT=live["z", i][:, b * P:(b + 1) * P], rhs=q_mov[:, t, 64 * half + b, :],
                     start=True, stop=True,
                 )
 
         def collect(i):
             half = i % 2
             if half == 0:
-                st["ct"] = ctp.tile([P, 8, P], F32, name="ct", tag="ct")
-            nc.scalar.copy(out=st["ct"][:, :, 64 * half:64 * half + 64], in_=st["mm"][:].rearrange("p b n -> p n b"))
+                live["ct"] = ct_pool.tile([P, 8, P], F32, name="ct", tag="ct")
+            nc.scalar.copy(out=live["ct"][:, :, 64 * half:64 * half + 64], in_=live["mm"][:].rearrange("p b n -> p n b"))
 
         def back_transposes():
             for a in range(2):
-                rb = psc.tile([P, 4, P], F32, name="rb", tag="c")
-                st["rb%d" % a] = rb
+                live["rb", a] = ps_misc.tile([P, 4, P], F32, name="rb", tag="misc")
                 for n in range(4):
-                    nc.tensor.transpose(rb[:, n, :], st["ct"][:, 4 * a + n, :], ident_f[:])
+                    nc.tensor.transpose(live["rb", a][:, n, :], live["ct"][:, 4 * a + n, :], ident_f[:])
 
         def back_copies(t):
             for a in range(2):
@@ -194,156 +201,149 @@ def tile_multiscaleretention_pb_kernel(tc, x, qr, kr, decay, prev_kv, Wv, Wo, ou
                     m0 = 64 * a + hh
                     nc.scalar.activation(
                         out=r[:, h // 2, (h % 2) * DH:(h % 2) * DH + DH].rearrange("p (j e) -> p j e", e=2),
-                        in_=st["rb%d" % a][:, 2 * hh:2 * hh + 2, m0:m0 + 63:2].rearrange("p e j -> p j e"),
+                        in_=live["rb", a][:, 2 * hh:2 * hh + 2, m0:m0 + 63:2].rearrange("p e j -> p j e"),
                         func=ACT.Copy, scale=dec_f[:, h:h + 1],
                     )
 
         def product(hf):
             v, half = hf // 2, hf % 2
-            xv = st["xv%d" % v]
-            prod = prp.tile([P, 32, DK], F32, name="prod", tag="prod")
-            st["prod%d" % hf] = prod
-            if hf % 4 == 3:
-                nc.gpsimd.tensor_tensor(
-                    out=prod[:],
-                    in0=xv[:, half * 2048:(half + 1) * 2048].rearrange("p (d c) -> p d c", c=DK),
-                    in1=qd[:, v, :].unsqueeze(1).to_broadcast([P, 32, DK]),
-                    op=ALU.mult,
-                )
-            else:
-                nc.vector.scalar_tensor_tensor(
-                    out=prod[:],
-                    in0=xv[:, half * 2048:(half + 1) * 2048].rearrange("p (d c) -> p d c", c=DK),
-                    scalar=dec_f[:, V_HEADS[v]:V_HEADS[v] + 1],
-                    in1=qps[:, v, :].unsqueeze(1).to_broadcast([P, 32, DK]),
-                    op0=ALU.mult,
-                    op1=ALU.mult,
-                )
+            h = V_HEADS[v]
+            live["prod", hf] = prod_pool.tile([P, 32, DK], F32, name="prod", tag="prod")
+            nc.vector.scalar_tensor_tensor(
+                out=live["prod", hf][:],
+                in0=live["xv", v][:, half * 32 * DK:(half + 1) * 32 * DK].rearrange("p (d c) -> p d c", c=DK),
+                scalar=dec_f[:, h:h + 1],
+                in1=q_ps[:, v, :].unsqueeze(1).to_broadcast([P, 32, DK]),
+                op0=ALU.mult,
+                op1=ALU.mult,
+            )
 
-        def r_cols(hf):
+        def r_place(hf):
             h = V_HEADS[hf // 2]
             return h // 2, (h % 2) * DH + (hf % 2) * 32
 
-        def scalar_sums(hf, q):
-            prod = st["prod%d" % hf]
-            blk, c0 = r_cols(hf)
-            for dd in range(8 * q, 8 * q + 8):
+        def scalar_sums(hf, quarter):
+            block, c0 = r_place(hf)
+            prod = live["prod", hf]
+            for d in range(8 * quarter, 8 * quarter + 8):
                 nc.scalar.activation(
-                    out=prod[:, dd, :], in_=prod[:, dd, :], func=ACT.Copy, accum_out=r[:, blk, c0 + dd:c0 + dd + 1]
+                    out=prod[:, d, :], in_=prod[:, d, :], func=ACT.Copy, accum_out=r[:, block, c0 + d:c0 + d + 1]
                 )
 
         def vector_sums(hf):
-            blk, c0 = r_cols(hf)
-            nc.vector.tensor_reduce(out=r[:, blk, c0:c0 + 32], in_=st["prod%d" % hf][:], axis=AX.X, op=ALU.add)
+            block, c0 = r_place(hf)
+            nc.vector.tensor_reduce(out=r[:, block, c0:c0 + 32], in_=live["prod", hf][:], axis=AX.X, op=ALU.add)
 
         def regroup(c, j):
-            grp = grpp.tile([P, 2048], BF16, name="grp", tag="grp", align_bytes=64)
-            st["grp%d" % (3 * c + j)] = grp
+            live["grp", c, j] = grp_pool.tile([P, 2048], BF16, name="grp", tag="grp", align_bytes=64)
             nc.gpsimd.tensor_scalar(
-                out=grp[:].rearrange("p (w t) -> p w t", t=4),
-                in0=st["raw%d" % c][:, :, 512 * j:512 * j + 512].rearrange("p t w -> p w t"),
+                out=live["grp", c, j][:].rearrange("p (w t) -> p w t", t=4),
+                in0=live["raw", c][:, :, 512 * j:512 * j + 512].rearrange("p t w -> p w t"),
                 scalar1=1.0, scalar2=0.0, op0=ALU.mult, op1=ALU.add,
             )
 
         def quantise(c, j):
-            g = c % 3
+            cols = slice(512 * j, 512 * j + 512)
             nc.vector.quantize_mx(
-                out=wc[:, g, 512 * j:512 * j + 512].bitcast(FP8X4), scales=ws[:, g, 512 * j:512 * j + 512],
-                in_=st["grp%d" % (3 * c + j)][:],
+                out=w_codes[:, c % 3, cols].bitcast(FP8X4), scales=w_scales[:, c % 3, cols], in_=live["grp", c, j][:]
             )
 
-        def v_passes():
+        def x_transposes():
+            x_words = x_sb[:].bitcast(F32)
+            for g in range(3):
+                pool, tag = (ps_misc, "misc") if g < 2 else (ps_mm, "mm")
+                live["xt", g] = pool.tile([P, 2, P], F32, name="xt", tag=tag)
+                for u in range(2):
+                    w0 = 256 * g + 128 * u
+                    nc.tensor.transpose(live["xt", g][:, u, :], x_words[:, w0:w0 + 128], ident_f[:])
+
+        def x_quantise():
+            x_grp = keep.tile([P, 3, 512], BF16, align_bytes=64)
+            for g in range(3):
+                nc.vector.tensor_copy(
+                    out=x_grp[:, g, :].bitcast(F32).rearrange("p (b u) -> p b u", u=2),
+                    in_=live["xt", g][:].rearrange("p u b -> p b u"),
+                )
+            for g in range(3):
+                nc.vector.quantize_mx(out=x_codes[:, g, :].bitcast(FP8X4), scales=x_scales[:, g, :], in_=x_grp[:, g, :])
+
+        def big_passes(sums, codes, scales, g, first, last):
             for nb in range(3):
-                acc = psc.tile([P, 512], F32, name="acc%d" % nb, tag="c") if nb < 2 else psb.tile([P, 512], F32, name="acc2", tag="b")
-                st["acc%d" % nb] = acc
-                for g in range(3):
-                    nc.tensor.matmul_mx(
-                        out=acc[:],
-                        lhsT=xc[:, g, :].bitcast(FP8X4),
-                        lhsT_scale=xs[:, g, :],
-                        rhs=wc[:, g, 512 * nb:512 * nb + 512].bitcast(FP8X4),
-                        rhs_scale=ws[:, g, 512 * nb:512 * nb + 512],
-                        start=(g == 0),
-                        stop=(g == 2),
-                    )
+                cols = slice(512 * nb, 512 * nb + 512)
+                nc.tensor.matmul_mx(
+                    out=sums[nb][:],
+                    lhsT=codes[:, g, :].bitcast(FP8X4),
+                    lhsT_scale=scales[:, g, :],
+                    rhs=w_codes[:, g, cols].bitcast(FP8X4),
+                    rhs_scale=w_scales[:, g, cols],
+                    start=first,
+                    stop=last,
+                )
 
         def v_scale():
             for nb in range(3):
                 nc.vector.tensor_tensor(
                     out=sv[:, 4 * nb:4 * nb + 4, :].rearrange("p k (h d) -> p (k h) d", d=DH),
-                    in0=st["acc%d" % nb][:].rearrange("p (h d) -> p h d", d=DH),
-                    in1=s_t[:, 8 * nb:8 * nb + 8].unsqueeze(2).to_broadcast([P, 8, DH]),
+                    in0=live["v"][nb][:].rearrange("p (h d) -> p h d", d=DH),
+                    in1=qk_sum[:, 8 * nb:8 * nb + 8].unsqueeze(2).to_broadcast([P, 8, DH]),
                     op=ALU.mult,
                 )
 
-        def norm_a(ui):
+        def norm_sums(ui):
             b0, b1 = UNITS[ui]
-            rv = r[:, b0:b1 + 1:b1 - b0, :]
-            nc.vector.tensor_tensor(out=rv, in0=rv, in1=sv[:, b0:b1 + 1:b1 - b0, :], op=ALU.add)
+            r_unit = r[:, b0:b1 + 1:b1 - b0, :]
+            nc.vector.tensor_tensor(out=r_unit, in0=r_unit, in1=sv[:, b0:b1 + 1:b1 - b0, :], op=ALU.add)
             sq = small.tile([P, 2, P], F32, tag="sq")
-            nc.vector.tensor_tensor(out=sq[:], in0=rv, in1=rv, op=ALU.mult)
-            ss = small.tile([P, 4], F32, name="ss", tag="ss")
-            st["ss%d" % ui] = ss
-            nc.vector.tensor_reduce(out=ss[:], in_=sq[:].rearrange("p k (h d) -> p (k h) d", d=DH), axis=AX.X, op=ALU.add)
+            nc.vector.tensor_tensor(out=sq[:], in0=r_unit, in1=r_unit, op=ALU.mult)
+            live["ss", ui] = small.tile([P, 4], F32, name="ss", tag="ss")
+            nc.vector.tensor_reduce(
+                out=live["ss", ui][:], in_=sq[:].rearrange("p k (h d) -> p (k h) d", d=DH), axis=AX.X, op=ALU.add
+            )
 
-        def norm_s(ui):
-            rms = small.tile([P, 4], F32, name="rms", tag="rms")
-            st["rms%d" % ui] = rms
-            nc.scalar.activation(out=rms[:], in_=st["ss%d" % ui][:], func=ACT.Sqrt, bias=eps_t[:], scale=1.0 / DH)
+        def norm_root(ui):
+            live["rms", ui] = small.tile([P, 4], F32, name="rms", tag="rms")
+            nc.scalar.activation(
+                out=live["rms", ui][:], in_=live["ss", ui][:], func=ACT.Sqrt, bias=eps_t[:], scale=1.0 / DH
+            )
 
-        def norm_b(ui):
-            b0, b1 = UNITS[ui]
-            kg = ui // 2
-            if "nb%d" % kg not in st:
-                st["nb%d" % kg] = keep.tile([P, 4, P], BF16, name="nbf%d" % kg)
-            rstd = small.tile([P, 4], F32, tag="rstd")
-            nc.vector.reciprocal(out=rstd[:], in_=st["rms%d" % ui][:])
+        def norm_apply(ui):
+            g = ui // 2
+            if ("n", g) not in live:
+                live["n", g] = keep.tile([P, 4, P], BF16, name="n%d" % g)
+            inv = small.tile([P, 4], F32, tag="inv")
+            nc.vector.reciprocal(out=inv[:], in_=live["rms", ui][:])
             for k in range(2):
                 nc.vector.tensor_tensor(
-                    out=st["nb%d" % kg][:, 2 * (ui % 2) + k, :].rearrange("p (h d) -> p h d", d=DH),
-                    in0=r[:, (b0, b1)[k], :].rearrange("p (h d) -> p h d", d=DH),
-                    in1=rstd[:, 2 * k:2 * k + 2].unsqueeze(2).to_broadcast([P, 2, DH]),
+                    out=live["n", g][:, 2 * (ui % 2) + k, :].rearrange("p (h d) -> p h d", d=DH),
+                    in0=r[:, UNITS[ui][k], :].rearrange("p (h d) -> p h d", d=DH),
+                    in1=inv[:, 2 * k:2 * k + 2].unsqueeze(2).to_broadcast([P, 2, DH]),
                     op=ALU.mult,
                 )
 
-        def n_transposes(kg):
-            nt = psc.tile([P, 4, P], BF16, name="nt", tag="c")
-            st["nt"] = nt
+        def n_transposes(g):
+            live["nt"] = ps_misc.tile([P, 4, P], BF16, name="nt", tag="misc")
             for t in range(4):
-                nc.tensor.transpose(nt[:, t, :], st["nb%d" % kg][:, t, :], ident_b[:])
+                nc.tensor.transpose(live["nt"][:, t, :], live["n", g][:, t, :], ident_b[:])
 
-        def n_copy(kg):
-            ng = small.tile([P, 512], BF16, name="ng", tag="ng", align_bytes=64)
-            st["ng"] = ng
-            nc.scalar.copy(out=ng[:].rearrange("p (b t) -> p b t", t=4), in_=st["nt"][:].rearrange("p t b -> p b t"))
+        def n_copy():
+            live["ng"] = small.tile([P, 512], BF16, name="ng", tag="ng", align_bytes=64)
+            nc.scalar.copy(out=live["ng"][:].rearrange("p (b t) -> p b t", t=4), in_=live["nt"][:].rearrange("p t b -> p b t"))
 
-        def n_quantise(kg):
-            nc.vector.quantize_mx(out=ncd[:, kg, :].bitcast(FP8X4), scales=nsc[:, kg, :], in_=st["ng"][:])
-
-        def out_passes(kg):
-            for nb in range(3):
-                if kg == 0:
-                    st["oa%d" % nb] = psa.tile([P, 512], F32, name="oa%d" % nb, tag="a")
-                nc.tensor.matmul_mx(
-                    out=st["oa%d" % nb][:],
-                    lhsT=ncd[:, kg, :].bitcast(FP8X4),
-                    lhsT_scale=nsc[:, kg, :],
-                    rhs=wc[:, kg, 512 * nb:512 * nb + 512].bitcast(FP8X4),
-                    rhs_scale=ws[:, kg, 512 * nb:512 * nb + 512],
-                    start=(kg == 0),
-                    stop=(kg == 2),
-                )
+        def n_quantise(g):
+            nc.vector.quantize_mx(out=n_codes[:, g, :].bitcast(FP8X4), scales=n_scales[:, g, :], in_=live["ng"][:])
 
         for tick in range(N_TICKS):
-            rnd, k = tick // 8, tick % 8
+            rnd, k = divmod(tick, TICKS)
+
             if tick in (1, 3, 5):
-                rq_transposes(tick // 2)
+                q_transposes(tick // 2)
             if tick in (2, 4, 6):
-                rq_copy(tick // 2 - 1)
-            if rnd < 6:
+                q_copy(tick // 2 - 1)
+
+            if rnd < N_TILES:
                 transposes(rnd, 2 * k)
                 transposes(rnd, 2 * k + 1)
-            if 1 <= rnd <= 6:
+            if 1 <= rnd <= N_TILES:
                 if k < 4:
                     readout_matmuls(rnd - 1, k)
                 if k == 4:
@@ -352,69 +352,70 @@ def tile_multiscaleretention_pb_kernel(tc, x, qr, kr, decay, prev_kv, Wv, Wo, ou
                     back_transposes()
                 if k == 6 and rnd % 2 == 0:
                     back_copies(rnd // 2 - 1)
-            for hf in range(24):
-                if tick == (2 * hf - 2 if hf % 4 == 3 else 2 * hf):
-                    product(hf)
-            for hf in range(24):
-                if hf % 2 == 0 and 0 <= tick - 2 * hf - 3 < 4:
-                    scalar_sums(hf, tick - 2 * hf - 3)
-                if hf % 2 == 1 and tick == 2 * hf + 3:
-                    vector_sums(hf)
-            for c in range(6):
-                for j in range(3):
-                    if tick == 8 * c + PIECE_TICK[j]:
-                        regroup(c, j)
-                    if tick == 8 * c + PIECE_TICK[j] + 4:
-                        quantise(c, j)
+
+            if tick % 2 == 0 and tick // 2 < N_HALVES:
+                product(tick // 2)
+            late = tick - SUM_LAG
+            if late >= 0 and late % 6 < 4 and 3 * (late // 6) < N_HALVES:
+                scalar_sums(3 * (late // 6), late % 6)
+            if late >= 0 and late % 2 == 0 and (late // 2) % 3 != 0 and late // 2 < N_HALVES:
+                vector_sums(late // 2)
+
+            c_q, k_q = divmod(tick - QUANTISE_LAG, TICKS)
+            for j in range(3):
+                if rnd < 6 and k == PIECE_TICK[j]:
+                    regroup(rnd, j)
+                if 0 <= c_q < 6 and k_q == PIECE_TICK[j]:
+                    quantise(c_q, j)
+
             if tick == 12:
-                xw = x_sb[:].bitcast(F32)
-                for g in range(3):
-                    xt = psc.tile([P, 2, P], F32, name="xt%d" % g, tag="c") if g < 2 else psb.tile([P, 2, P], F32, name="xt2", tag="b")
-                    st["xt%d" % g] = xt
-                    for u in range(2):
-                        nc.tensor.transpose(xt[:, u, :], xw[:, 256 * g + 128 * u:256 * g + 128 * u + 128], ident_f[:])
+                x_transposes()
             if tick == 14:
-                nc.vector.tensor_reduce(out=s_t[:], in_=qk[:], axis=AX.X, op=ALU.add)
-                xg = keep.tile([P, 3 * 512], BF16, align_bytes=64)
+                nc.vector.tensor_reduce(out=qk_sum[:], in_=qk[:], axis=AX.X, op=ALU.add)
+                x_quantise()
+            if tick == V_TICK:
+                live["v"] = [
+                    ps_misc.tile([P, 512], F32, name="v0", tag="misc"),
+                    ps_misc.tile([P, 512], F32, name="v1", tag="misc"),
+                    ps_mm.tile([P, 512], F32, name="v2", tag="mm"),
+                ]
                 for g in range(3):
-                    nc.vector.tensor_copy(
-                        out=xg[:, 512 * g:512 * g + 512].bitcast(F32).rearrange("p (b u) -> p b u", u=2),
-                        in_=st["xt%d" % g][:].rearrange("p u b -> p b u"),
-                    )
-                for g in range(3):
-                    nc.vector.quantize_mx(out=xc[:, g, :].bitcast(FP8X4), scales=xs[:, g, :], in_=xg[:, 512 * g:512 * g + 512])
-            if tick == 28:
-                v_passes()
-            if tick == 31:
+                    big_passes(live["v"], x_codes, x_scales, g, g == 0, g == 2)
+            if tick == V_TICK + 3:
                 v_scale()
-            if k == 7 and rnd + 2 < 6:
-                load_xp(rnd + 2)
+
+            if k == 7 and rnd + 2 < N_TILES:
+                load_tile(rnd + 2)
             if k == 0 and rnd + 1 < 6:
-                load_raw(rnd + 1)
-            if tick % 4 == 0 and 3 <= tick // 4 + 2 < 12:
-                load_xv(tick // 4 + 2)
+                load_weights(rnd + 1)
+            if tick % 4 == 0 and 3 <= tick // 4 + 2 < len(V_HEADS):
+                load_head(tick // 4 + 2)
+
             for ui in range(6):
-                if tick == UNIT_TICK[ui]:
-                    norm_a(ui)
-                if tick == UNIT_TICK[ui] + 1:
-                    norm_s(ui)
-                if tick == UNIT_TICK[ui] + 2:
-                    norm_b(ui)
-            for kg in range(3):
-                t0 = max(UNIT_TICK[2 * kg], UNIT_TICK[2 * kg + 1])
-                if tick == t0 + 3:
-                    n_transposes(kg)
-                if tick == t0 + 4:
-                    n_copy(kg)
-                if tick == t0 + 5:
-                    n_quantise(kg)
-                if tick == max(t0 + 6, 49 + kg):
-                    out_passes(kg)
+                step = tick - unit_tick(ui)
+                if step == 0:
+                    norm_sums(ui)
+                if step == 1:
+                    norm_root(ui)
+                if step == 2:
+                    norm_apply(ui)
+            for g in range(3):
+                step = tick - pass_tick(g)
+                if step == 0:
+                    n_transposes(g)
+                if step == 1:
+                    n_copy()
+                if step == 2:
+                    n_quantise(g)
+                if tick == max(pass_tick(g) + 3, N_TILES * TICKS + 1 + g):
+                    if g == 0:
+                        live["o"] = [ps_rot.tile([P, 512], F32, name="o%d" % nb, tag="rot") for nb in range(3)]
+                    big_passes(live["o"], n_codes, n_scales, g, g == 0, g == 2)
 
         for nb in range(3):
-            ob = prp.tile([P, 512], F32, tag="prod")
+            o_sb = prod_pool.tile([P, 512], F32, tag="prod")
             if nb == 1:
-                nc.vector.tensor_copy(out=ob[:], in_=st["oa%d" % nb][:])
+                nc.vector.tensor_copy(out=o_sb[:], in_=live["o"][nb][:])
             else:
-                nc.scalar.copy(out=ob[:], in_=st["oa%d" % nb][:])
-            nc.sync.dma_start(out=of[:, 512 * nb:512 * nb + 512], in_=ob[:])
+                nc.scalar.copy(out=o_sb[:], in_=live["o"][nb][:])
+            nc.sync.dma_start(out=out_rows[:, 512 * nb:512 * nb + 512], in_=o_sb[:])

@@ -18,29 +18,21 @@ HEAD = DH * DK
 EPS = 1e-6
 FLOPS = 2 * 2 * P * E * V + 4 * P * H * DH * DK
 
-N_TILES = 6
-V_HEADS = (6, 7, 8, 9, 10, 11, 18, 19, 20, 21, 22, 23)
+A_BLOCKS = (0, 2, 4, 5, 7, 9, 10)
+V_BLOCKS = (1, 3, 6, 8, 11)
+N_A = len(A_BLOCKS)
+V_HEADS = tuple(2 * b + a for b in V_BLOCKS for a in range(2))
 N_HALVES = 2 * len(V_HEADS)
-UNITS = ((0, 6), (3, 4), (1, 7), (5, 9), (2, 8), (10, 11))
-TICKS = 8
-PIECE_TICK = (2, 4, 7)
-QUANTISE_LAG = 4
-SUM_LAG = 3
-V_TICK = 28
-FIRST_NORM_TICK = V_TICK + 4
-N_TICKS = 62
+GROUPS = 16
+A_END = N_A * GROUPS
 
-
-def unit_tick(ui):
-    if ui % 2 == 0:
-        ready = TICKS * (ui + 2) + 7
-    else:
-        ready = 2 * (4 * ui + 3) + SUM_LAG + 4
-    return max(FIRST_NORM_TICK, ready)
-
-
-def pass_tick(g):
-    return max(unit_tick(2 * g), unit_tick(2 * g + 1)) + 3
+PAIR = 12
+Q_FIRST, Q_STEP = 12, 6
+N_PIECES = 18
+S_ROWS = 24
+V_GROUP = Q_FIRST + 8 * Q_STEP + 1
+NORM_GROUPS = (66, 72, 79, 95, 111, 128)
+N_GROUPS = 136
 
 
 def tile_multiscaleretention_pb_kernel(tc, x, qr, kr, decay, prev_kv, Wv, Wo, out):
@@ -48,15 +40,14 @@ def tile_multiscaleretention_pb_kernel(tc, x, qr, kr, decay, prev_kv, Wv, Wo, ou
     x_rows = x.rearrange("b t e -> b (t e)")
     q_rows = qr.rearrange("b h t c -> b (h t c)")
     k_rows = kr.rearrange("b h t c -> b (h t c)")
-    state_by_seq = prev_kv.rearrange("b h d c -> b (h d c)")
-    state_by_half = prev_kv.rearrange("b (hh hp) d c -> (b hh) (hp d c)", hh=2)
+    state = prev_kv.rearrange("b h d c -> b (h d c)")
     out_rows = out.rearrange("b t e -> b (t e)")
 
     with ExitStack() as ctx:
         keep = ctx.enter_context(tc.tile_pool(name="keep", bufs=1))
         small = ctx.enter_context(tc.tile_pool(name="small", bufs=2))
         raw_pool = ctx.enter_context(tc.tile_pool(name="raw_pool", bufs=2))
-        grp_pool = ctx.enter_context(tc.tile_pool(name="grp_pool", bufs=2))
+        grp_pool = ctx.enter_context(tc.tile_pool(name="grp_pool", bufs=1))
         xp_pool = ctx.enter_context(tc.tile_pool(name="xp_pool", bufs=2))
         z_pool = ctx.enter_context(tc.tile_pool(name="z_pool", bufs=2))
         xv_pool = ctx.enter_context(tc.tile_pool(name="xv_pool", bufs=3))
@@ -71,16 +62,18 @@ def tile_multiscaleretention_pb_kernel(tc, x, qr, kr, decay, prev_kv, Wv, Wo, ou
         live = {}
 
         def load_tile(i):
-            t, half = i // 2, i % 2
-            live["xp", i] = xp_pool.tile([P, 2 * HEAD], BF16, name="xp", tag="xp")
-            nc.sync.dma_start(
-                out=live["xp", i][:], in_=state_by_half[P * half:P * half + P, 2 * t * HEAD:(2 * t + 2) * HEAD]
-            )
+            c0 = 2 * A_BLOCKS[i] * HEAD
+            xp = xp_pool.tile([P, 2 * HEAD], BF16, name="xp", tag="xp")
+            live["xp", i] = xp
+            for a in range(2):
+                nc.sync.dma_start(out=xp[:, a * HEAD:(a + 1) * HEAD], in_=state[:, c0 + a * HEAD:c0 + (a + 1) * HEAD])
 
-        def load_head(v):
+        def load_head(v, parts=1):
             h = V_HEADS[v]
             live["xv", v] = xv_pool.tile([P, HEAD], BF16, name="xv", tag="xv")
-            nc.sync.dma_start(out=live["xv", v][:], in_=state_by_seq[:, h * HEAD:(h + 1) * HEAD])
+            w = HEAD // parts
+            for c0 in range(0, HEAD, w):
+                nc.sync.dma_start(out=live["xv", v][:, c0:c0 + w], in_=state[:, h * HEAD + c0:h * HEAD + c0 + w])
 
         def load_weights(c):
             raw = raw_pool.tile([P, 4, V], BF16, name="raw", tag="raw")
@@ -90,55 +83,55 @@ def tile_multiscaleretention_pb_kernel(tc, x, qr, kr, decay, prev_kv, Wv, Wo, ou
                     rows = Wv[512 * c + 256 * u:512 * c + 256 * u + 256, :]
                     nc.sync.dma_start(out=raw[:, 2 * u:2 * u + 2, :], in_=rows.rearrange("(q e) c -> q e c", e=2))
             else:
-                for t in range(4):
-                    block = UNITS[2 * (c - 3) + t // 2][t % 2]
-                    nc.sync.dma_start(out=raw[:, t, :], in_=Wo[P * block:P * block + P, :])
+                rows = Wo[512 * (c - 3):512 * (c - 3) + 512, :]
+                nc.sync.dma_start(out=raw[:], in_=rows.rearrange("(t p) c -> p t c", t=4))
 
         q_sb = keep.tile([P, E], BF16)
         nc.sync.dma_start(out=q_sb[:], in_=q_rows)
         dec_b = keep.tile([P, H], BF16)
         nc.sync.dma_start(out=dec_b[:], in_=decay.partition_broadcast(P))
+        load_head(0, 2)
         load_tile(0)
-        load_head(0)
+        load_weights(0)
+        load_head(1)
+        load_tile(1)
         k_sb = keep.tile([P, E], BF16)
         nc.sync.dma_start(out=k_sb[:], in_=k_rows)
         x_sb = keep.tile([P, E], BF16)
         nc.sync.dma_start(out=x_sb[:], in_=x_rows)
-        load_head(1)
-        load_weights(0)
-        load_tile(1)
         load_head(2)
+        load_weights(1)
 
-        ident_b = keep.tile([P, P], BF16)
-        make_identity(nc, ident_b[:])
-        ident_f = keep.tile([P, P], F32)
-        make_identity(nc, ident_f[:])
         eps_t = keep.tile([P, 1], F32)
         nc.vector.memset(eps_t[:], EPS)
         warm = keep.tile([P, 1], F32)
         nc.scalar.activation(out=warm[:], in_=eps_t[:], func=ACT.Sqrt)
+        ident_b = keep.tile([P, P], BF16)
+        make_identity(nc, ident_b[:])
+        ident_f = keep.tile([P, P], F32)
+        make_identity(nc, ident_f[:])
+        perm = keep.tile([P, P], BF16)
+        nc.vector.tensor_copy(
+            out=perm[:].rearrange("p (j b2) -> p j b2", b2=2), in_=ident_b[:].rearrange("p (b2 j) -> p j b2", b2=2)
+        )
+        q_pad = z_pool.tile([P, 12 * 2 * 2 * P], BF16, tag="z")
+        nc.gpsimd.memset(q_pad[:].bitcast(U32), 0)
 
-        q_pad = z_pool.tile([P, 6 * 2 * 2 * P], BF16, tag="z")
-        nc.vector.memset(q_pad[:], 0.0)
-        q_pad_v = q_pad[:].rearrange("p (hp hh e k) -> p hp hh e k", hh=2, e=2, k=P)
-        q_tensor = q_sb[:].rearrange("p (hh hp c) -> p hp hh c", hh=2, c=DK)[:, 0:6, :, :]
-        nc.vector.tensor_copy(out=q_pad_v[:, :, :, 0, 0:DK], in_=q_tensor)
-        nc.vector.tensor_copy(out=q_pad_v[:, :, :, 1, DK:P], in_=q_tensor)
-        dec_f = keep.tile([P, H], F32)
-        nc.vector.tensor_copy(out=dec_f[:], in_=dec_b[:])
-        q_up = ps_rot.tile([P, 6, P], BF16, tag="rot")
-        for j in range(6):
-            h = V_HEADS[2 * j]
-            nc.tensor.transpose(q_up[:, j, :], q_sb[:, h * DK:h * DK + P], ident_b[:])
-        q_t = keep.tile([P, 6, P], BF16)
+        q_up = ps_rot.tile([P, 5, P], BF16, tag="rot")
+        for j in range(5):
+            nc.tensor.transpose(q_up[:, j, :], q_sb[:, V_BLOCKS[j] * P:V_BLOCKS[j] * P + P], ident_b[:])
+        q_t = keep.tile([P, 5, P], BF16)
         nc.scalar.copy(out=q_t[:], in_=q_up[:])
         q_ps = ps_q.tile([P, len(V_HEADS), DK], BF16, tag="q")
-        for j in range(6):
+        for j in range(5):
             nc.tensor.transpose(q_ps[:, 2 * j:2 * j + 2, :].rearrange("p a c -> p (a c)"), q_t[:, j, :], ident_b[:])
+        dec_f = keep.tile([P, H], F32)
+        nc.vector.tensor_copy(out=dec_f[:], in_=dec_b[:])
+        q_pad_v = q_pad[:].rearrange("p (h e k) -> p h e k", e=2, k=P)
+        q_heads = q_sb[:].rearrange("p (h c) -> p h c", c=DK)
         qk = keep.tile([P, H, DK], F32)
-        nc.gpsimd.tensor_tensor(out=qk[:].rearrange("p h c -> p (h c)"), in0=q_sb[:], in1=k_sb[:], op=ALU.mult)
 
-        q_mov = keep.tile([P, 3, P, 8], BF16)
+        q_mov = keep.tile([P, N_A, P, 4], BF16)
         qk_sum = keep.tile([P, H], F32)
         x_codes = keep.tile([P, 3, P], U32, align_bytes=64)
         x_scales = keep.tile([P, 3, P], U8, align_bytes=64)
@@ -149,61 +142,61 @@ def tile_multiscaleretention_pb_kernel(tc, x, qr, kr, decay, prev_kv, Wv, Wo, ou
         n_codes = keep.tile([P, 3, P], U32, align_bytes=64)
         n_scales = keep.tile([P, 3, P], U8, align_bytes=64)
 
-        def q_transposes(t):
-            live["qm"] = ps_rot.tile([P, 8, P], BF16, name="qm", tag="rot")
+        def q_transposes(i):
+            live["qm"] = ps_rot.tile([P, 4, P], BF16, name="qm", tag="rot")
             for a in range(2):
-                for hh in range(2):
-                    for e in range(2):
-                        nc.tensor.transpose(live["qm"][:, a * 4 + hh * 2 + e, :], q_pad_v[:, 2 * t + a, hh, e, :], ident_b[:])
+                for e in range(2):
+                    nc.tensor.transpose(live["qm"][:, 2 * a + e, :], q_pad_v[:, 2 * A_BLOCKS[i] + a, e, :], perm[:])
 
-        def q_copy(t):
-            nc.scalar.copy(out=q_mov[:, t], in_=live["qm"][:].rearrange("p n b -> p b n"))
+        def q_copy(i):
+            nc.scalar.copy(out=q_mov[:, i], in_=live["qm"][:].rearrange("p n b -> p b n"))
 
         def transposes(i, g):
             if g == 0:
                 live["z", i] = z_pool.tile([P, 64 * P], BF16, name="z", tag="z")
-            z_words = live["z", i][:].bitcast(F32).rearrange("p (b s) -> p b s", s=64)
+            z_words = live["z", i][:].bitcast(F32).rearrange("p (j s) -> p j s", s=64)
             up = ps_rot.tile([P, 4, P], BF16, tag="rot")
             for k in range(4):
                 s = 4 * g + k
-                nc.tensor.transpose(up[:, k, :], live["xp", i][:, s * P:(s + 1) * P], ident_b[:])
+                nc.tensor.transpose(up[:, k, :], live["xp", i][:, s * P:(s + 1) * P], perm[:])
             nc.scalar.copy(
                 out=z_words[:, :, 4 * g:4 * g + 4].rearrange("p (v i) k -> p v k i", i=2),
                 in_=up[:].bitcast(F32).rearrange("p k (v i) -> p v k i", i=2),
             )
 
-        def readout_matmuls(i, quarter):
-            t, half = i // 2, i % 2
-            if quarter == 0:
+        def readout_matmuls(i, j0, n):
+            if j0 == 0:
                 live["mm"] = ps_mm.tile([P, 64, 8], F32, name="mm", tag="mm")
-            for b in range(16 * quarter, 16 * quarter + 16):
+            for j in range(j0, j0 + n):
                 nc.tensor.matmul(
-                    out=live["mm"][:, b, :], lhsT=live["z", i][:, b * P:(b + 1) * P], rhs=q_mov[:, t, 64 * half + b, :],
+                    out=live["mm"][:, j, :], lhsT=live["z", i][:, j * P:(j + 1) * P],
+                    rhs=q_mov[:, i, 2 * j:2 * j + 2, :].rearrange("p b n -> p (b n)"),
                     start=True, stop=True,
                 )
 
         def collect(i):
-            half = i % 2
-            if half == 0:
-                live["ct"] = ct_pool.tile([P, 8, P], F32, name="ct", tag="ct")
-            nc.scalar.copy(out=live["ct"][:, :, 64 * half:64 * half + 64], in_=live["mm"][:].rearrange("p b n -> p n b"))
+            live["ct"] = ct_pool.tile([P, 2, P], F32, name="ct", tag="ct")
+            for a in range(2):
+                rows = slice(64 * a, 64 * a + 64)
+                h = 2 * A_BLOCKS[i] + a
+                nc.scalar.activation(
+                    out=live["ct"][rows, :, :].rearrange("p e (b2 j) -> p e b2 j", b2=2),
+                    in_=live["mm"][rows, :, :].rearrange("p j (b2 a e) -> p a e b2 j", b2=2, a=2)[:, a],
+                    func=ACT.Copy, scale=dec_f[rows, h:h + 1],
+                )
 
         def back_transposes():
-            for a in range(2):
-                live["rb", a] = ps_misc.tile([P, 4, P], F32, name="rb", tag="misc")
-                for n in range(4):
-                    nc.tensor.transpose(live["rb", a][:, n, :], live["ct"][:, 4 * a + n, :], ident_f[:])
+            live["rb"] = ps_misc.tile([P, 2, P], F32, name="rb", tag="misc")
+            for e in range(2):
+                nc.tensor.transpose(live["rb"][:, e, :], live["ct"][:, e, :], ident_f[:])
 
-        def back_copies(t):
-            for a in range(2):
-                for hh in range(2):
-                    h = hh * 12 + 2 * t + a
-                    m0 = 64 * a + hh
-                    nc.scalar.activation(
-                        out=r[:, h // 2, (h % 2) * DH:(h % 2) * DH + DH].rearrange("p (j e) -> p j e", e=2),
-                        in_=live["rb", a][:, 2 * hh:2 * hh + 2, m0:m0 + 63:2].rearrange("p e j -> p j e"),
-                        func=ACT.Copy, scale=dec_f[:, h:h + 1],
-                    )
+        def back_copies(i):
+            for b2 in range(2):
+                rows = slice(64 * b2, 64 * b2 + 64)
+                nc.scalar.copy(
+                    out=r[rows, A_BLOCKS[i], :].rearrange("p (d e) -> p d e", e=2),
+                    in_=live["rb"][rows, :, :].rearrange("p e (d b2) -> p b2 d e", b2=2)[:, b2],
+                )
 
         def product(hf):
             v, half = hf // 2, hf % 2
@@ -213,7 +206,7 @@ def tile_multiscaleretention_pb_kernel(tc, x, qr, kr, decay, prev_kv, Wv, Wo, ou
                 out=live["prod", hf][:],
                 in0=live["xv", v][:, half * 32 * DK:(half + 1) * 32 * DK].rearrange("p (d c) -> p d c", c=DK),
                 scalar=dec_f[:, h:h + 1],
-                in1=q_ps[:, v, :].unsqueeze(1).to_broadcast([P, 32, DK]),
+                in1=(q_ps[:, v, :] if v else q_sb[:, h * DK:h * DK + DK]).unsqueeze(1).to_broadcast([P, 32, DK]),
                 op0=ALU.mult,
                 op1=ALU.mult,
             )
@@ -222,30 +215,34 @@ def tile_multiscaleretention_pb_kernel(tc, x, qr, kr, decay, prev_kv, Wv, Wo, ou
             h = V_HEADS[hf // 2]
             return h // 2, (h % 2) * DH + (hf % 2) * 32
 
-        def scalar_sums(hf, quarter):
+        def scalar_sums(hf, d0, n):
             block, c0 = r_place(hf)
             prod = live["prod", hf]
-            for d in range(8 * quarter, 8 * quarter + 8):
+            for d in range(d0, d0 + n):
                 nc.scalar.activation(
                     out=prod[:, d, :], in_=prod[:, d, :], func=ACT.Copy, accum_out=r[:, block, c0 + d:c0 + d + 1]
                 )
 
-        def vector_sums(hf):
+        def vector_sums(hf, d0, n):
             block, c0 = r_place(hf)
-            nc.vector.tensor_reduce(out=r[:, block, c0:c0 + 32], in_=live["prod", hf][:], axis=AX.X, op=ALU.add)
+            nc.vector.tensor_reduce(
+                out=r[:, block, c0 + d0:c0 + d0 + n], in_=live["prod", hf][:, d0:d0 + n, :], axis=AX.X, op=ALU.add
+            )
 
-        def regroup(c, j):
-            live["grp", c, j] = grp_pool.tile([P, 2048], BF16, name="grp", tag="grp", align_bytes=64)
+        def regroup(p):
+            c, j = divmod(p, 3)
+            live["grp"] = grp_pool.tile([P, 2048], BF16, name="grp", tag="grp", align_bytes=64)
             nc.gpsimd.tensor_scalar(
-                out=live["grp", c, j][:].rearrange("p (w t) -> p w t", t=4),
+                out=live["grp"][:].rearrange("p (w t) -> p w t", t=4),
                 in0=live["raw", c][:, :, 512 * j:512 * j + 512].rearrange("p t w -> p w t"),
                 scalar1=1.0, scalar2=0.0, op0=ALU.mult, op1=ALU.add,
             )
 
-        def quantise(c, j):
+        def quantise(p):
+            c, j = divmod(p, 3)
             cols = slice(512 * j, 512 * j + 512)
             nc.vector.quantize_mx(
-                out=w_codes[:, c % 3, cols].bitcast(FP8X4), scales=w_scales[:, c % 3, cols], in_=live["grp", c, j][:]
+                out=w_codes[:, c % 3, cols].bitcast(FP8X4), scales=w_scales[:, c % 3, cols], in_=live["grp"][:]
             )
 
         def x_transposes():
@@ -257,15 +254,19 @@ def tile_multiscaleretention_pb_kernel(tc, x, qr, kr, decay, prev_kv, Wv, Wo, ou
                     w0 = 256 * g + 128 * u
                     nc.tensor.transpose(live["xt", g][:, u, :], x_words[:, w0:w0 + 128], ident_f[:])
 
-        def x_quantise():
-            x_grp = keep.tile([P, 3, 512], BF16, align_bytes=64)
+        def x_copies():
+            live["x_grp"] = keep.tile([P, 3, 512], BF16, name="x_grp", align_bytes=64)
             for g in range(3):
                 nc.vector.tensor_copy(
-                    out=x_grp[:, g, :].bitcast(F32).rearrange("p (b u) -> p b u", u=2),
+                    out=live["x_grp"][:, g, :].bitcast(F32).rearrange("p (b u) -> p b u", u=2),
                     in_=live["xt", g][:].rearrange("p u b -> p b u"),
                 )
+
+        def x_quantise():
             for g in range(3):
-                nc.vector.quantize_mx(out=x_codes[:, g, :].bitcast(FP8X4), scales=x_scales[:, g, :], in_=x_grp[:, g, :])
+                nc.vector.quantize_mx(
+                    out=x_codes[:, g, :].bitcast(FP8X4), scales=x_scales[:, g, :], in_=live["x_grp"][:, g, :]
+                )
 
         def big_passes(sums, codes, scales, g, first, last):
             for nb in range(3):
@@ -289,22 +290,18 @@ def tile_multiscaleretention_pb_kernel(tc, x, qr, kr, decay, prev_kv, Wv, Wo, ou
                     op=ALU.mult,
                 )
 
-        def norm_sums(ui):
-            b0, b1 = UNITS[ui]
-            r_unit = r[:, b0:b1 + 1:b1 - b0, :]
-            nc.vector.tensor_tensor(out=r_unit, in0=r_unit, in1=sv[:, b0:b1 + 1:b1 - b0, :], op=ALU.add)
-            sq = small.tile([P, 2, P], F32, tag="sq")
-            nc.vector.tensor_tensor(out=sq[:], in0=r_unit, in1=r_unit, op=ALU.mult)
-            live["ss", ui] = small.tile([P, 4], F32, name="ss", tag="ss")
-            nc.vector.tensor_reduce(
-                out=live["ss", ui][:], in_=sq[:].rearrange("p k (h d) -> p (k h) d", d=DH), axis=AX.X, op=ALU.add
-            )
+        def norm_add(ui):
+            r_unit = r[:, 2 * ui:2 * ui + 2, :]
+            nc.vector.tensor_tensor(out=r_unit, in0=r_unit, in1=sv[:, 2 * ui:2 * ui + 2, :], op=ALU.add)
 
         def norm_root(ui):
+            ss = small.tile([P, 4], F32, name="ss", tag="ss")
+            sq = small.tile([P, 4, DH], F32, name="sq", tag="sq")
+            r_heads = r[:, 2 * ui:2 * ui + 2, :].rearrange("p k (h d) -> p (k h) d", d=DH)
+            for hh in range(4):
+                nc.scalar.activation(out=sq[:, hh, :], in_=r_heads[:, hh, :], func=ACT.Square, accum_out=ss[:, hh:hh + 1])
             live["rms", ui] = small.tile([P, 4], F32, name="rms", tag="rms")
-            nc.scalar.activation(
-                out=live["rms", ui][:], in_=live["ss", ui][:], func=ACT.Sqrt, bias=eps_t[:], scale=1.0 / DH
-            )
+            nc.scalar.activation(out=live["rms", ui][:], in_=ss[:], func=ACT.Sqrt, bias=eps_t[:], scale=1.0 / DH)
 
         def norm_apply(ui):
             g = ui // 2
@@ -312,13 +309,12 @@ def tile_multiscaleretention_pb_kernel(tc, x, qr, kr, decay, prev_kv, Wv, Wo, ou
                 live["n", g] = keep.tile([P, 4, P], BF16, name="n%d" % g)
             inv = small.tile([P, 4], F32, tag="inv")
             nc.vector.reciprocal(out=inv[:], in_=live["rms", ui][:])
-            for k in range(2):
-                nc.vector.tensor_tensor(
-                    out=live["n", g][:, 2 * (ui % 2) + k, :].rearrange("p (h d) -> p h d", d=DH),
-                    in0=r[:, UNITS[ui][k], :].rearrange("p (h d) -> p h d", d=DH),
-                    in1=inv[:, 2 * k:2 * k + 2].unsqueeze(2).to_broadcast([P, 2, DH]),
-                    op=ALU.mult,
-                )
+            nc.vector.tensor_tensor(
+                out=live["n", g][:, 2 * (ui % 2):2 * (ui % 2) + 2, :].rearrange("p k (h d) -> p (k h) d", d=DH),
+                in0=r[:, 2 * ui:2 * ui + 2, :].rearrange("p k (h d) -> p (k h) d", d=DH),
+                in1=inv[:].unsqueeze(2).to_broadcast([P, 4, DH]),
+                op=ALU.mult,
+            )
 
         def n_transposes(g):
             live["nt"] = ps_misc.tile([P, 4, P], BF16, name="nt", tag="misc")
@@ -332,85 +328,111 @@ def tile_multiscaleretention_pb_kernel(tc, x, qr, kr, decay, prev_kv, Wv, Wo, ou
         def n_quantise(g):
             nc.vector.quantize_mx(out=n_codes[:, g, :].bitcast(FP8X4), scales=n_scales[:, g, :], in_=live["ng"][:])
 
-        for tick in range(N_TICKS):
-            rnd, k = divmod(tick, TICKS)
+        regroup(0)
+        for g in range(N_GROUPS):
+            i, gg = divmod(g, GROUPS)
 
-            if tick in (1, 3, 5):
-                q_transposes(tick // 2)
-            if tick in (2, 4, 6):
-                q_copy(tick // 2 - 1)
+            for ui in range(6):
+                step = g - NORM_GROUPS[ui]
+                if step == 0:
+                    norm_add(ui)
+                if step == 1:
+                    norm_root(ui)
+                if step == 3:
+                    norm_apply(ui)
+            for ps in range(3):
+                step = g - NORM_GROUPS[2 * ps + 1] - 4
+                if step == 0:
+                    n_transposes(ps)
+                if step == 1:
+                    n_copy()
+                if step == 2:
+                    n_quantise(ps)
+            for p in range(N_PIECES):
+                if g == Q_FIRST + Q_STEP * p:
+                    quantise(p)
+                    if p + 1 < N_PIECES:
+                        regroup(p + 1)
 
-            if rnd < N_TILES:
-                transposes(rnd, 2 * k)
-                transposes(rnd, 2 * k + 1)
-            if 1 <= rnd <= N_TILES:
-                if k < 4:
-                    readout_matmuls(rnd - 1, k)
-                if k == 4:
-                    collect(rnd - 1)
-                if k == 5 and rnd % 2 == 0:
-                    back_transposes()
-                if k == 6 and rnd % 2 == 0:
-                    back_copies(rnd // 2 - 1)
+            if g < A_END:
+                transposes(i, gg)
+            if g == 2:
+                nc.vector.tensor_copy(out=q_pad_v[:, :, 0, 0:DK], in_=q_heads)
+                nc.vector.tensor_copy(out=q_pad_v[:, :, 1, DK:P], in_=q_heads)
+            if 4 <= g < 4 + N_A:
+                q_transposes(g - 4)
+                q_copy(g - 4)
+            if 1 <= i <= N_A:
+                if i < N_A:
+                    if gg < 8:
+                        readout_matmuls(i - 1, 8 * gg, 8)
+                    if gg == 9:
+                        collect(i - 1)
+                    if gg == 10:
+                        back_transposes()
+                    if gg == 12:
+                        back_copies(i - 1)
+                else:
+                    if gg < 4:
+                        readout_matmuls(i - 1, 16 * gg, 16)
+                    if gg == 5:
+                        collect(i - 1)
+                    if gg == 6:
+                        back_transposes()
+                    if gg == 7:
+                        back_copies(i - 1)
 
-            if tick % 2 == 0 and tick // 2 < N_HALVES:
-                product(tick // 2)
-            late = tick - SUM_LAG
-            if late >= 0 and late % 6 < 4 and 3 * (late // 6) < N_HALVES:
-                scalar_sums(3 * (late // 6), late % 6)
-            if late >= 0 and late % 2 == 0 and (late // 2) % 3 != 0 and late // 2 < N_HALVES:
-                vector_sums(late // 2)
+            m, pg = divmod(g, PAIR)
+            if 2 * m < N_HALVES:
+                if pg == 0:
+                    product(2 * m)
+                if pg == 8:
+                    product(2 * m + 1)
+            if m >= 1 and 2 * (m - 1) < N_HALVES:
+                if pg == 4:
+                    vector_sums(2 * (m - 1), 0, 16)
+                if pg == 6:
+                    vector_sums(2 * (m - 1), 16, 16)
+                    vector_sums(2 * (m - 1) + 1, S_ROWS, 32 - S_ROWS)
+            late = g - 11
+            ml, lg = divmod(late, PAIR)
+            if late >= 0 and 2 * ml < N_HALVES and lg < 8:
+                scalar_sums(2 * ml + 1, lg * S_ROWS // 8, S_ROWS // 8)
 
-            c_q, k_q = divmod(tick - QUANTISE_LAG, TICKS)
-            for j in range(3):
-                if rnd < 6 and k == PIECE_TICK[j]:
-                    regroup(rnd, j)
-                if 0 <= c_q < 6 and k_q == PIECE_TICK[j]:
-                    quantise(c_q, j)
-
-            if tick == 12:
-                x_transposes()
-            if tick == 14:
+            if g == 26:
+                nc.gpsimd.tensor_tensor(out=qk[:].rearrange("p h c -> p (h c)"), in0=q_sb[:], in1=k_sb[:], op=ALU.mult)
+            if g == 40:
                 nc.vector.tensor_reduce(out=qk_sum[:], in_=qk[:], axis=AX.X, op=ALU.add)
+            if g == 28:
+                x_transposes()
+            if g == 29:
+                x_copies()
+            if g == 30:
                 x_quantise()
-            if tick == V_TICK:
+            if g == V_GROUP:
                 live["v"] = [
                     ps_misc.tile([P, 512], F32, name="v0", tag="misc"),
                     ps_misc.tile([P, 512], F32, name="v1", tag="misc"),
                     ps_mm.tile([P, 512], F32, name="v2", tag="mm"),
                 ]
-                for g in range(3):
-                    big_passes(live["v"], x_codes, x_scales, g, g == 0, g == 2)
-            if tick == V_TICK + 3:
+                for c in range(3):
+                    big_passes(live["v"], x_codes, x_scales, c, c == 0, c == 2)
+            if g == V_GROUP + 2:
                 v_scale()
 
-            if k == 7 and rnd + 2 < N_TILES:
-                load_tile(rnd + 2)
-            if k == 0 and rnd + 1 < 6:
-                load_weights(rnd + 1)
-            if tick % 4 == 0 and 3 <= tick // 4 + 2 < len(V_HEADS):
-                load_head(tick // 4 + 2)
+            if gg == 15 and i + 2 < N_A:
+                load_tile(i + 2)
+            if pg == 8 and m + 3 < len(V_HEADS):
+                load_head(m + 3)
+            pd, pr = divmod(g - Q_FIRST, Q_STEP)
+            if pr == 1 and pd % 3 == 1 and 2 <= pd // 3 + 2 < 6:
+                load_weights(pd // 3 + 2)
 
-            for ui in range(6):
-                step = tick - unit_tick(ui)
-                if step == 0:
-                    norm_sums(ui)
-                if step == 1:
-                    norm_root(ui)
-                if step == 2:
-                    norm_apply(ui)
-            for g in range(3):
-                step = tick - pass_tick(g)
-                if step == 0:
-                    n_transposes(g)
-                if step == 1:
-                    n_copy()
-                if step == 2:
-                    n_quantise(g)
-                if tick == max(pass_tick(g) + 3, N_TILES * TICKS + 1 + g):
-                    if g == 0:
+            for ps in range(3):
+                if g == max(NORM_GROUPS[2 * ps + 1] + 7, A_END + 1 + 2 * ps):
+                    if ps == 0:
                         live["o"] = [ps_rot.tile([P, 512], F32, name="o%d" % nb, tag="rot") for nb in range(3)]
-                    big_passes(live["o"], n_codes, n_scales, g, g == 0, g == 2)
+                    big_passes(live["o"], n_codes, n_scales, ps, ps == 0, ps == 2)
 
         for nb in range(3):
             o_sb = prod_pool.tile([P, 512], F32, tag="prod")

@@ -21,18 +21,27 @@ FLOPS = 2 * 2 * P * E * V + 4 * P * H * DH * DK
 A_BLOCKS = (0, 2, 4, 5, 7, 9, 10)
 V_BLOCKS = (1, 3, 6, 8, 11)
 N_A = len(A_BLOCKS)
-V_HEADS = tuple(2 * b + a for b in V_BLOCKS for a in range(2))
-N_HALVES = 2 * len(V_HEADS)
 GROUPS = 16
 A_END = N_A * GROUPS
+HALVES = tuple((block, quarter) for block in V_BLOCKS for quarter in range(4))
+N_HALVES = len(HALVES)
+PRODUCT_GROUPS = tuple(11 * n // 2 for n in range(N_HALVES))
+XV_BUFS = 6
+S_ROWS = 16
 
-PAIR = 12
-Q_FIRST, Q_STEP = 12, 6
-N_PIECES = 18
-S_ROWS = 24
-V_GROUP = Q_FIRST + 8 * Q_STEP + 1
-NORM_GROUPS = (66, 72, 79, 95, 111, 128)
-N_GROUPS = 136
+QUANT_GROUPS = tuple(18 + 19 * p // 2 for p in range(10))
+QK_GROUP = 36
+X_GROUP = 40
+V_GROUP = QUANT_GROUPS[4] + 3
+NORM_GROUPS = (70, 72, 80, 97, 112, 121)
+N_GROUPS = 132
+N_SLACK = 2
+LOADS = sorted(
+    [(GROUPS * i + 4 * k, "tile", 4 * i + k) for i in range(N_A) for k in range(4)]
+    + [(PRODUCT_GROUPS[n] + 1, "half", n) for n in range(N_HALVES)]
+    + [(QUANT_GROUPS[p] - 9, "weights", c) for c, p in enumerate((0, 1, 3, 5, 6, 8))]
+    + [(QK_GROUP - 6, "k", 0), (X_GROUP - 6, "x", 0)]
+)
 
 
 def tile_multiscaleretention_pb_kernel(tc, x, qr, kr, decay, prev_kv, Wv, Wo, out):
@@ -50,7 +59,7 @@ def tile_multiscaleretention_pb_kernel(tc, x, qr, kr, decay, prev_kv, Wv, Wo, ou
         grp_pool = ctx.enter_context(tc.tile_pool(name="grp_pool", bufs=1))
         xp_pool = ctx.enter_context(tc.tile_pool(name="xp_pool", bufs=2))
         z_pool = ctx.enter_context(tc.tile_pool(name="z_pool", bufs=2))
-        xv_pool = ctx.enter_context(tc.tile_pool(name="xv_pool", bufs=3))
+        xv_pool = ctx.enter_context(tc.tile_pool(name="xv_pool", bufs=XV_BUFS))
         prod_pool = ctx.enter_context(tc.tile_pool(name="prod_pool", bufs=4))
         ct_pool = ctx.enter_context(tc.tile_pool(name="ct_pool", bufs=1))
         ps_rot = ctx.enter_context(tc.psum_pool(name="ps_rot", bufs=4))
@@ -61,19 +70,19 @@ def tile_multiscaleretention_pb_kernel(tc, x, qr, kr, decay, prev_kv, Wv, Wo, ou
 
         live = {}
 
-        def load_tile(i):
-            c0 = 2 * A_BLOCKS[i] * HEAD
-            xp = xp_pool.tile([P, 2 * HEAD], BF16, name="xp", tag="xp")
-            live["xp", i] = xp
-            for a in range(2):
-                nc.sync.dma_start(out=xp[:, a * HEAD:(a + 1) * HEAD], in_=state[:, c0 + a * HEAD:c0 + (a + 1) * HEAD])
+        def load_tile(part):
+            i, k = divmod(part, 4)
+            if k == 0:
+                live["xp", i] = xp_pool.tile([P, 2 * HEAD], BF16, name="xp", tag="xp")
+            w = HEAD // 2
+            c0 = 2 * A_BLOCKS[i] * HEAD + k * w
+            nc.sync.dma_start(out=live["xp", i][:, k * w:(k + 1) * w], in_=state[:, c0:c0 + w])
 
-        def load_head(v, parts=1):
-            h = V_HEADS[v]
-            live["xv", v] = xv_pool.tile([P, HEAD], BF16, name="xv", tag="xv")
-            w = HEAD // parts
-            for c0 in range(0, HEAD, w):
-                nc.sync.dma_start(out=live["xv", v][:, c0:c0 + w], in_=state[:, h * HEAD + c0:h * HEAD + c0 + w])
+        def load_half(n):
+            block, quarter = HALVES[n]
+            c0 = 2 * block * HEAD + quarter * (HEAD // 2)
+            live["xv", n] = xv_pool.tile([P, HEAD // 2], BF16, name="xv", tag="xv")
+            nc.sync.dma_start(out=live["xv", n][:], in_=state[:, c0:c0 + HEAD // 2])
 
         def load_weights(c):
             raw = raw_pool.tile([P, 4, V], BF16, name="raw", tag="raw")
@@ -90,17 +99,33 @@ def tile_multiscaleretention_pb_kernel(tc, x, qr, kr, decay, prev_kv, Wv, Wo, ou
         nc.sync.dma_start(out=q_sb[:], in_=q_rows)
         dec_b = keep.tile([P, H], BF16)
         nc.sync.dma_start(out=dec_b[:], in_=decay.partition_broadcast(P))
-        load_head(0, 2)
-        load_tile(0)
-        load_weights(0)
-        load_head(1)
-        load_tile(1)
         k_sb = keep.tile([P, E], BF16)
-        nc.sync.dma_start(out=k_sb[:], in_=k_rows)
         x_sb = keep.tile([P, E], BF16)
-        nc.sync.dma_start(out=x_sb[:], in_=x_rows)
-        load_head(2)
-        load_weights(1)
+        queue = list(LOADS)
+        done = {"tile": 0, "half": 0, "weights": 0}
+
+        def load_ready():
+            while queue:
+                kind, i = queue[0][1:]
+                if kind == "tile":
+                    if i // 4 - 2 >= done["tile"]:
+                        return
+                    load_tile(i)
+                elif kind == "half":
+                    if i - XV_BUFS >= done["half"]:
+                        return
+                    load_half(i)
+                elif kind == "weights":
+                    if i - 2 >= done["weights"]:
+                        return
+                    load_weights(i)
+                elif kind == "k":
+                    nc.sync.dma_start(out=k_sb[:], in_=k_rows)
+                else:
+                    nc.sync.dma_start(out=x_sb[:], in_=x_rows)
+                queue.remove(queue[0])
+
+        load_ready()
 
         eps_t = keep.tile([P, 1], F32)
         nc.vector.memset(eps_t[:], EPS)
@@ -108,30 +133,26 @@ def tile_multiscaleretention_pb_kernel(tc, x, qr, kr, decay, prev_kv, Wv, Wo, ou
         nc.scalar.activation(out=warm[:], in_=eps_t[:], func=ACT.Sqrt)
         ident_b = keep.tile([P, P], BF16)
         make_identity(nc, ident_b[:])
-        ident_f = keep.tile([P, P], F32)
-        make_identity(nc, ident_f[:])
         perm = keep.tile([P, P], BF16)
         nc.vector.tensor_copy(
             out=perm[:].rearrange("p (j b2) -> p j b2", b2=2), in_=ident_b[:].rearrange("p (b2 j) -> p j b2", b2=2)
         )
-        q_pad = z_pool.tile([P, 12 * 2 * 2 * P], BF16, tag="z")
-        nc.gpsimd.memset(q_pad[:].bitcast(U32), 0)
+        ident_f = keep.tile([P, P], F32)
+        make_identity(nc, ident_f[:])
+        q_mov = keep.tile([P, N_A, 2, P, 2], BF16)
+        nc.gpsimd.memset(q_mov[:].rearrange("p i e b a -> p (i e b a)").bitcast(U32), 0)
 
         q_up = ps_rot.tile([P, 5, P], BF16, tag="rot")
         for j in range(5):
             nc.tensor.transpose(q_up[:, j, :], q_sb[:, V_BLOCKS[j] * P:V_BLOCKS[j] * P + P], ident_b[:])
         q_t = keep.tile([P, 5, P], BF16)
         nc.scalar.copy(out=q_t[:], in_=q_up[:])
-        q_ps = ps_q.tile([P, len(V_HEADS), DK], BF16, tag="q")
-        for j in range(5):
-            nc.tensor.transpose(q_ps[:, 2 * j:2 * j + 2, :].rearrange("p a c -> p (a c)"), q_t[:, j, :], ident_b[:])
         dec_f = keep.tile([P, H], F32)
         nc.vector.tensor_copy(out=dec_f[:], in_=dec_b[:])
-        q_pad_v = q_pad[:].rearrange("p (h e k) -> p h e k", e=2, k=P)
-        q_heads = q_sb[:].rearrange("p (h c) -> p h c", c=DK)
+        q_ps = ps_q.tile([P, 2 * len(V_BLOCKS), DK], BF16, tag="q")
+        q_twice = keep.tile([P, H, 2, DK], BF16)
         qk = keep.tile([P, H, DK], F32)
 
-        q_mov = keep.tile([P, N_A, P, 4], BF16)
         qk_sum = keep.tile([P, H], F32)
         x_codes = keep.tile([P, 3, P], U32, align_bytes=64)
         x_scales = keep.tile([P, 3, P], U8, align_bytes=64)
@@ -143,13 +164,15 @@ def tile_multiscaleretention_pb_kernel(tc, x, qr, kr, decay, prev_kv, Wv, Wo, ou
         n_scales = keep.tile([P, 3, P], U8, align_bytes=64)
 
         def q_transposes(i):
-            live["qm"] = ps_rot.tile([P, 4, P], BF16, name="qm", tag="rot")
+            block = A_BLOCKS[i]
+            live["qm"] = ps_rot.tile([P, 2, P], BF16, name="qm", tag="rot")
             for a in range(2):
-                for e in range(2):
-                    nc.tensor.transpose(live["qm"][:, 2 * a + e, :], q_pad_v[:, 2 * A_BLOCKS[i] + a, e, :], perm[:])
+                nc.tensor.transpose(live["qm"][:, a, :], q_twice[:, 2 * block + a].rearrange("p e c -> p (e c)"), perm[:])
 
-        def q_copy(i):
-            nc.scalar.copy(out=q_mov[:, i], in_=live["qm"][:].rearrange("p n b -> p b n"))
+        def q_copies(i):
+            for e in range(2):
+                rows = slice(64 * e, 64 * e + 64)
+                nc.scalar.copy(out=q_mov[rows, i, e], in_=live["qm"][rows, :, :].rearrange("p a b -> p b a"))
 
         def transposes(i, g):
             if g == 0:
@@ -170,7 +193,7 @@ def tile_multiscaleretention_pb_kernel(tc, x, qr, kr, decay, prev_kv, Wv, Wo, ou
             for j in range(j0, j0 + n):
                 nc.tensor.matmul(
                     out=live["mm"][:, j, :], lhsT=live["z", i][:, j * P:(j + 1) * P],
-                    rhs=q_mov[:, i, 2 * j:2 * j + 2, :].rearrange("p b n -> p (b n)"),
+                    rhs=q_mov[:, i, :, 2 * j:2 * j + 2, :].rearrange("p e b a -> p e (b a)"),
                     start=True, stop=True,
                 )
 
@@ -181,7 +204,7 @@ def tile_multiscaleretention_pb_kernel(tc, x, qr, kr, decay, prev_kv, Wv, Wo, ou
                 h = 2 * A_BLOCKS[i] + a
                 nc.scalar.activation(
                     out=live["ct"][rows, :, :].rearrange("p e (b2 j) -> p e b2 j", b2=2),
-                    in_=live["mm"][rows, :, :].rearrange("p j (b2 a e) -> p a e b2 j", b2=2, a=2)[:, a],
+                    in_=live["mm"][rows, :, :].rearrange("p j (e b2 a) -> p a e b2 j", b2=2, a=2)[:, a],
                     func=ACT.Copy, scale=dec_f[rows, h:h + 1],
                 )
 
@@ -198,97 +221,108 @@ def tile_multiscaleretention_pb_kernel(tc, x, qr, kr, decay, prev_kv, Wv, Wo, ou
                     in_=live["rb"][rows, :, :].rearrange("p e (d b2) -> p b2 d e", b2=2)[:, b2],
                 )
 
-        def product(hf):
-            v, half = hf // 2, hf % 2
-            h = V_HEADS[v]
-            live["prod", hf] = prod_pool.tile([P, 32, DK], F32, name="prod", tag="prod")
+        def product(n):
+            block, quarter = HALVES[n]
+            h = 2 * block + quarter // 2
+            if n < 1:
+                q_row = q_sb[:, h * DK:h * DK + DK]
+            else:
+                q_row = q_ps[:, 2 * V_BLOCKS.index(block) + quarter // 2, :]
+            live["prod", n] = prod_pool.tile([P, 32, DK], F32, name="prod", tag="prod")
             nc.vector.scalar_tensor_tensor(
-                out=live["prod", hf][:],
-                in0=live["xv", v][:, half * 32 * DK:(half + 1) * 32 * DK].rearrange("p (d c) -> p d c", c=DK),
+                out=live["prod", n][:],
+                in0=live["xv", n][:].rearrange("p (d c) -> p d c", c=DK),
                 scalar=dec_f[:, h:h + 1],
-                in1=(q_ps[:, v, :] if v else q_sb[:, h * DK:h * DK + DK]).unsqueeze(1).to_broadcast([P, 32, DK]),
+                in1=q_row.unsqueeze(1).to_broadcast([P, 32, DK]),
                 op0=ALU.mult,
                 op1=ALU.mult,
             )
 
-        def r_place(hf):
-            h = V_HEADS[hf // 2]
-            return h // 2, (h % 2) * DH + (hf % 2) * 32
+        def scalar_sums(n, d0, rows):
+            block, quarter = HALVES[n]
+            prod = live["prod", n]
+            for d in range(d0, d0 + rows):
+                c0 = 32 * quarter + d
+                nc.scalar.activation(out=prod[:, d, :], in_=prod[:, d, :], func=ACT.Copy, accum_out=r[:, block, c0:c0 + 1])
 
-        def scalar_sums(hf, d0, n):
-            block, c0 = r_place(hf)
-            prod = live["prod", hf]
-            for d in range(d0, d0 + n):
-                nc.scalar.activation(
-                    out=prod[:, d, :], in_=prod[:, d, :], func=ACT.Copy, accum_out=r[:, block, c0 + d:c0 + d + 1]
-                )
-
-        def vector_sums(hf, d0, n):
-            block, c0 = r_place(hf)
+        def vector_sums(n, d0, rows):
+            block, quarter = HALVES[n]
+            c0 = 32 * quarter + d0
             nc.vector.tensor_reduce(
-                out=r[:, block, c0 + d0:c0 + d0 + n], in_=live["prod", hf][:, d0:d0 + n, :], axis=AX.X, op=ALU.add
+                out=r[:, block, c0:c0 + rows], in_=live["prod", n][:, d0:d0 + rows, :], axis=AX.X, op=ALU.add
             )
+
+        def piece(p):
+            w, pp = divmod(p, 5)
+            return w, 2 * pp, min(2 * pp + 2, 9)
 
         def regroup(p):
-            c, j = divmod(p, 3)
-            live["grp"] = grp_pool.tile([P, 2048], BF16, name="grp", tag="grp", align_bytes=64)
-            nc.gpsimd.tensor_scalar(
-                out=live["grp"][:].rearrange("p (w t) -> p w t", t=4),
-                in0=live["raw", c][:, :, 512 * j:512 * j + 512].rearrange("p t w -> p w t"),
-                scalar1=1.0, scalar2=0.0, op0=ALU.mult, op1=ALU.add,
-            )
+            w, s0, s1 = piece(p)
+            live["grp"] = grp_pool.tile([P, 4096], BF16, name="grp", tag="grp", align_bytes=64)
+            for s in range(s0, s1):
+                c, j = divmod(s, 3)
+                at = 2048 * (s - s0)
+                nc.gpsimd.tensor_scalar(
+                    out=live["grp"][:, at:at + 2048].rearrange("p (w t) -> p w t", t=4),
+                    in0=live["raw", 3 * w + c][:, :, 512 * j:512 * j + 512].rearrange("p t w -> p w t"),
+                    scalar1=1.0, scalar2=0.0, op0=ALU.mult, op1=ALU.add,
+                )
+            done["weights"] = 3 * w + s1 // 3
 
         def quantise(p):
-            c, j = divmod(p, 3)
-            cols = slice(512 * j, 512 * j + 512)
+            w, s0, s1 = piece(p)
+            cols = slice(512 * s0, 512 * s1)
             nc.vector.quantize_mx(
-                out=w_codes[:, c % 3, cols].bitcast(FP8X4), scales=w_scales[:, c % 3, cols], in_=live["grp"][:]
+                out=w_codes[:].rearrange("p g c -> p (g c)")[:, cols].bitcast(FP8X4),
+                scales=w_scales[:].rearrange("p g c -> p (g c)")[:, cols],
+                in_=live["grp"][:, 0:2048 * (s1 - s0)],
             )
 
-        def x_transposes():
-            x_words = x_sb[:].bitcast(F32)
-            for g in range(3):
-                pool, tag = (ps_misc, "misc") if g < 2 else (ps_mm, "mm")
-                live["xt", g] = pool.tile([P, 2, P], F32, name="xt", tag=tag)
-                for u in range(2):
-                    w0 = 256 * g + 128 * u
-                    nc.tensor.transpose(live["xt", g][:, u, :], x_words[:, w0:w0 + 128], ident_f[:])
+        x_grp = keep.tile([P, 3, 512], BF16, align_bytes=64)
 
-        def x_copies():
-            live["x_grp"] = keep.tile([P, 3, 512], BF16, name="x_grp", align_bytes=64)
-            for g in range(3):
-                nc.vector.tensor_copy(
-                    out=live["x_grp"][:, g, :].bitcast(F32).rearrange("p (b u) -> p b u", u=2),
-                    in_=live["xt", g][:].rearrange("p u b -> p b u"),
-                )
+        def x_transposes(g):
+            x_words = x_sb[:].bitcast(F32)
+            live["xt"] = ps_misc.tile([P, 2, P], F32, name="xt", tag="misc")
+            for u in range(2):
+                w0 = 256 * g + 128 * u
+                nc.tensor.transpose(live["xt"][:, u, :], x_words[:, w0:w0 + 128], ident_f[:])
+
+        def x_copies(g):
+            nc.vector.tensor_copy(
+                out=x_grp[:, g, :].bitcast(F32).rearrange("p (b u) -> p b u", u=2),
+                in_=live["xt"][:].rearrange("p u b -> p b u"),
+            )
 
         def x_quantise():
             for g in range(3):
                 nc.vector.quantize_mx(
-                    out=x_codes[:, g, :].bitcast(FP8X4), scales=x_scales[:, g, :], in_=live["x_grp"][:, g, :]
+                    out=x_codes[:, g, :].bitcast(FP8X4), scales=x_scales[:, g, :], in_=x_grp[:, g, :]
                 )
 
-        def big_passes(sums, codes, scales, g, first, last):
-            for nb in range(3):
-                cols = slice(512 * nb, 512 * nb + 512)
-                nc.tensor.matmul_mx(
-                    out=sums[nb][:],
-                    lhsT=codes[:, g, :].bitcast(FP8X4),
-                    lhsT_scale=scales[:, g, :],
-                    rhs=w_codes[:, g, cols].bitcast(FP8X4),
-                    rhs_scale=w_scales[:, g, cols],
-                    start=first,
-                    stop=last,
-                )
+        def mx_pass(out, codes, scales, g, nb, first, last):
+            cols = slice(512 * nb, 512 * nb + 512)
+            nc.tensor.matmul_mx(
+                out=out,
+                lhsT=codes[:, g, :].bitcast(FP8X4),
+                lhsT_scale=scales[:, g, :],
+                rhs=w_codes[:, g, cols].bitcast(FP8X4),
+                rhs_scale=w_scales[:, g, cols],
+                start=first,
+                stop=last,
+            )
 
-        def v_scale():
-            for nb in range(3):
-                nc.vector.tensor_tensor(
-                    out=sv[:, 4 * nb:4 * nb + 4, :].rearrange("p k (h d) -> p (k h) d", d=DH),
-                    in0=live["v"][nb][:].rearrange("p (h d) -> p h d", d=DH),
-                    in1=qk_sum[:, 8 * nb:8 * nb + 8].unsqueeze(2).to_broadcast([P, 8, DH]),
-                    op=ALU.mult,
-                )
+        def v_matmul(nb):
+            live["v", nb] = ps_misc.tile([P, 512], F32, name="v", tag="misc")
+            for c in range(3):
+                mx_pass(live["v", nb][:], x_codes, x_scales, c, nb, c == 0, c == 2)
+
+        def v_scale(nb):
+            nc.vector.tensor_tensor(
+                out=sv[:, 4 * nb:4 * nb + 4, :].rearrange("p k (h d) -> p (k h) d", d=DH),
+                in0=live["v", nb][:].rearrange("p (h d) -> p h d", d=DH),
+                in1=qk_sum[:, 8 * nb:8 * nb + 8].unsqueeze(2).to_broadcast([P, 8, DH]),
+                op=ALU.mult,
+            )
 
         def norm_add(ui):
             r_unit = r[:, 2 * ui:2 * ui + 2, :]
@@ -305,7 +339,7 @@ def tile_multiscaleretention_pb_kernel(tc, x, qr, kr, decay, prev_kv, Wv, Wo, ou
 
         def norm_apply(ui):
             g = ui // 2
-            if ("n", g) not in live:
+            if ui % 2 == 0:
                 live["n", g] = keep.tile([P, 4, P], BF16, name="n%d" % g)
             inv = small.tile([P, 4], F32, tag="inv")
             nc.vector.reciprocal(out=inv[:], in_=live["rms", ui][:])
@@ -328,6 +362,11 @@ def tile_multiscaleretention_pb_kernel(tc, x, qr, kr, decay, prev_kv, Wv, Wo, ou
         def n_quantise(g):
             nc.vector.quantize_mx(out=n_codes[:, g, :].bitcast(FP8X4), scales=n_scales[:, g, :], in_=live["ng"][:])
 
+        def o_pass(ps, nb):
+            if ps == 0:
+                live["o", nb] = ps_rot.tile([P, 512], F32, name="o", tag="rot")
+            mx_pass(live["o", nb][:], n_codes, n_scales, ps, nb, ps == 0, ps == 2)
+
         regroup(0)
         for g in range(N_GROUPS):
             i, gg = divmod(g, GROUPS)
@@ -341,103 +380,96 @@ def tile_multiscaleretention_pb_kernel(tc, x, qr, kr, decay, prev_kv, Wv, Wo, ou
                 if step == 3:
                     norm_apply(ui)
             for ps in range(3):
-                step = g - NORM_GROUPS[2 * ps + 1] - 4
-                if step == 0:
+                lag = g - NORM_GROUPS[2 * ps + 1]
+                slow = N_SLACK if ps < 2 else 0
+                if lag == 4 + slow:
                     n_transposes(ps)
-                if step == 1:
+                if lag == 5 + 2 * slow:
                     n_copy()
-                if step == 2:
+                if lag == 6 + 3 * slow:
                     n_quantise(ps)
-            for p in range(N_PIECES):
-                if g == Q_FIRST + Q_STEP * p:
-                    quantise(p)
-                    if p + 1 < N_PIECES:
-                        regroup(p + 1)
+                if lag == 7 and ps == 2:
+                    for nb in range(3):
+                        o_pass(2, nb)
+            if g in QUANT_GROUPS:
+                p = QUANT_GROUPS.index(g)
+                quantise(p)
+                if p + 1 < len(QUANT_GROUPS):
+                    regroup(p + 1)
+
+            for n in range(N_HALVES):
+                step = g - PRODUCT_GROUPS[n]
+                if step == 0:
+                    product(n)
+                    done["half"] = n + 1
+                s_rows = S_ROWS if n < N_HALVES - 2 else S_ROWS // 2
+                if step == 8:
+                    vector_sums(n, s_rows, 32 - s_rows)
 
             if g < A_END:
                 transposes(i, gg)
             if g == 2:
-                nc.vector.tensor_copy(out=q_pad_v[:, :, 0, 0:DK], in_=q_heads)
-                nc.vector.tensor_copy(out=q_pad_v[:, :, 1, DK:P], in_=q_heads)
+                for e in range(2):
+                    nc.vector.tensor_copy(out=q_twice[:, :, e, :], in_=q_sb[:].rearrange("p (h c) -> p h c", c=DK))
+            if g == 1:
+                for j in range(5):
+                    nc.tensor.transpose(q_ps[:, 2 * j:2 * j + 2, :].rearrange("p a c -> p (a c)"), q_t[:, j, :], ident_b[:])
             if 4 <= g < 4 + N_A:
                 q_transposes(g - 4)
-                q_copy(g - 4)
+                q_copies(g - 4)
             if 1 <= i <= N_A:
                 if i < N_A:
-                    if gg < 8:
-                        readout_matmuls(i - 1, 8 * gg, 8)
-                    if gg == 9:
-                        collect(i - 1)
+                    if 1 <= gg < 9:
+                        readout_matmuls(i - 1, 8 * gg - 8, 8)
                     if gg == 10:
-                        back_transposes()
+                        collect(i - 1)
                     if gg == 12:
+                        back_transposes()
+                    if gg == 14:
                         back_copies(i - 1)
                 else:
-                    if gg < 4:
-                        readout_matmuls(i - 1, 16 * gg, 16)
-                    if gg == 5:
+                    if gg < 2:
+                        readout_matmuls(i - 1, 32 * gg, 32)
+                    if gg == 3:
                         collect(i - 1)
-                    if gg == 6:
+                    if gg == 4:
                         back_transposes()
-                    if gg == 7:
+                        for ps in range(2):
+                            for nb in range(3):
+                                o_pass(ps, nb)
+                    if gg == 5:
                         back_copies(i - 1)
+            for n in range(N_HALVES):
+                step = g - PRODUCT_GROUPS[n]
+                s_rows = S_ROWS if n < N_HALVES - 2 else S_ROWS // 2
+                if 3 <= step < 11:
+                    scalar_sums(n, (step - 3) * s_rows // 8, s_rows // 8)
 
-            m, pg = divmod(g, PAIR)
-            if 2 * m < N_HALVES:
-                if pg == 0:
-                    product(2 * m)
-                if pg == 8:
-                    product(2 * m + 1)
-            if m >= 1 and 2 * (m - 1) < N_HALVES:
-                if pg == 4:
-                    vector_sums(2 * (m - 1), 0, 16)
-                if pg == 6:
-                    vector_sums(2 * (m - 1), 16, 16)
-                    vector_sums(2 * (m - 1) + 1, S_ROWS, 32 - S_ROWS)
-            late = g - 11
-            ml, lg = divmod(late, PAIR)
-            if late >= 0 and 2 * ml < N_HALVES and lg < 8:
-                scalar_sums(2 * ml + 1, lg * S_ROWS // 8, S_ROWS // 8)
-
-            if g == 26:
+            if g == QK_GROUP:
                 nc.gpsimd.tensor_tensor(out=qk[:].rearrange("p h c -> p (h c)"), in0=q_sb[:], in1=k_sb[:], op=ALU.mult)
-            if g == 40:
+            if g == QK_GROUP + 12:
                 nc.vector.tensor_reduce(out=qk_sum[:], in_=qk[:], axis=AX.X, op=ALU.add)
-            if g == 28:
-                x_transposes()
-            if g == 29:
-                x_copies()
-            if g == 30:
+            for c in range(3):
+                if g == X_GROUP + 2 * c:
+                    x_transposes(c)
+                if g == X_GROUP + 2 * c + 2:
+                    x_copies(c)
+            if g == X_GROUP + 8:
                 x_quantise()
-            if g == V_GROUP:
-                live["v"] = [
-                    ps_misc.tile([P, 512], F32, name="v0", tag="misc"),
-                    ps_misc.tile([P, 512], F32, name="v1", tag="misc"),
-                    ps_mm.tile([P, 512], F32, name="v2", tag="mm"),
-                ]
-                for c in range(3):
-                    big_passes(live["v"], x_codes, x_scales, c, c == 0, c == 2)
-            if g == V_GROUP + 2:
-                v_scale()
+            for nb in range(3):
+                if g == V_GROUP + 3 * nb:
+                    v_matmul(nb)
+                if g == V_GROUP + 3 * nb + 2:
+                    v_scale(nb)
 
-            if gg == 15 and i + 2 < N_A:
-                load_tile(i + 2)
-            if pg == 8 and m + 3 < len(V_HEADS):
-                load_head(m + 3)
-            pd, pr = divmod(g - Q_FIRST, Q_STEP)
-            if pr == 1 and pd % 3 == 1 and 2 <= pd // 3 + 2 < 6:
-                load_weights(pd // 3 + 2)
-
-            for ps in range(3):
-                if g == max(NORM_GROUPS[2 * ps + 1] + 7, A_END + 1 + 2 * ps):
-                    if ps == 0:
-                        live["o"] = [ps_rot.tile([P, 512], F32, name="o%d" % nb, tag="rot") for nb in range(3)]
-                    big_passes(live["o"], n_codes, n_scales, ps, ps == 0, ps == 2)
+            if gg == 15:
+                done["tile"] = i + 1
+            load_ready()
 
         for nb in range(3):
             o_sb = prod_pool.tile([P, 512], F32, tag="prod")
             if nb == 1:
-                nc.vector.tensor_copy(out=o_sb[:], in_=live["o"][nb][:])
+                nc.vector.tensor_copy(out=o_sb[:], in_=live["o", nb][:])
             else:
-                nc.scalar.copy(out=o_sb[:], in_=live["o"][nb][:])
+                nc.scalar.copy(out=o_sb[:], in_=live["o", nb][:])
             nc.sync.dma_start(out=out_rows[:, 512 * nb:512 * nb + 512], in_=o_sb[:])

@@ -25,17 +25,28 @@ GROUPS = 16
 A_END = N_A * GROUPS
 HALVES = tuple((block, quarter) for block in V_BLOCKS for quarter in range(4))
 N_HALVES = len(HALVES)
-PRODUCT_GROUPS = tuple(11 * n // 2 for n in range(N_HALVES))
+PRODUCT_GROUPS = tuple(23 * n // 4 for n in range(N_HALVES))
 XV_BUFS = 6
 S_ROWS = 16
 
-QUANT_GROUPS = tuple(18 + 19 * p // 2 for p in range(10))
-QK_GROUP = 36
-X_GROUP = 40
-V_GROUP = QUANT_GROUPS[4] + 3
-NORM_GROUPS = (70, 72, 80, 97, 112, 121)
-N_GROUPS = 132
-N_SLACK = 2
+QUANT_GROUPS = tuple(18 + 10 * p for p in range(10))
+QK_GROUP = QUANT_GROUPS[1]
+X_GROUP = QUANT_GROUPS[3] - 10
+X_STEP = 3
+V_STEP = 5
+V_GROUP = QUANT_GROUPS[4] + 2
+ADD_GROUPS = (QUANT_GROUPS[5], QUANT_GROUPS[5], QUANT_GROUPS[7], QUANT_GROUPS[8], 113, 121)
+ROOT_LAG = (2, 2, 2, 2, 1, 1)
+APPLY_GROUPS = (QUANT_GROUPS[6], QUANT_GROUPS[6], QUANT_GROUPS[8], QUANT_GROUPS[9], 116, 124)
+N_LAG = (4, 2, 1)
+NQ_GROUPS = (QUANT_GROUPS[7], 113, 127)
+N_GROUPS = 130
+READ_LAG = 2
+BACK_LAG = 4
+V_PIECES = ()
+S_FIRST = 3
+S_SPAN = 6
+V_SUM = 8
 LOADS = sorted(
     [(GROUPS * i + 4 * k, "tile", 4 * i + k) for i in range(N_A) for k in range(4)]
     + [(PRODUCT_GROUPS[n] + 1, "half", n) for n in range(N_HALVES)]
@@ -262,11 +273,12 @@ def tile_multiscaleretention_pb_kernel(tc, x, qr, kr, decay, prev_kv, Wv, Wo, ou
             for s in range(s0, s1):
                 c, j = divmod(s, 3)
                 at = 2048 * (s - s0)
-                nc.gpsimd.tensor_scalar(
-                    out=live["grp"][:, at:at + 2048].rearrange("p (w t) -> p w t", t=4),
-                    in0=live["raw", 3 * w + c][:, :, 512 * j:512 * j + 512].rearrange("p t w -> p w t"),
-                    scalar1=1.0, scalar2=0.0, op0=ALU.mult, op1=ALU.add,
-                )
+                words = live["grp"][:, at:at + 2048].rearrange("p (w t) -> p w t", t=4)
+                rows = live["raw", 3 * w + c][:, :, 512 * j:512 * j + 512].rearrange("p t w -> p w t")
+                if s in V_PIECES:
+                    nc.vector.tensor_copy(out=words, in_=rows)
+                else:
+                    nc.gpsimd.tensor_scalar(out=words, in0=rows, scalar1=1.0, scalar2=0.0, op0=ALU.mult, op1=ALU.add)
             done["weights"] = 3 * w + s1 // 3
 
         def quantise(p):
@@ -372,25 +384,25 @@ def tile_multiscaleretention_pb_kernel(tc, x, qr, kr, decay, prev_kv, Wv, Wo, ou
             i, gg = divmod(g, GROUPS)
 
             for ui in range(6):
-                step = g - NORM_GROUPS[ui]
-                if step == 0:
+                if g == ADD_GROUPS[ui]:
                     norm_add(ui)
-                if step == 1:
+                if g == ADD_GROUPS[ui] + ROOT_LAG[ui]:
                     norm_root(ui)
-                if step == 3:
+                if g == APPLY_GROUPS[ui]:
                     norm_apply(ui)
             for ps in range(3):
-                lag = g - NORM_GROUPS[2 * ps + 1]
-                slow = N_SLACK if ps < 2 else 0
-                if lag == 4 + slow:
+                lag = g - APPLY_GROUPS[2 * ps + 1]
+                if lag == N_LAG[ps]:
                     n_transposes(ps)
-                if lag == 5 + 2 * slow:
+                if lag == N_LAG[ps] + (2 if ps < 2 else 1):
                     n_copy()
-                if lag == 6 + 3 * slow:
+                if g == NQ_GROUPS[ps]:
                     n_quantise(ps)
-                if lag == 7 and ps == 2:
+                if ps == 2 and g == NQ_GROUPS[ps] + 1:
                     for nb in range(3):
                         o_pass(2, nb)
+            if g == QUANT_GROUPS[3]:
+                x_quantise()
             if g in QUANT_GROUPS:
                 p = QUANT_GROUPS.index(g)
                 quantise(p)
@@ -403,7 +415,7 @@ def tile_multiscaleretention_pb_kernel(tc, x, qr, kr, decay, prev_kv, Wv, Wo, ou
                     product(n)
                     done["half"] = n + 1
                 s_rows = S_ROWS if n < N_HALVES - 2 else S_ROWS // 2
-                if step == 8:
+                if step == V_SUM:
                     vector_sums(n, s_rows, 32 - s_rows)
 
             if g < A_END:
@@ -419,13 +431,13 @@ def tile_multiscaleretention_pb_kernel(tc, x, qr, kr, decay, prev_kv, Wv, Wo, ou
                 q_copies(g - 4)
             if 1 <= i <= N_A:
                 if i < N_A:
-                    if 1 <= gg < 9:
-                        readout_matmuls(i - 1, 8 * gg - 8, 8)
-                    if gg == 10:
+                    if 0 <= gg - READ_LAG < 8:
+                        readout_matmuls(i - 1, 8 * (gg - READ_LAG), 8)
+                    if gg == READ_LAG + 8:
                         collect(i - 1)
-                    if gg == 12:
+                    if gg == READ_LAG + 8 + BACK_LAG:
                         back_transposes()
-                    if gg == 14:
+                    if gg == READ_LAG + 9 + BACK_LAG:
                         back_copies(i - 1)
                 else:
                     if gg < 2:
@@ -442,24 +454,29 @@ def tile_multiscaleretention_pb_kernel(tc, x, qr, kr, decay, prev_kv, Wv, Wo, ou
             for n in range(N_HALVES):
                 step = g - PRODUCT_GROUPS[n]
                 s_rows = S_ROWS if n < N_HALVES - 2 else S_ROWS // 2
-                if 3 <= step < 11:
-                    scalar_sums(n, (step - 3) * s_rows // 8, s_rows // 8)
+                k = step - S_FIRST
+                if 0 <= k < S_SPAN:
+                    d0, d1 = k * s_rows // S_SPAN, (k + 1) * s_rows // S_SPAN
+                    scalar_sums(n, d0, d1 - d0)
 
-            if g == QK_GROUP:
-                nc.gpsimd.tensor_tensor(out=qk[:].rearrange("p h c -> p (h c)"), in0=q_sb[:], in1=k_sb[:], op=ALU.mult)
-            if g == QK_GROUP + 12:
+            for part in range(2):
+                if g == QUANT_GROUPS[1 + part]:
+                    c0 = part * (E // 2)
+                    nc.gpsimd.tensor_tensor(
+                        out=qk[:].rearrange("p h c -> p (h c)")[:, c0:c0 + E // 2],
+                        in0=q_sb[:, c0:c0 + E // 2], in1=k_sb[:, c0:c0 + E // 2], op=ALU.mult,
+                    )
+            if g == QUANT_GROUPS[4]:
                 nc.vector.tensor_reduce(out=qk_sum[:], in_=qk[:], axis=AX.X, op=ALU.add)
             for c in range(3):
-                if g == X_GROUP + 2 * c:
+                if g == X_GROUP + X_STEP * c:
                     x_transposes(c)
-                if g == X_GROUP + 2 * c + 2:
+                if g == X_GROUP + X_STEP * c + 2:
                     x_copies(c)
-            if g == X_GROUP + 8:
-                x_quantise()
             for nb in range(3):
-                if g == V_GROUP + 3 * nb:
+                if g == V_GROUP + V_STEP * nb:
                     v_matmul(nb)
-                if g == V_GROUP + 3 * nb + 2:
+                if g == V_GROUP + V_STEP * nb + V_STEP - 1:
                     v_scale(nb)
 
             if gg == 15:

@@ -27,7 +27,7 @@ HALVES = tuple((block, quarter) for block in V_BLOCKS for quarter in range(4))
 N_HALVES = len(HALVES)
 PRODUCT_GROUPS = tuple(23 * n // 4 for n in range(N_HALVES))
 XV_BUFS = 6
-S_ROWS = 16
+S_ROWS = 12
 
 QUANT_GROUPS = tuple(18 + 10 * p for p in range(10))
 QK_GROUP = QUANT_GROUPS[1]

@@ -27,11 +27,16 @@ HALVES = tuple((block, quarter) for block in V_BLOCKS for quarter in range(4))
 N_HALVES = len(HALVES)
 PRODUCT_GROUPS = tuple(23 * n // 4 for n in range(N_HALVES))
 XV_BUFS = 6
+EARLY = 8
+S_EARLY = 16
 S_ROWS = 12
 
 QUANT_GROUPS = tuple(18 + 10 * p for p in range(10))
-QK_GROUP = QUANT_GROUPS[1]
-X_GROUP = QUANT_GROUPS[3] - 10
+X_Q = 3
+X_GROUP = QUANT_GROUPS[X_Q] - 10
+QK_Q = 2
+W_LEAD = 9
+H_LEAD = 0
 X_STEP = 3
 V_STEP = 5
 V_GROUP = QUANT_GROUPS[4] + 2
@@ -49,9 +54,9 @@ S_SPAN = 6
 V_SUM = 8
 LOADS = sorted(
     [(GROUPS * i + 4 * k, "tile", 4 * i + k) for i in range(N_A) for k in range(4)]
-    + [(PRODUCT_GROUPS[n] + 1, "half", n) for n in range(N_HALVES)]
-    + [(QUANT_GROUPS[p] - 9, "weights", c) for c, p in enumerate((0, 1, 3, 5, 6, 8))]
-    + [(QK_GROUP - 6, "k", 0), (X_GROUP - 6, "x", 0)]
+    + [(PRODUCT_GROUPS[n] + 1 - H_LEAD, "half", n) for n in range(N_HALVES)]
+    + [(QUANT_GROUPS[p] - W_LEAD, "weights", c) for c, p in enumerate((0, 1, 3, 5, 6, 8))]
+    + [(QUANT_GROUPS[QK_Q] - 6, "k", 0), (X_GROUP - 6, "x", 0)]
 )
 
 
@@ -194,8 +199,8 @@ def tile_multiscaleretention_pb_kernel(tc, x, qr, kr, decay, prev_kv, Wv, Wo, ou
                 s = 4 * g + k
                 nc.tensor.transpose(up[:, k, :], live["xp", i][:, s * P:(s + 1) * P], perm[:])
             nc.scalar.copy(
-                out=z_words[:, :, 4 * g:4 * g + 4].rearrange("p (v i) k -> p v k i", i=2),
-                in_=up[:].bitcast(F32).rearrange("p k (v i) -> p v k i", i=2),
+                out=z_words[:, :, 4 * g:4 * g + 4],
+                in_=up[:].bitcast(F32).rearrange("p k j -> p j k"),
             )
 
         def readout_matmuls(i, j0, n):
@@ -401,7 +406,7 @@ def tile_multiscaleretention_pb_kernel(tc, x, qr, kr, decay, prev_kv, Wv, Wo, ou
                 if ps == 2 and g == NQ_GROUPS[ps] + 1:
                     for nb in range(3):
                         o_pass(2, nb)
-            if g == QUANT_GROUPS[3]:
+            if g == QUANT_GROUPS[X_Q]:
                 x_quantise()
             if g in QUANT_GROUPS:
                 p = QUANT_GROUPS.index(g)
@@ -414,7 +419,7 @@ def tile_multiscaleretention_pb_kernel(tc, x, qr, kr, decay, prev_kv, Wv, Wo, ou
                 if step == 0:
                     product(n)
                     done["half"] = n + 1
-                s_rows = S_ROWS if n < N_HALVES - 2 else S_ROWS // 2
+                s_rows = S_EARLY if n < EARLY else S_ROWS if n < N_HALVES - 2 else S_ROWS // 2
                 if step == V_SUM:
                     vector_sums(n, s_rows, 32 - s_rows)
 
@@ -453,14 +458,14 @@ def tile_multiscaleretention_pb_kernel(tc, x, qr, kr, decay, prev_kv, Wv, Wo, ou
                         back_copies(i - 1)
             for n in range(N_HALVES):
                 step = g - PRODUCT_GROUPS[n]
-                s_rows = S_ROWS if n < N_HALVES - 2 else S_ROWS // 2
+                s_rows = S_EARLY if n < EARLY else S_ROWS if n < N_HALVES - 2 else S_ROWS // 2
                 k = step - S_FIRST
                 if 0 <= k < S_SPAN:
                     d0, d1 = k * s_rows // S_SPAN, (k + 1) * s_rows // S_SPAN
                     scalar_sums(n, d0, d1 - d0)
 
             for part in range(2):
-                if g == QUANT_GROUPS[1 + part]:
+                if g == QUANT_GROUPS[QK_Q + part]:
                     c0 = part * (E // 2)
                     nc.gpsimd.tensor_tensor(
                         out=qk[:].rearrange("p h c -> p (h c)")[:, c0:c0 + E // 2],

@@ -103,13 +103,8 @@ def tile_multiscaleretention_pb_kernel(tc, x, qr, kr, decay, prev_kv, Wv, Wo, ou
         def load_weights(c):
             raw = raw_pool.tile([P, 4, V], BF16, name="raw", tag="raw")
             live["raw", c] = raw
-            if c < 3:
-                for u in range(2):
-                    rows = Wv[512 * c + 256 * u:512 * c + 256 * u + 256, :]
-                    nc.sync.dma_start(out=raw[:, 2 * u:2 * u + 2, :], in_=rows.rearrange("(q e) c -> q e c", e=2))
-            else:
-                rows = Wo[512 * (c - 3):512 * (c - 3) + 512, :]
-                nc.sync.dma_start(out=raw[:], in_=rows.rearrange("(t p) c -> p t c", t=4))
+            rows = (Wv, Wo)[c // 3][512 * (c % 3):512 * (c % 3) + 512, :]
+            nc.sync.dma_start(out=raw[:], in_=rows.rearrange("(p t) c -> p t c", t=4))
 
         q_sb = keep.tile([P, E], BF16)
         nc.sync.dma_start(out=q_sb[:], in_=q_rows)
@@ -194,21 +189,21 @@ def tile_multiscaleretention_pb_kernel(tc, x, qr, kr, decay, prev_kv, Wv, Wo, ou
             if g == 0:
                 live["z", i] = z_pool.tile([P, 64 * P], BF16, name="z", tag="z")
             z_words = live["z", i][:].bitcast(F32).rearrange("p (j s) -> p j s", s=64)
-            up = ps_rot.tile([P, 4, P], BF16, tag="rot")
+            up = ps_rot.tile([P, 64, 4, 2], BF16, tag="rot")
             for k in range(4):
                 s = 4 * g + k
-                nc.tensor.transpose(up[:, k, :], live["xp", i][:, s * P:(s + 1) * P], perm[:])
+                nc.tensor.transpose(up[:, :, k, :], live["xp", i][:, s * P:(s + 1) * P], perm[:])
             nc.scalar.copy(
                 out=z_words[:, :, 4 * g:4 * g + 4],
-                in_=up[:].bitcast(F32).rearrange("p k j -> p j k"),
+                in_=up[:].rearrange("p j k b -> p (j k b)").bitcast(F32).rearrange("p (j k) -> p j k", k=4),
             )
 
         def readout_matmuls(i, j0, n):
             if j0 == 0:
-                live["mm"] = ps_mm.tile([P, 64, 8], F32, name="mm", tag="mm")
+                live["mm"] = ps_mm.tile([P, 8, 64], F32, name="mm", tag="mm")
             for j in range(j0, j0 + n):
                 nc.tensor.matmul(
-                    out=live["mm"][:, j, :], lhsT=live["z", i][:, j * P:(j + 1) * P],
+                    out=live["mm"][:, :, j], lhsT=live["z", i][:, j * P:(j + 1) * P],
                     rhs=q_mov[:, i, :, 2 * j:2 * j + 2, :].rearrange("p e b a -> p e (b a)"),
                     start=True, stop=True,
                 )
@@ -220,7 +215,7 @@ def tile_multiscaleretention_pb_kernel(tc, x, qr, kr, decay, prev_kv, Wv, Wo, ou
                 h = 2 * A_BLOCKS[i] + a
                 nc.scalar.activation(
                     out=live["ct"][rows, :, :].rearrange("p e (b2 j) -> p e b2 j", b2=2),
-                    in_=live["mm"][rows, :, :].rearrange("p j (e b2 a) -> p a e b2 j", b2=2, a=2)[:, a],
+                    in_=live["mm"][rows, :, :].rearrange("p (e b2 a) j -> p a e b2 j", b2=2, a=2)[:, a],
                     func=ACT.Copy, scale=dec_f[rows, h:h + 1],
                 )
 
@@ -301,8 +296,7 @@ def tile_multiscaleretention_pb_kernel(tc, x, qr, kr, decay, prev_kv, Wv, Wo, ou
             x_words = x_sb[:].bitcast(F32)
             live["xt"] = ps_misc.tile([P, 2, P], F32, name="xt", tag="misc")
             for u in range(2):
-                w0 = 256 * g + 128 * u
-                nc.tensor.transpose(live["xt"][:, u, :], x_words[:, w0:w0 + 128], ident_f[:])
+                nc.tensor.transpose(live["xt"][:, u, :], x_words[:, 256 * g + u:256 * (g + 1):2], ident_f[:])
 
         def x_copies(g):
             nc.vector.tensor_copy(
@@ -370,7 +364,7 @@ def tile_multiscaleretention_pb_kernel(tc, x, qr, kr, decay, prev_kv, Wv, Wo, ou
         def n_transposes(g):
             live["nt"] = ps_misc.tile([P, 4, P], BF16, name="nt", tag="misc")
             for t in range(4):
-                nc.tensor.transpose(live["nt"][:, t, :], live["n", g][:, t, :], ident_b[:])
+                nc.tensor.transpose(live["nt"][:, t, :], live["n", g][:].rearrange("p k c -> p (k c)")[:, t::4], ident_b[:])
 
         def n_copy():
             live["ng"] = small.tile([P, 512], BF16, name="ng", tag="ng", align_bytes=64)

@@ -22,12 +22,15 @@ A_BLOCKS = (0, 2, 4, 5, 7, 9, 10)
 V_BLOCKS = (1, 3, 6, 8, 11)
 N_A = len(A_BLOCKS)
 GROUPS = 16
+BANK = 2
 A_END = N_A * GROUPS
 HALVES = tuple((block, quarter) for block in V_BLOCKS for quarter in range(4))
 N_HALVES = len(HALVES)
 PRODUCT_GROUPS = tuple(23 * n // 4 for n in range(N_HALVES))
 XV_BUFS = 6
-EARLY = 8
+EARLY = 10
+SPLIT = 1
+FIRST_NEED = 1
 S_EARLY = 16
 S_ROWS = 12
 
@@ -47,14 +50,16 @@ N_LAG = (4, 2, 1)
 NQ_GROUPS = (QUANT_GROUPS[7], 113, 127)
 N_GROUPS = 130
 READ_LAG = 2
+FIRST_ADDED = 6
+ADDED = ((0, 2), (2, 2), (4, 2), (6, 2), (8, 2), (11, 1))
 BACK_LAG = 4
 V_PIECES = ()
 S_FIRST = 3
 S_SPAN = 6
-V_SUM = 8
+V_SUM = 6
 LOADS = sorted(
     [(GROUPS * i + 4 * k, "tile", 4 * i + k) for i in range(N_A) for k in range(4)]
-    + [(PRODUCT_GROUPS[n] + 1 - H_LEAD, "half", n) for n in range(N_HALVES)]
+    + [(PRODUCT_GROUPS[n] + (1 if n else FIRST_NEED), "half", n) for n in range(N_HALVES)]
     + [(QUANT_GROUPS[p] - W_LEAD, "weights", c) for c, p in enumerate((0, 1, 3, 5, 6, 8))]
     + [(QUANT_GROUPS[QK_Q] - 6, "k", 0), (X_GROUP - 6, "x", 0)]
 )
@@ -94,11 +99,16 @@ def tile_multiscaleretention_pb_kernel(tc, x, qr, kr, decay, prev_kv, Wv, Wo, ou
             c0 = 2 * A_BLOCKS[i] * HEAD + k * w
             nc.sync.dma_start(out=live["xp", i][:, k * w:(k + 1) * w], in_=state[:, c0:c0 + w])
 
+        def pieces(n):
+            return ((0, 16), (16, 16)) if n < SPLIT else ((0, 32),)
+
         def load_half(n):
             block, quarter = HALVES[n]
             c0 = 2 * block * HEAD + quarter * (HEAD // 2)
             live["xv", n] = xv_pool.tile([P, HEAD // 2], BF16, name="xv", tag="xv")
-            nc.sync.dma_start(out=live["xv", n][:], in_=state[:, c0:c0 + HEAD // 2])
+            for p0, w in pieces(n):
+                w0, w1 = p0 * DK, (p0 + w) * DK
+                nc.sync.dma_start(out=live["xv", n][:, w0:w1], in_=state[:, c0 + w0:c0 + w1])
 
         def load_weights(c):
             raw = raw_pool.tile([P, 4, V], BF16, name="raw", tag="raw")
@@ -145,7 +155,7 @@ def tile_multiscaleretention_pb_kernel(tc, x, qr, kr, decay, prev_kv, Wv, Wo, ou
         ident_b = keep.tile([P, P], BF16)
         make_identity(nc, ident_b[:])
         perm = keep.tile([P, P], BF16)
-        nc.vector.tensor_copy(
+        nc.gpsimd.tensor_copy(
             out=perm[:].rearrange("p (j b2) -> p j b2", b2=2), in_=ident_b[:].rearrange("p (b2 j) -> p j b2", b2=2)
         )
         ident_f = keep.tile([P, P], F32)
@@ -189,14 +199,17 @@ def tile_multiscaleretention_pb_kernel(tc, x, qr, kr, decay, prev_kv, Wv, Wo, ou
             if g == 0:
                 live["z", i] = z_pool.tile([P, 64 * P], BF16, name="z", tag="z")
             z_words = live["z", i][:].bitcast(F32).rearrange("p (j s) -> p j s", s=64)
-            up = ps_rot.tile([P, 64, 4, 2], BF16, tag="rot")
+            if g % BANK == 0:
+                live["up"] = ps_rot.tile([P, 64, 4 * BANK, 2], BF16, name="up", tag="rot")
+            up = live["up"]
             for k in range(4):
                 s = 4 * g + k
-                nc.tensor.transpose(up[:, :, k, :], live["xp", i][:, s * P:(s + 1) * P], perm[:])
-            nc.scalar.copy(
-                out=z_words[:, :, 4 * g:4 * g + 4],
-                in_=up[:].rearrange("p j k b -> p (j k b)").bitcast(F32).rearrange("p (j k) -> p j k", k=4),
-            )
+                nc.tensor.transpose(up[:, :, s % (4 * BANK), :], live["xp", i][:, s * P:(s + 1) * P], perm[:])
+            if g % BANK == BANK - 1:
+                nc.scalar.copy(
+                    out=z_words[:, :, 4 * (g + 1 - BANK):4 * (g + 1)],
+                    in_=up[:].rearrange("p j k b -> p (j k b)").bitcast(F32).rearrange("p (j k) -> p j k", k=4 * BANK),
+                )
 
         def readout_matmuls(i, j0, n):
             if j0 == 0:
@@ -232,6 +245,16 @@ def tile_multiscaleretention_pb_kernel(tc, x, qr, kr, decay, prev_kv, Wv, Wo, ou
                     in_=live["rb"][rows, :, :].rearrange("p e (d b2) -> p b2 d e", b2=2)[:, b2],
                 )
 
+        def back_adds(i):
+            for b2 in range(2):
+                rows = slice(64 * b2, 64 * b2 + 64)
+                nc.vector.tensor_tensor(
+                    out=r[rows, A_BLOCKS[i], :].rearrange("p (d e) -> p d e", e=2),
+                    in0=live["rb"][rows, :, :].rearrange("p e (d b2) -> p b2 d e", b2=2)[:, b2],
+                    in1=sv[rows, A_BLOCKS[i], :].rearrange("p (d e) -> p d e", e=2),
+                    op=ALU.add,
+                )
+
         def product(n):
             block, quarter = HALVES[n]
             h = 2 * block + quarter // 2
@@ -240,14 +263,15 @@ def tile_multiscaleretention_pb_kernel(tc, x, qr, kr, decay, prev_kv, Wv, Wo, ou
             else:
                 q_row = q_ps[:, 2 * V_BLOCKS.index(block) + quarter // 2, :]
             live["prod", n] = prod_pool.tile([P, 32, DK], F32, name="prod", tag="prod")
-            nc.vector.scalar_tensor_tensor(
-                out=live["prod", n][:],
-                in0=live["xv", n][:].rearrange("p (d c) -> p d c", c=DK),
-                scalar=dec_f[:, h:h + 1],
-                in1=q_row.unsqueeze(1).to_broadcast([P, 32, DK]),
-                op0=ALU.mult,
-                op1=ALU.mult,
-            )
+            for p0, w in pieces(n):
+                nc.vector.scalar_tensor_tensor(
+                    out=live["prod", n][:, p0:p0 + w, :],
+                    in0=live["xv", n][:].rearrange("p (d c) -> p d c", c=DK)[:, p0:p0 + w, :],
+                    scalar=dec_f[:, h:h + 1],
+                    in1=q_row.unsqueeze(1).to_broadcast([P, w, DK]),
+                    op0=ALU.mult,
+                    op1=ALU.mult,
+                )
 
         def scalar_sums(n, d0, rows):
             block, quarter = HALVES[n]
@@ -336,8 +360,9 @@ def tile_multiscaleretention_pb_kernel(tc, x, qr, kr, decay, prev_kv, Wv, Wo, ou
             )
 
         def norm_add(ui):
-            r_unit = r[:, 2 * ui:2 * ui + 2, :]
-            nc.vector.tensor_tensor(out=r_unit, in0=r_unit, in1=sv[:, 2 * ui:2 * ui + 2, :], op=ALU.add)
+            b0, nb = ADDED[ui]
+            blocks = r[:, b0:b0 + nb, :]
+            nc.vector.tensor_tensor(out=blocks, in0=blocks, in1=sv[:, b0:b0 + nb, :], op=ALU.add)
 
         def norm_root(ui):
             ss = small.tile([P, 4], F32, name="ss", tag="ss")
@@ -437,7 +462,10 @@ def tile_multiscaleretention_pb_kernel(tc, x, qr, kr, decay, prev_kv, Wv, Wo, ou
                     if gg == READ_LAG + 8 + BACK_LAG:
                         back_transposes()
                     if gg == READ_LAG + 9 + BACK_LAG:
-                        back_copies(i - 1)
+                        if i - 1 < FIRST_ADDED:
+                            back_copies(i - 1)
+                        else:
+                            back_adds(i - 1)
                 else:
                     if gg < 2:
                         readout_matmuls(i - 1, 32 * gg, 32)
@@ -449,7 +477,7 @@ def tile_multiscaleretention_pb_kernel(tc, x, qr, kr, decay, prev_kv, Wv, Wo, ou
                             for nb in range(3):
                                 o_pass(ps, nb)
                     if gg == 5:
-                        back_copies(i - 1)
+                        back_adds(i - 1)
             for n in range(N_HALVES):
                 step = g - PRODUCT_GROUPS[n]
                 s_rows = S_EARLY if n < EARLY else S_ROWS if n < N_HALVES - 2 else S_ROWS // 2

from contextlib import ExitStack

import concourse.mybir as mybir
from concourse.masks import make_identity

F32 = mybir.dt.float32
BF16 = mybir.dt.bfloat16
U8 = mybir.dt.uint8
U32 = mybir.dt.uint32
FP8X4 = mybir.dt.float8_e4m3fn_x4
ALU = mybir.AluOpType
ACT = mybir.ActivationFunctionType
AX = mybir.AxisListType

P = 128
H, DK, DH, E, V = 24, 64, 64, 1536, 1536
HEAD = DH * DK
EPS = 1e-6
FLOPS = 2 * 2 * P * E * V + 4 * P * H * DH * DK

A_BLOCKS = (0, 2, 4, 5, 7, 9, 10)
V_BLOCKS = (1, 3, 6, 8, 11)
N_A = len(A_BLOCKS)
GROUPS = 16
BANK = 2
A_END = N_A * GROUPS
HALVES = tuple((block, quarter) for block in V_BLOCKS for quarter in range(4))
N_HALVES = len(HALVES)
PRODUCT_GROUPS = tuple(23 * n // 4 for n in range(N_HALVES))
XV_BUFS = 6
EARLY = 10
SPLIT = 1
FIRST_NEED = 1
S_EARLY = 16
S_ROWS = 12

QUANT_GROUPS = tuple(18 + 10 * p for p in range(10))
X_Q = 3
X_GROUP = QUANT_GROUPS[X_Q] - 10
QK_Q = 2
W_LEAD = 9
H_LEAD = 0
X_STEP = 3
V_STEP = 5
V_GROUP = QUANT_GROUPS[4] + 2
ADD_GROUPS = (QUANT_GROUPS[5], QUANT_GROUPS[5], QUANT_GROUPS[7], QUANT_GROUPS[8], 113, 121)
ROOT_LAG = (2, 2, 2, 2, 1, 1)
APPLY_GROUPS = (QUANT_GROUPS[6], QUANT_GROUPS[6], QUANT_GROUPS[8], QUANT_GROUPS[9], 116, 124)
N_LAG = (4, 2, 1)
NQ_GROUPS = (QUANT_GROUPS[7], 113, 127)
N_GROUPS = 130
READ_LAG = 2
FIRST_ADDED = 6
ADDED = ((0, 2), (2, 2), (4, 2), (6, 2), (8, 2), (11, 1))
BACK_LAG = 4
V_PIECES = ()
S_FIRST = 3
S_SPAN = 6
V_SUM = 6
LOADS = sorted(
    [(GROUPS * i + 4 * k, "tile", 4 * i + k) for i in range(N_A) for k in range(4)]
    + [(PRODUCT_GROUPS[n] + (1 if n else FIRST_NEED), "half", n) for n in range(N_HALVES)]
    + [(QUANT_GROUPS[p] - W_LEAD, "weights", c) for c, p in enumerate((0, 1, 3, 5, 6, 8))]
    + [(QUANT_GROUPS[QK_Q] - 6, "k", 0), (X_GROUP - 6, "x", 0)]
)


def tile_multiscaleretention_pb_kernel(tc, x, qr, kr, decay, prev_kv, Wv, Wo, out):
    nc = tc.nc
    x_rows = x.rearrange("b t e -> b (t e)")
    q_rows = qr.rearrange("b h t c -> b (h t c)")
    k_rows = kr.rearrange("b h t c -> b (h t c)")
    state = prev_kv.rearrange("b h d c -> b (h d c)")
    out_rows = out.rearrange("b t e -> b (t e)")

    with ExitStack() as ctx:
        keep = ctx.enter_context(tc.tile_pool(name="keep", bufs=1))
        small = ctx.enter_context(tc.tile_pool(name="small", bufs=2))
        raw_pool = ctx.enter_context(tc.tile_pool(name="raw_pool", bufs=2))
        grp_pool = ctx.enter_context(tc.tile_pool(name="grp_pool", bufs=1))
        xp_pool = ctx.enter_context(tc.tile_pool(name="xp_pool", bufs=2))
        z_pool = ctx.enter_context(tc.tile_pool(name="z_pool", bufs=2))
        xv_pool = ctx.enter_context(tc.tile_pool(name="xv_pool", bufs=XV_BUFS))
        prod_pool = ctx.enter_context(tc.tile_pool(name="prod_pool", bufs=4))
        ct_pool = ctx.enter_context(tc.tile_pool(name="ct_pool", bufs=1))
        ps_rot = ctx.enter_context(tc.psum_pool(name="ps_rot", bufs=4))
        ps_mm = ctx.enter_context(tc.psum_pool(name="ps_mm", bufs=1))
        ps_misc = ctx.enter_context(tc.psum_pool(name="ps_misc", bufs=2))
        ps_q = ctx.enter_context(tc.psum_pool(name="ps_q", bufs=1))
        ctx.enter_context(tc.manual_schedule())

        live = {}

        def load_tile(part):
            i, k = divmod(part, 4)
            if k == 0:
                live["xp", i] = xp_pool.tile([P, 2 * HEAD], BF16, name="xp", tag="xp")
            w = HEAD // 2
            c0 = 2 * A_BLOCKS[i] * HEAD + k * w
            nc.sync.dma_start(out=live["xp", i][:, k * w:(k + 1) * w], in_=state[:, c0:c0 + w])

        def pieces(n):
            return ((0, 16), (16, 16)) if n < SPLIT else ((0, 32),)

        def load_half(n):
            block, quarter = HALVES[n]
            c0 = 2 * block * HEAD + quarter * (HEAD // 2)
            live["xv", n] = xv_pool.tile([P, HEAD // 2], BF16, name="xv", tag="xv")
            for p0, w in pieces(n):
                w0, w1 = p0 * DK, (p0 + w) * DK
                nc.sync.dma_start(out=live["xv", n][:, w0:w1], in_=state[:, c0 + w0:c0 + w1])

        def load_weights(c):
            raw = raw_pool.tile([P, 4, V], BF16, name="raw", tag="raw")
            live["raw", c] = raw
            rows = (Wv, Wo)[c // 3][512 * (c % 3):512 * (c % 3) + 512, :]
            nc.sync.dma_start(out=raw[:], in_=rows.rearrange("(p t) c -> p t c", t=4))

        q_sb = keep.tile([P, E], BF16)
        nc.sync.dma_start(out=q_sb[:], in_=q_rows)
        dec_b = keep.tile([P, H], BF16)
        nc.sync.dma_start(out=dec_b[:], in_=decay.partition_broadcast(P))
        k_sb = keep.tile([P, E], BF16)
        x_sb = keep.tile([P, E], BF16)
        queue = list(LOADS)
        done = {"tile": 0, "half": 0, "weights": 0}

        def load_ready():
            while queue:
                kind, i = queue[0][1:]
                if kind == "tile":
                    if i // 4 - 2 >= done["tile"]:
                        return
                    load_tile(i)
                elif kind == "half":
                    if i - XV_BUFS >= done["half"]:
                        return
                    load_half(i)
                elif kind == "weights":
                    if i - 2 >= done["weights"]:
                        return
                    load_weights(i)
                elif kind == "k":
                    nc.sync.dma_start(out=k_sb[:], in_=k_rows)
                else:
                    nc.sync.dma_start(out=x_sb[:], in_=x_rows)
                queue.remove(queue[0])

        load_ready()

        eps_t = keep.tile([P, 1], F32)
        nc.vector.memset(eps_t[:], EPS)
        warm = keep.tile([P, 1], F32)
        nc.scalar.activation(out=warm[:], in_=eps_t[:], func=ACT.Sqrt)
        ident_b = keep.tile([P, P], BF16)
        make_identity(nc, ident_b[:])
        perm = keep.tile([P, P], BF16)
        nc.gpsimd.tensor_copy(
            out=perm[:].rearrange("p (j b2) -> p j b2", b2=2), in_=ident_b[:].rearrange("p (b2 j) -> p j b2", b2=2)
        )
        ident_f = keep.tile([P, P], F32)
        make_identity(nc, ident_f[:])
        q_mov = keep.tile([P, N_A, 2, P, 2], BF16)
        nc.gpsimd.memset(q_mov[:].rearrange("p i e b a -> p (i e b a)").bitcast(U32), 0)

        q_up = ps_rot.tile([P, 5, P], BF16, tag="rot")
        for j in range(5):
            nc.tensor.transpose(q_up[:, j, :], q_sb[:, V_BLOCKS[j] * P:V_BLOCKS[j] * P + P], ident_b[:])
        q_t = keep.tile([P, 5, P], BF16)
        nc.scalar.copy(out=q_t[:], in_=q_up[:])
        dec_f = keep.tile([P, H], F32)
        nc.vector.tensor_copy(out=dec_f[:], in_=dec_b[:])
        q_ps = ps_q.tile([P, 2 * len(V_BLOCKS), DK], BF16, tag="q")
        q_twice = keep.tile([P, H, 2, DK], BF16)
        qk = keep.tile([P, H, DK], F32)

        qk_sum = keep.tile([P, H], F32)
        x_codes = keep.tile([P, 3, P], U32, align_bytes=64)
        x_scales = keep.tile([P, 3, P], U8, align_bytes=64)
        w_codes = keep.tile([P, 3, V], U32, align_bytes=64)
        w_scales = keep.tile([P, 3, V], U8, align_bytes=64)
        sv = keep.tile([P, 12, P], F32)
        r = keep.tile([P, 12, P], F32)
        n_codes = keep.tile([P, 3, P], U32, align_bytes=64)
        n_scales = keep.tile([P, 3, P], U8, align_bytes=64)

        def q_transposes(i):
            block = A_BLOCKS[i]
            live["qm"] = ps_rot.tile([P, 2, P], BF16, name="qm", tag="rot")
            for a in range(2):
                nc.tensor.transpose(live["qm"][:, a, :], q_twice[:, 2 * block + a].rearrange("p e c -> p (e c)"), perm[:])

        def q_copies(i):
            for e in range(2):
                rows = slice(64 * e, 64 * e + 64)
                nc.scalar.copy(out=q_mov[rows, i, e], in_=live["qm"][rows, :, :].rearrange("p a b -> p b a"))

        def transposes(i, g):
            if g == 0:
                live["z", i] = z_pool.tile([P, 64 * P], BF16, name="z", tag="z")
            z_words = live["z", i][:].bitcast(F32).rearrange("p (j s) -> p j s", s=64)
            if g % BANK == 0:
                live["up"] = ps_rot.tile([P, 64, 4 * BANK, 2], BF16, name="up", tag="rot")
            up = live["up"]
            for k in range(4):
                s = 4 * g + k
                nc.tensor.transpose(up[:, :, s % (4 * BANK), :], live["xp", i][:, s * P:(s + 1) * P], perm[:])
            if g % BANK == BANK - 1:
                nc.scalar.copy(
                    out=z_words[:, :, 4 * (g + 1 - BANK):4 * (g + 1)],
                    in_=up[:].rearrange("p j k b -> p (j k b)").bitcast(F32).rearrange("p (j k) -> p j k", k=4 * BANK),
                )

        def readout_matmuls(i, j0, n):
            if j0 == 0:
                live["mm"] = ps_mm.tile([P, 8, 64], F32, name="mm", tag="mm")
            for j in range(j0, j0 + n):
                nc.tensor.matmul(
                    out=live["mm"][:, :, j], lhsT=live["z", i][:, j * P:(j + 1) * P],
                    rhs=q_mov[:, i, :, 2 * j:2 * j + 2, :].rearrange("p e b a -> p e (b a)"),
                    start=True, stop=True,
                )

        def collect(i):
            live["ct"] = ct_pool.tile([P, 2, P], F32, name="ct", tag="ct")
            for a in range(2):
                rows = slice(64 * a, 64 * a + 64)
                h = 2 * A_BLOCKS[i] + a
                nc.scalar.activation(
                    out=live["ct"][rows, :, :].rearrange("p e (b2 j) -> p e b2 j", b2=2),
                    in_=live["mm"][rows, :, :].rearrange("p (e b2 a) j -> p a e b2 j", b2=2, a=2)[:, a],
                    func=ACT.Copy, scale=dec_f[rows, h:h + 1],
                )

        def back_transposes():
            live["rb"] = ps_misc.tile([P, 2, P], F32, name="rb", tag="misc")
            for e in range(2):
                nc.tensor.transpose(live["rb"][:, e, :], live["ct"][:, e, :], ident_f[:])

        def back_copies(i):
            for b2 in range(2):
                rows = slice(64 * b2, 64 * b2 + 64)
                nc.scalar.copy(
                    out=r[rows, A_BLOCKS[i], :].rearrange("p (d e) -> p d e", e=2),
                    in_=live["rb"][rows, :, :].rearrange("p e (d b2) -> p b2 d e", b2=2)[:, b2],
                )

        def back_adds(i):
            for b2 in range(2):
                rows = slice(64 * b2, 64 * b2 + 64)
                nc.vector.tensor_tensor(
                    out=r[rows, A_BLOCKS[i], :].rearrange("p (d e) -> p d e", e=2),
                    in0=live["rb"][rows, :, :].rearrange("p e (d b2) -> p b2 d e", b2=2)[:, b2],
                    in1=sv[rows, A_BLOCKS[i], :].rearrange("p (d e) -> p d e", e=2),
                    op=ALU.add,
                )

        def product(n):
            block, quarter = HALVES[n]
            h = 2 * block + quarter // 2
            if n < 1:
                q_row = q_sb[:, h * DK:h * DK + DK]
            else:
                q_row = q_ps[:, 2 * V_BLOCKS.index(block) + quarter // 2, :]
            live["prod", n] = prod_pool.tile([P, 32, DK], F32, name="prod", tag="prod")
            for p0, w in pieces(n):
                nc.vector.scalar_tensor_tensor(
                    out=live["prod", n][:, p0:p0 + w, :],
                    in0=live["xv", n][:].rearrange("p (d c) -> p d c", c=DK)[:, p0:p0 + w, :],
                    scalar=dec_f[:, h:h + 1],
                    in1=q_row.unsqueeze(1).to_broadcast([P, w, DK]),
                    op0=ALU.mult,
                    op1=ALU.mult,
                )

        def scalar_sums(n, d0, rows):
            block, quarter = HALVES[n]
            prod = live["prod", n]
            for d in range(d0, d0 + rows):
                c0 = 32 * quarter + d
                nc.scalar.activation(out=prod[:, d, :], in_=prod[:, d, :], func=ACT.Copy, accum_out=r[:, block, c0:c0 + 1])

        def vector_sums(n, d0, rows):
            block, quarter = HALVES[n]
            c0 = 32 * quarter + d0
            nc.vector.tensor_reduce(
                out=r[:, block, c0:c0 + rows], in_=live["prod", n][:, d0:d0 + rows, :], axis=AX.X, op=ALU.add
            )

        def piece(p):
            w, pp = divmod(p, 5)
            return w, 2 * pp, min(2 * pp + 2, 9)

        def regroup(p):
            w, s0, s1 = piece(p)
            live["grp"] = grp_pool.tile([P, 4096], BF16, name="grp", tag="grp", align_bytes=64)
            for s in range(s0, s1):
                c, j = divmod(s, 3)
                at = 2048 * (s - s0)
                words = live["grp"][:, at:at + 2048].rearrange("p (w t) -> p w t", t=4)
                rows = live["raw", 3 * w + c][:, :, 512 * j:512 * j + 512].rearrange("p t w -> p w t")
                if s in V_PIECES:
                    nc.vector.tensor_copy(out=words, in_=rows)
                else:
                    nc.gpsimd.tensor_scalar(out=words, in0=rows, scalar1=1.0, scalar2=0.0, op0=ALU.mult, op1=ALU.add)
            done["weights"] = 3 * w + s1 // 3

        def quantise(p):
            w, s0, s1 = piece(p)
            cols = slice(512 * s0, 512 * s1)
            nc.vector.quantize_mx(
                out=w_codes[:].rearrange("p g c -> p (g c)")[:, cols].bitcast(FP8X4),
                scales=w_scales[:].rearrange("p g c -> p (g c)")[:, cols],
                in_=live["grp"][:, 0:2048 * (s1 - s0)],
            )

        x_grp = keep.tile([P, 3, 512], BF16, align_bytes=64)

        def x_transposes(g):
            x_words = x_sb[:].bitcast(F32)
            live["xt"] = ps_misc.tile([P, 2, P], F32, name="xt", tag="misc")
            for u in range(2):
                nc.tensor.transpose(live["xt"][:, u, :], x_words[:, 256 * g + u:256 * (g + 1):2], ident_f[:])

        def x_copies(g):
            nc.vector.tensor_copy(
                out=x_grp[:, g, :].bitcast(F32).rearrange("p (b u) -> p b u", u=2),
                in_=live["xt"][:].rearrange("p u b -> p b u"),
            )

        def x_quantise():
            for g in range(3):
                nc.vector.quantize_mx(
                    out=x_codes[:, g, :].bitcast(FP8X4), scales=x_scales[:, g, :], in_=x_grp[:, g, :]
                )

        def mx_pass(out, codes, scales, g, nb, first, last):
            cols = slice(512 * nb, 512 * nb + 512)
            nc.tensor.matmul_mx(
                out=out,
                lhsT=codes[:, g, :].bitcast(FP8X4),
                lhsT_scale=scales[:, g, :],
                rhs=w_codes[:, g, cols].bitcast(FP8X4),
                rhs_scale=w_scales[:, g, cols],
                start=first,
                stop=last,
            )

        def v_matmul(nb):
            live["v", nb] = ps_misc.tile([P, 512], F32, name="v", tag="misc")
            for c in range(3):
                mx_pass(live["v", nb][:], x_codes, x_scales, c, nb, c == 0, c == 2)

        def v_scale(nb):
            nc.vector.tensor_tensor(
                out=sv[:, 4 * nb:4 * nb + 4, :].rearrange("p k (h d) -> p (k h) d", d=DH),
                in0=live["v", nb][:].rearrange("p (h d) -> p h d", d=DH),
                in1=qk_sum[:, 8 * nb:8 * nb + 8].unsqueeze(2).to_broadcast([P, 8, DH]),
                op=ALU.mult,
            )

        def norm_add(ui):
            b0, nb = ADDED[ui]
            blocks = r[:, b0:b0 + nb, :]
            nc.vector.tensor_tensor(out=blocks, in0=blocks, in1=sv[:, b0:b0 + nb, :], op=ALU.add)

        def norm_root(ui):
            ss = small.tile([P, 4], F32, name="ss", tag="ss")
            sq = small.tile([P, 4, DH], F32, name="sq", tag="sq")
            r_heads = r[:, 2 * ui:2 * ui + 2, :].rearrange("p k (h d) -> p (k h) d", d=DH)
            for hh in range(4):
                nc.scalar.activation(out=sq[:, hh, :], in_=r_heads[:, hh, :], func=ACT.Square, accum_out=ss[:, hh:hh + 1])
            live["rms", ui] = small.tile([P, 4], F32, name="rms", tag="rms")
            nc.scalar.activation(out=live["rms", ui][:], in_=ss[:], func=ACT.Sqrt, bias=eps_t[:], scale=1.0 / DH)

        def norm_apply(ui):
            g = ui // 2
            if ui % 2 == 0:
                live["n", g] = keep.tile([P, 4, P], BF16, name="n%d" % g)
            inv = small.tile([P, 4], F32, tag="inv")
            nc.vector.reciprocal(out=inv[:], in_=live["rms", ui][:])
            nc.vector.tensor_tensor(
                out=live["n", g][:, 2 * (ui % 2):2 * (ui % 2) + 2, :].rearrange("p k (h d) -> p (k h) d", d=DH),
                in0=r[:, 2 * ui:2 * ui + 2, :].rearrange("p k (h d) -> p (k h) d", d=DH),
                in1=inv[:].unsqueeze(2).to_broadcast([P, 4, DH]),
                op=ALU.mult,
            )

        def n_transposes(g):
            live["nt"] = ps_misc.tile([P, 4, P], BF16, name="nt", tag="misc")
            for t in range(4):
                nc.tensor.transpose(live["nt"][:, t, :], live["n", g][:].rearrange("p k c -> p (k c)")[:, t::4], ident_b[:])

        def n_copy():
            live["ng"] = small.tile([P, 512], BF16, name="ng", tag="ng", align_bytes=64)
            nc.scalar.copy(out=live["ng"][:].rearrange("p (b t) -> p b t", t=4), in_=live["nt"][:].rearrange("p t b -> p b t"))

        def n_quantise(g):
            nc.vector.quantize_mx(out=n_codes[:, g, :].bitcast(FP8X4), scales=n_scales[:, g, :], in_=live["ng"][:])

        def o_pass(ps, nb):
            if ps == 0:
                live["o", nb] = ps_rot.tile([P, 512], F32, name="o", tag="rot")
            mx_pass(live["o", nb][:], n_codes, n_scales, ps, nb, ps == 0, ps == 2)

        regroup(0)
        for g in range(N_GROUPS):
            i, gg = divmod(g, GROUPS)

            for ui in range(6):
                if g == ADD_GROUPS[ui]:
                    norm_add(ui)
                if g == ADD_GROUPS[ui] + ROOT_LAG[ui]:
                    norm_root(ui)
                if g == APPLY_GROUPS[ui]:
                    norm_apply(ui)
            for ps in range(3):
                lag = g - APPLY_GROUPS[2 * ps + 1]
                if lag == N_LAG[ps]:
                    n_transposes(ps)
                if lag == N_LAG[ps] + (2 if ps < 2 else 1):
                    n_copy()
                if g == NQ_GROUPS[ps]:
                    n_quantise(ps)
                if ps == 2 and g == NQ_GROUPS[ps] + 1:
                    for nb in range(3):
                        o_pass(2, nb)
            if g == QUANT_GROUPS[X_Q]:
                x_quantise()
            if g in QUANT_GROUPS:
                p = QUANT_GROUPS.index(g)
                quantise(p)
                if p + 1 < len(QUANT_GROUPS):
                    regroup(p + 1)

            for n in range(N_HALVES):
                step = g - PRODUCT_GROUPS[n]
                if step == 0:
                    product(n)
                    done["half"] = n + 1
                s_rows = S_EARLY if n < EARLY else S_ROWS if n < N_HALVES - 2 else S_ROWS // 2
                if step == V_SUM:
                    vector_sums(n, s_rows, 32 - s_rows)

            if g < A_END:
                transposes(i, gg)
            if g == 2:
                for e in range(2):
                    nc.vector.tensor_copy(out=q_twice[:, :, e, :], in_=q_sb[:].rearrange("p (h c) -> p h c", c=DK))
            if g == 1:
                for j in range(5):
                    nc.tensor.transpose(q_ps[:, 2 * j:2 * j + 2, :].rearrange("p a c -> p (a c)"), q_t[:, j, :], ident_b[:])
            if 4 <= g < 4 + N_A:
                q_transposes(g - 4)
                q_copies(g - 4)
            if 1 <= i <= N_A:
                if i < N_A:
                    if 0 <= gg - READ_LAG < 8:
                        readout_matmuls(i - 1, 8 * (gg - READ_LAG), 8)
                    if gg == READ_LAG + 8:
                        collect(i - 1)
                    if gg == READ_LAG + 8 + BACK_LAG:
                        back_transposes()
                    if gg == READ_LAG + 9 + BACK_LAG:
                        if i - 1 < FIRST_ADDED:
                            back_copies(i - 1)
                        else:
                            back_adds(i - 1)
                else:
                    if gg < 2:
                        readout_matmuls(i - 1, 32 * gg, 32)
                    if gg == 3:
                        collect(i - 1)
                    if gg == 4:
                        back_transposes()
                        for ps in range(2):
                            for nb in range(3):
                                o_pass(ps, nb)
                    if gg == 5:
                        back_adds(i - 1)
            for n in range(N_HALVES):
                step = g - PRODUCT_GROUPS[n]
                s_rows = S_EARLY if n < EARLY else S_ROWS if n < N_HALVES - 2 else S_ROWS // 2
                k = step - S_FIRST
                if 0 <= k < S_SPAN:
                    d0, d1 = k * s_rows // S_SPAN, (k + 1) * s_rows // S_SPAN
                    scalar_sums(n, d0, d1 - d0)

            for part in range(2):
                if g == QUANT_GROUPS[QK_Q + part]:
                    c0 = part * (E // 2)
                    nc.gpsimd.tensor_tensor(
                        out=qk[:].rearrange("p h c -> p (h c)")[:, c0:c0 + E // 2],
                        in0=q_sb[:, c0:c0 + E // 2], in1=k_sb[:, c0:c0 + E // 2], op=ALU.mult,
                    )
            if g == QUANT_GROUPS[4]:
                nc.vector.tensor_reduce(out=qk_sum[:], in_=qk[:], axis=AX.X, op=ALU.add)
            for c in range(3):
                if g == X_GROUP + X_STEP * c:
                    x_transposes(c)
                if g == X_GROUP + X_STEP * c + 2:
                    x_copies(c)
            for nb in range(3):
                if g == V_GROUP + V_STEP * nb:
                    v_matmul(nb)
                if g == V_GROUP + V_STEP * nb + V_STEP - 1:
                    v_scale(nb)

            if gg == 15:
                done["tile"] = i + 1
            load_ready()

        for nb in range(3):
            o_sb = prod_pool.tile([P, 512], F32, tag="prod")
            if nb == 1:
                nc.vector.tensor_copy(out=o_sb[:], in_=live["o", nb][:])
            else:
                nc.scalar.copy(out=o_sb[:], in_=live["o", nb][:])
            nc.sync.dma_start(out=out_rows[:, 512 * nb:512 * nb + 512], in_=o_sb[:])
